import numpy as np
import ml_dtypes


def mxq(x, axis, fmt="e4m3"):
    dtype, down = {"e4m3": (ml_dtypes.float8_e4m3fn, 7), "e5m2": (ml_dtypes.float8_e5m2, 14)}[fmt]
    v = np.moveaxis(np.asarray(x, np.float32).astype(ml_dtypes.bfloat16).astype(np.float64), axis, -1)
    blocks = v.reshape(v.shape[:-1] + (-1, 32))
    amax = np.abs(blocks).max(-1, keepdims=True)
    byte = np.maximum(np.where(amax > 0, np.frexp(amax)[1] - 1 + 127, 0) - down, 1)
    scale = np.exp2(byte - 127.0)
    codes = (blocks / scale).astype(np.float32).astype(dtype).astype(np.float64)
    return np.moveaxis((codes * scale).reshape(v.shape), -1, axis)


WIDE = False


def mx_kscale(k):
    if not WIDE:
        return np.ones(k)
    levels = np.array([10, -10, 5, -5, 0])
    a = np.random.permutation(np.resize(levels, k // 512 * 4)).reshape(k // 512, 4)
    idx = np.arange(k)
    return np.exp2(a[idx // 512, idx % 128 // 32])


BF16 = ml_dtypes.bfloat16


def bf(x):
    return np.asarray(x, np.float32).astype(BF16)


def f64(x):
    return np.asarray(x).astype(np.float64)


B, I, H = 4096, 1024, 512
DT = 0.1
STEPS = 2


def sigmoid(v):
    return 1.0 / (1.0 + np.exp(-v))


def setup_inputs():
    s = mx_kscale(H)
    r = np.minimum(s, 1.0)
    return {"h": bf(np.random.standard_normal((B, H)) * 0.7 * s),
            "input_contrib": bf(np.random.standard_normal((B, H)) * 0.9),
            "x_tau": bf(np.random.standard_normal((B, H)) * 0.9),
            "W_rec": bf(np.random.standard_normal((H, H)) * 1.0 / np.sqrt(H) / s),
            "tau_w_h": bf(np.random.standard_normal((H, H)) * 1.2 / np.sqrt(H) / s),
            "tau_adapt_b": bf(np.random.standard_normal(H) * 0.5),
            "tau_base": bf((0.3 + 0.3 * np.random.random(H)) / r)}


def reference(h, input_contrib, x_tau, W_rec, tau_w_h, tau_adapt_b, tau_base):
    h = f64(h)
    wr = mxq(f64(W_rec), 1, "e4m3")
    wt = mxq(f64(tau_w_h), 1, "e4m3")
    tau = None
    for _ in range(STEPS):
        hq = mxq(h, 1, "e4m3")
        tau_logits = f64(x_tau) + (hq @ wt.T) + f64(tau_adapt_b)
        tau = f64(tau_base) * (0.5 + sigmoid(tau_logits))
        activated = np.tanh((hq @ wr.T) + f64(input_contrib))
        h = h + DT * (-h + activated) / tau
    return (h, tau)

@@ -1,0 +1,269 @@
+import math
+from contextlib import ExitStack
+
+import concourse.mybir as mybir
+from concourse.masks import make_identity
+
+F32 = mybir.dt.float32
+BF16 = mybir.dt.bfloat16
+U32 = mybir.dt.uint32
+U8 = mybir.dt.uint8
+FP8X4 = mybir.dt.float8_e4m3fn_x4
+ALU = mybir.AluOpType
+ACT = mybir.ActivationFunctionType
+
+B = 4096
+H = 512
+DT = 0.1
+P = 128
+PACK = 4
+CHUNK = 512
+BLOCKS = CHUNK // P
+HALF = CHUNK // 2
+N_CHUNKS = B // CHUNK
+
+FLOPS = 4 * 2 * B * H * H
+
+
+def load_rows(nc, pool, dram_rows):
+    rows = pool.tile([P, BLOCKS, H], BF16, tag="rows")
+    nc.sync.dma_start(out=rows[:], in_=dram_rows.rearrange("(j p) f -> p j f", p=P))
+    return rows
+
+
+def flip_half(nc, banks, rows, half, ident_bf16):
+    flipped = banks.tile([P, PACK, HALF], BF16, tag="flipped")
+    for t in range(PACK):
+        for jj in range(HALF // P):
+            nc.tensor.transpose(
+                flipped[:, t, jj * P : (jj + 1) * P],
+                rows[:, half * (HALF // P) + jj, t * P : (t + 1) * P],
+                ident_bf16[:],
+            )
+    return flipped
+
+
+def flip_plain(nc, banks, pool, rows, ident_bf16):
+    plain = pool.tile([P, PACK, CHUNK], BF16, tag="plain")
+    for half in range(2):
+        flipped = flip_half(nc, banks, rows, half, ident_bf16)
+        nc.scalar.copy(out=plain[:, :, half * HALF : (half + 1) * HALF], in_=flipped[:])
+    return plain
+
+
+def flip_grouped(nc, banks, pool, rows, ident_bf16):
+    grouped = pool.tile([P, CHUNK, PACK], BF16, tag="grouped", align_bytes=64)
+    for half in range(2):
+        flipped = flip_half(nc, banks, rows, half, ident_bf16)
+        nc.scalar.copy(
+            out=grouped[:, half * HALF : (half + 1) * HALF, :],
+            in_=flipped[:].rearrange("p t r -> p r t"),
+        )
+    return grouped
+
+
+def quantise(nc, pool, grouped, tag):
+    codes = pool.tile([P, CHUNK], U32, tag=tag + "_codes", align_bytes=64)
+    scales = pool.tile([P, CHUNK], U8, tag=tag + "_scales", align_bytes=64)
+    nc.vector.quantize_mx(
+        out=codes[:].bitcast(FP8X4),
+        scales=scales[:],
+        in_=grouped[:].rearrange("p r t -> p (r t)"),
+    )
+    return codes, scales
+
+
+def weight_times_state(nc, banks, tag, weight, m, state):
+    w_codes, w_scales = weight
+    s_codes, s_scales = state
+    product = banks.tile([P, CHUNK], F32, tag=tag)
+    nc.tensor.matmul_mx(
+        out=product[:],
+        lhsT=w_codes[:, m * P : (m + 1) * P].bitcast(FP8X4),
+        lhsT_scale=w_scales[:, m * P : (m + 1) * P],
+        rhs=s_codes[:].bitcast(FP8X4),
+        rhs_scale=s_scales[:],
+        start=True,
+        stop=True,
+    )
+    return product
+
+
+def unflip_and_store(nc, banks, pool, flipped, ident_f32, dram_rows):
+    rows = pool.tile([P, BLOCKS, H], F32, tag="out_rows")
+    for m in range(PACK):
+        back = banks.tile([P, BLOCKS, P], F32, tag="back")
+        for j in range(BLOCKS):
+            nc.tensor.transpose(back[:, j, :], flipped[:, m, j * P : (j + 1) * P], ident_f32[:])
+        nc.scalar.copy(out=rows[:, :, m * P : (m + 1) * P], in_=back[:])
+    nc.sync.dma_start(out=dram_rows.rearrange("(j p) f -> p j f", p=P), in_=rows[:])
+
+
+def tile_liquidcell_pb_t_kernel(
+    tc, h, input_contrib, x_tau, W_rec, tau_w_h, tau_adapt_b, tau_base, out_0, out_1
+):
+    nc = tc.nc
+    with ExitStack() as ctx:
+        ctx.enter_context(tc.manual_schedule())
+        const = ctx.enter_context(tc.tile_pool(name="const", bufs=1))
+        loads = ctx.enter_context(tc.tile_pool(name="loads", bufs=6))
+        flips = ctx.enter_context(tc.tile_pool(name="flips", bufs=2))
+        plains = ctx.enter_context(tc.tile_pool(name="plains", bufs=4))
+        mx = ctx.enter_context(tc.tile_pool(name="mx", bufs=2))
+        work = ctx.enter_context(tc.tile_pool(name="work", bufs=2))
+        stores = ctx.enter_context(tc.tile_pool(name="stores", bufs=4))
+        banks = ctx.enter_context(tc.psum_pool(name="banks", bufs=2))
+
+        ident_bf16 = const.tile([P, P], BF16)
+        make_identity(nc, ident_bf16[:])
+        ident_f32 = const.tile([P, P], F32)
+        make_identity(nc, ident_f32[:])
+
+        vector_rows = const.tile([P, P], BF16)
+        nc.vector.memset(vector_rows[:], 0.0)
+        nc.sync.dma_start(out=vector_rows[0:PACK, :], in_=tau_adapt_b.rearrange("(m p) -> m p", p=P))
+        nc.sync.dma_start(out=vector_rows[PACK : 2 * PACK, :], in_=tau_base.rearrange("(m p) -> m p", p=P))
+        tau_weight_rows = load_rows(nc, loads, tau_w_h)
+        rec_weight_rows = load_rows(nc, loads, W_rec)
+
+        vector_cols = banks.tile([P, P], BF16, tag="flipped")
+        nc.tensor.transpose(vector_cols[:], vector_rows[:], ident_bf16[:])
+        adapt_b = const.tile([P, PACK], F32)
+        nc.vector.tensor_copy(out=adapt_b[:], in_=vector_cols[:, 0:PACK])
+        base = const.tile([P, PACK], F32)
+        nc.vector.tensor_copy(out=base[:], in_=vector_cols[:, PACK : 2 * PACK])
+
+        bias_tau = const.tile([P, PACK], F32)
+        nc.vector.tensor_scalar(out=bias_tau[:], in0=adapt_b[:], scalar1=0.5, scalar2=None, op0=ALU.mult)
+        bias_rate = const.tile([P, PACK], F32)
+        nc.vector.tensor_scalar(
+            out=bias_rate[:], in0=adapt_b[:], scalar1=0.5, scalar2=0.5 * math.log(3.0), op0=ALU.mult, op1=ALU.add
+        )
+        half_base = const.tile([P, PACK], F32)
+        nc.vector.tensor_scalar(out=half_base[:], in0=base[:], scalar1=0.5, scalar2=None, op0=ALU.mult)
+        inverse_base = const.tile([P, PACK], F32)
+        nc.vector.reciprocal(out=inverse_base[:], in_=base[:])
+        gain = const.tile([P, PACK], F32)
+        nc.vector.tensor_scalar(
+            out=gain[:], in0=inverse_base[:], scalar1=-2.0 * DT / 3.0, scalar2=None, op0=ALU.mult
+        )
+
+        tau_weight = quantise(nc, const, flip_grouped(nc, banks, flips, tau_weight_rows, ident_bf16), "tau_weight")
+        rec_weight = quantise(nc, const, flip_grouped(nc, banks, flips, rec_weight_rows, ident_bf16), "rec_weight")
+
+        rows_of = {}
+        flipped_of = {}
+        state_of = {}
+        rate_of = {}
+        move_of = {}
+        h1_of = {}
+        tau2_of = {}
+        h2_of = {}
+
+        def chunk_rows(c):
+            return slice(c * CHUNK, (c + 1) * CHUNK)
+
+        def load(c):
+            rows_of[c] = (
+                load_rows(nc, loads, h[chunk_rows(c), :]),
+                load_rows(nc, loads, x_tau[chunk_rows(c), :]),
+                load_rows(nc, loads, input_contrib[chunk_rows(c), :]),
+            )
+
+        def flip(c):
+            h_rows, x_rows, ic_rows = rows_of[c]
+            flipped_of[c] = (
+                flip_grouped(nc, banks, flips, h_rows, ident_bf16),
+                flip_plain(nc, banks, plains, x_rows, ident_bf16),
+                flip_plain(nc, banks, plains, ic_rows, ident_bf16),
+            )
+
+        def quantise_input(c):
+            state_of[c] = quantise(nc, mx, flipped_of[c][0], "h0")
+
+        def old_state(c, step):
+            if step == 1:
+                return flipped_of[c][0][:].rearrange("p r t -> p t r")
+            return h1_of[c][:]
+
+        def matmuls_and_functions(c, step):
+            x_flipped, ic_flipped = flipped_of[c][1], flipped_of[c][2]
+            rate = work.tile([P, PACK, CHUNK], F32, tag="rate")
+            move = work.tile([P, PACK, CHUNK], F32, tag="move")
+            rate_of[c], move_of[c] = rate, move
+            if step == 2:
+                tau2 = work.tile([P, PACK, CHUNK], F32, tag="tau2")
+                tau2_of[c] = tau2
+            for m in range(PACK):
+                drive = weight_times_state(nc, banks, "drive", rec_weight, m, state_of[c])
+                logits = weight_times_state(nc, banks, "logits", tau_weight, m, state_of[c])
+                nc.vector.tensor_tensor(out=move[:, m, :], in0=drive[:], in1=ic_flipped[:, m, :], op=ALU.add)
+                nc.vector.tensor_tensor(out=rate[:, m, :], in0=logits[:], in1=x_flipped[:, m, :], op=ALU.add)
+                nc.scalar.activation(out=move[:, m, :], in_=move[:, m, :], func=ACT.Tanh)
+                if step == 2:
+                    nc.scalar.activation(
+                        out=tau2[:, m, :], in_=rate[:, m, :], func=ACT.Tanh, bias=bias_tau[:, m : m + 1], scale=0.5
+                    )
+                nc.scalar.activation(
+                    out=rate[:, m, :], in_=rate[:, m, :], func=ACT.Tanh, bias=bias_rate[:, m : m + 1], scale=0.5
+                )
+                if step == 2:
+                    nc.gpsimd.tensor_tensor(
+                        out=move[:, m, :], in0=move[:, m, :], in1=h1_of[c][:, m, :], op=ALU.subtract
+                    )
+                    nc.gpsimd.tensor_scalar(
+                        out=tau2[:, m, :], in0=tau2[:, m, :],
+                        scalar1=half_base[:, m : m + 1], scalar2=base[:, m : m + 1], op0=ALU.mult, op1=ALU.add,
+                    )
+
+        def update(c, step):
+            rate, move, old = rate_of[c], move_of[c], old_state(c, step)
+            new = work.tile([P, PACK, CHUNK], F32, tag="h%d" % step)
+            if step == 1:
+                h1_of[c] = new
+                for m in range(PACK):
+                    nc.vector.tensor_tensor(out=move[:, m, :], in0=move[:, m, :], in1=old[:, m, :], op=ALU.subtract)
+            else:
+                h2_of[c] = new
+            for m in range(PACK):
+                nc.vector.scalar_tensor_tensor(
+                    out=move[:, m, :], in0=rate[:, m, :], scalar=2.0, in1=move[:, m, :],
+                    op0=ALU.subtract, op1=ALU.mult,
+                )
+            for m in range(PACK):
+                nc.vector.scalar_tensor_tensor(
+                    out=new[:, m, :], in0=move[:, m, :], scalar=gain[:, m : m + 1], in1=old[:, m, :],
+                    op0=ALU.mult, op1=ALU.add,
+                )
+
+        def round_and_quantise_h1(c):
+            h1_grouped = flips.tile([P, CHUNK, PACK], BF16, tag="h1_grouped", align_bytes=64)
+            nc.vector.tensor_copy(out=h1_grouped[:], in_=h1_of[c][:].rearrange("p t r -> p r t"))
+            state_of[c] = quantise(nc, mx, h1_grouped, "h1")
+
+        def store(c):
+            unflip_and_store(nc, banks, stores, tau2_of[c], ident_f32, out_1[chunk_rows(c), :])
+            unflip_and_store(nc, banks, stores, h2_of[c], ident_f32, out_0[chunk_rows(c), :])
+
+        load(0)
+        load(1)
+        flip(0)
+        quantise_input(0)
+        for i in range(N_CHUNKS + 1):
+            if i + 2 < N_CHUNKS:
+                load(i + 2)
+            if i < N_CHUNKS:
+                matmuls_and_functions(i, 1)
+            if i >= 1:
+                update(i - 1, 2)
+            if i + 1 < N_CHUNKS:
+                flip(i + 1)
+            if i >= 1:
+                store(i - 1)
+            if i < N_CHUNKS:
+                update(i, 1)
+            if i + 1 < N_CHUNKS:
+                quantise_input(i + 1)
+            if i < N_CHUNKS:
+                round_and_quantise_h1(i)
+                matmuls_and_functions(i, 2)

@@ -17,6 +17,7 @@ H = 512
 DT = 0.1
 P = 128
 PACK = 4
+PAIR = 2
 CHUNK = 512
 BLOCKS = CHUNK // P
 HALF = CHUNK // 2
@@ -27,37 +28,36 @@ FLOPS = 4 * 2 * B * H * H
 
 def load_rows(nc, pool, dram_rows):
     rows = pool.tile([P, BLOCKS, H], BF16, tag="rows")
-    nc.sync.dma_start(out=rows[:], in_=dram_rows.rearrange("(j p) f -> p j f", p=P))
+    nc.sync.dma_start(out=rows[:], in_=dram_rows.rearrange("(p j) f -> p j f", j=BLOCKS))
     return rows
 
 
-def flip_half(nc, banks, rows, half, ident_bf16):
-    flipped = banks.tile([P, PACK, HALF], BF16, tag="flipped")
-    for t in range(PACK):
-        for jj in range(HALF // P):
-            nc.tensor.transpose(
-                flipped[:, t, jj * P : (jj + 1) * P],
-                rows[:, half * (HALF // P) + jj, t * P : (t + 1) * P],
-                ident_bf16[:],
-            )
+def flip_half(nc, banks, rows, half, ident_f32):
+    flipped = banks.tile([P, PAIR, HALF], F32, tag="flipped")
+    for jj in range(HALF // P):
+        words = rows[:, half * (HALF // P) + jj, :].bitcast(F32).rearrange("p (w u) -> p u w", u=PAIR)
+        for u in range(PAIR):
+            nc.tensor.transpose(flipped[:, u, jj * P : (jj + 1) * P], words[:, u, :], ident_f32[:])
     return flipped
 
 
-def flip_plain(nc, banks, pool, rows, ident_bf16):
-    plain = pool.tile([P, PACK, CHUNK], BF16, tag="plain")
+def flip_plain(nc, banks, pool, rows, ident_f32):
+    plain = pool.tile([P, PACK * CHUNK], BF16, tag="plain")
+    plain_words = plain[:].bitcast(F32).rearrange("p (u c) -> p u c", u=PAIR)
     for half in range(2):
-        flipped = flip_half(nc, banks, rows, half, ident_bf16)
-        nc.scalar.copy(out=plain[:, :, half * HALF : (half + 1) * HALF], in_=flipped[:])
-    return plain
+        flipped = flip_half(nc, banks, rows, half, ident_f32)
+        nc.scalar.copy(out=plain_words[:, :, half * HALF : (half + 1) * HALF], in_=flipped[:])
+    return plain[:].rearrange("p (u c e) -> p u c e", u=PAIR, e=PAIR)
 
 
-def flip_grouped(nc, banks, pool, rows, ident_bf16):
-    grouped = pool.tile([P, CHUNK, PACK], BF16, tag="grouped", align_bytes=64)
+def flip_grouped(nc, banks, pool, rows, ident_f32):
+    grouped = pool.tile([P, CHUNK * PACK], BF16, tag="grouped", align_bytes=64)
+    grouped_words = grouped[:].bitcast(F32).rearrange("p (c u) -> p c u", u=PAIR)
     for half in range(2):
-        flipped = flip_half(nc, banks, rows, half, ident_bf16)
+        flipped = flip_half(nc, banks, rows, half, ident_f32)
         nc.scalar.copy(
-            out=grouped[:, half * HALF : (half + 1) * HALF, :],
-            in_=flipped[:].rearrange("p t r -> p r t"),
+            out=grouped_words[:, half * HALF : (half + 1) * HALF, :],
+            in_=flipped[:].rearrange("p u c -> p c u"),
         )
     return grouped
 
@@ -65,11 +65,7 @@ def flip_grouped(nc, banks, pool, rows, ident_bf16):
 def quantise(nc, pool, grouped, tag):
     codes = pool.tile([P, CHUNK], U32, tag=tag + "_codes", align_bytes=64)
     scales = pool.tile([P, CHUNK], U8, tag=tag + "_scales", align_bytes=64)
-    nc.vector.quantize_mx(
-        out=codes[:].bitcast(FP8X4),
-        scales=scales[:],
-        in_=grouped[:].rearrange("p r t -> p (r t)"),
-    )
+    nc.vector.quantize_mx(out=codes[:].bitcast(FP8X4), scales=scales[:], in_=grouped[:])
     return codes, scales
 
 
@@ -91,12 +87,14 @@ def weight_times_state(nc, banks, tag, weight, m, state):
 
 def unflip_and_store(nc, banks, pool, flipped, ident_f32, dram_rows):
     rows = pool.tile([P, BLOCKS, H], F32, tag="out_rows")
-    for m in range(PACK):
-        back = banks.tile([P, BLOCKS, P], F32, tag="back")
-        for j in range(BLOCKS):
-            nc.tensor.transpose(back[:, j, :], flipped[:, m, j * P : (j + 1) * P], ident_f32[:])
-        nc.scalar.copy(out=rows[:, :, m * P : (m + 1) * P], in_=back[:])
-    nc.sync.dma_start(out=dram_rows.rearrange("(j p) f -> p j f", p=P), in_=rows[:])
+    for j in range(BLOCKS):
+        back = banks.tile([P, PACK, P], F32, tag="back")
+        for m in range(PACK):
+            nc.tensor.transpose(back[:, m, :], flipped[:, m, j * P : (j + 1) * P], ident_f32[:])
+        nc.scalar.copy(
+            out=rows[:, j, :].rearrange("r (p m) -> r p m", m=PACK), in_=back[:].rearrange("r m p -> r p m")
+        )
+    nc.sync.dma_start(out=dram_rows.rearrange("(p j) f -> p j f", j=BLOCKS), in_=rows[:])
 
 
 def tile_liquidcell_pb_t_kernel(
@@ -114,33 +112,28 @@ def tile_liquidcell_pb_t_kernel(
         stores = ctx.enter_context(tc.tile_pool(name="stores", bufs=4))
         banks = ctx.enter_context(tc.psum_pool(name="banks", bufs=2))
 
-        ident_bf16 = const.tile([P, P], BF16)
-        make_identity(nc, ident_bf16[:])
         ident_f32 = const.tile([P, P], F32)
         make_identity(nc, ident_f32[:])
 
-        vector_rows = const.tile([P, P], BF16)
-        nc.vector.memset(vector_rows[:], 0.0)
-        nc.sync.dma_start(out=vector_rows[0:PACK, :], in_=tau_adapt_b.rearrange("(m p) -> m p", p=P))
-        nc.sync.dma_start(out=vector_rows[PACK : 2 * PACK, :], in_=tau_base.rearrange("(m p) -> m p", p=P))
         tau_weight_rows = load_rows(nc, loads, tau_w_h)
         rec_weight_rows = load_rows(nc, loads, W_rec)
 
-        vector_cols = banks.tile([P, P], BF16, tag="flipped")
-        nc.tensor.transpose(vector_cols[:], vector_rows[:], ident_bf16[:])
-        adapt_b = const.tile([P, PACK], F32)
-        nc.vector.tensor_copy(out=adapt_b[:], in_=vector_cols[:, 0:PACK])
-        base = const.tile([P, PACK], F32)
-        nc.vector.tensor_copy(out=base[:], in_=vector_cols[:, PACK : 2 * PACK])
+        adapt_b_bf16 = const.tile([P, PACK], BF16)
+        nc.sync.dma_start(out=adapt_b_bf16[:], in_=tau_adapt_b.rearrange("(p m) -> p m", m=PACK))
+        base_bf16 = const.tile([P, PACK], BF16)
+        nc.sync.dma_start(out=base_bf16[:], in_=tau_base.rearrange("(p m) -> p m", m=PACK))
 
         bias_tau = const.tile([P, PACK], F32)
-        nc.vector.tensor_scalar(out=bias_tau[:], in0=adapt_b[:], scalar1=0.5, scalar2=None, op0=ALU.mult)
+        nc.vector.tensor_scalar(out=bias_tau[:], in0=adapt_b_bf16[:], scalar1=0.5, scalar2=None, op0=ALU.mult)
         bias_rate = const.tile([P, PACK], F32)
         nc.vector.tensor_scalar(
-            out=bias_rate[:], in0=adapt_b[:], scalar1=0.5, scalar2=0.5 * math.log(3.0), op0=ALU.mult, op1=ALU.add
+            out=bias_rate[:], in0=adapt_b_bf16[:], scalar1=0.5, scalar2=0.5 * math.log(3.0),
+            op0=ALU.mult, op1=ALU.add,
         )
+        base = const.tile([P, PACK], F32)
+        nc.vector.tensor_copy(out=base[:], in_=base_bf16[:])
         half_base = const.tile([P, PACK], F32)
-        nc.vector.tensor_scalar(out=half_base[:], in0=base[:], scalar1=0.5, scalar2=None, op0=ALU.mult)
+        nc.vector.tensor_scalar(out=half_base[:], in0=base_bf16[:], scalar1=0.5, scalar2=None, op0=ALU.mult)
         inverse_base = const.tile([P, PACK], F32)
         nc.vector.reciprocal(out=inverse_base[:], in_=base[:])
         gain = const.tile([P, PACK], F32)
@@ -148,11 +141,13 @@ def tile_liquidcell_pb_t_kernel(
             out=gain[:], in0=inverse_base[:], scalar1=-2.0 * DT / 3.0, scalar2=None, op0=ALU.mult
         )
 
-        tau_weight = quantise(nc, const, flip_grouped(nc, banks, flips, tau_weight_rows, ident_bf16), "tau_weight")
-        rec_weight = quantise(nc, const, flip_grouped(nc, banks, flips, rec_weight_rows, ident_bf16), "rec_weight")
+        tau_weight = quantise(nc, const, flip_grouped(nc, banks, flips, tau_weight_rows, ident_f32), "tau_weight")
+        rec_weight = quantise(nc, const, flip_grouped(nc, banks, flips, rec_weight_rows, ident_f32), "rec_weight")
 
         rows_of = {}
-        flipped_of = {}
+        h0_of = {}
+        x_of = {}
+        ic_of = {}
         state_of = {}
         rate_of = {}
         move_of = {}
@@ -166,28 +161,25 @@ def tile_liquidcell_pb_t_kernel(
         def load(c):
             rows_of[c] = (
                 load_rows(nc, loads, h[chunk_rows(c), :]),
-                load_rows(nc, loads, x_tau[chunk_rows(c), :]),
                 load_rows(nc, loads, input_contrib[chunk_rows(c), :]),
+                load_rows(nc, loads, x_tau[chunk_rows(c), :]),
             )
 
         def flip(c):
-            h_rows, x_rows, ic_rows = rows_of[c]
-            flipped_of[c] = (
-                flip_grouped(nc, banks, flips, h_rows, ident_bf16),
-                flip_plain(nc, banks, plains, x_rows, ident_bf16),
-                flip_plain(nc, banks, plains, ic_rows, ident_bf16),
-            )
+            h_rows, ic_rows, x_rows = rows_of[c]
+            h0_of[c] = flip_grouped(nc, banks, flips, h_rows, ident_f32)
+            ic_of[c] = flip_plain(nc, banks, plains, ic_rows, ident_f32)
+            x_of[c] = flip_plain(nc, banks, plains, x_rows, ident_f32)
 
-        def quantise_input(c):
-            state_of[c] = quantise(nc, mx, flipped_of[c][0], "h0")
+        def quantise_h0(c):
+            state_of[c] = quantise(nc, mx, h0_of[c], "h0")
 
         def old_state(c, step):
             if step == 1:
-                return flipped_of[c][0][:].rearrange("p r t -> p t r")
+                return h0_of[c][:].rearrange("p (c t) -> p t c", t=PACK)
             return h1_of[c][:]
 
         def matmuls_and_functions(c, step):
-            x_flipped, ic_flipped = flipped_of[c][1], flipped_of[c][2]
             rate = work.tile([P, PACK, CHUNK], F32, tag="rate")
             move = work.tile([P, PACK, CHUNK], F32, tag="move")
             rate_of[c], move_of[c] = rate, move
@@ -197,8 +189,8 @@ def tile_liquidcell_pb_t_kernel(
             for m in range(PACK):
                 drive = weight_times_state(nc, banks, "drive", rec_weight, m, state_of[c])
                 logits = weight_times_state(nc, banks, "logits", tau_weight, m, state_of[c])
-                nc.vector.tensor_tensor(out=move[:, m, :], in0=drive[:], in1=ic_flipped[:, m, :], op=ALU.add)
-                nc.vector.tensor_tensor(out=rate[:, m, :], in0=logits[:], in1=x_flipped[:, m, :], op=ALU.add)
+                nc.vector.tensor_tensor(out=move[:, m, :], in0=drive[:], in1=ic_of[c][:, m // PAIR, :, m % PAIR], op=ALU.add)
+                nc.vector.tensor_tensor(out=rate[:, m, :], in0=logits[:], in1=x_of[c][:, m // PAIR, :, m % PAIR], op=ALU.add)
                 nc.scalar.activation(out=move[:, m, :], in_=move[:, m, :], func=ACT.Tanh)
                 if step == 2:
                     nc.scalar.activation(
@@ -216,54 +208,67 @@ def tile_liquidcell_pb_t_kernel(
                         scalar1=half_base[:, m : m + 1], scalar2=base[:, m : m + 1], op0=ALU.mult, op1=ALU.add,
                     )
 
-        def update(c, step):
-            rate, move, old = rate_of[c], move_of[c], old_state(c, step)
-            new = work.tile([P, PACK, CHUNK], F32, tag="h%d" % step)
-            if step == 1:
-                h1_of[c] = new
-                for m in range(PACK):
-                    nc.vector.tensor_tensor(out=move[:, m, :], in0=move[:, m, :], in1=old[:, m, :], op=ALU.subtract)
-            else:
-                h2_of[c] = new
+        def subtract_old(c, step):
+            move, old = move_of[c], old_state(c, step)
+            for m in range(PACK):
+                nc.vector.tensor_tensor(out=move[:, m, :], in0=move[:, m, :], in1=old[:, m, :], op=ALU.subtract)
+
+        def times_rate(c):
+            rate, move = rate_of[c], move_of[c]
             for m in range(PACK):
                 nc.vector.scalar_tensor_tensor(
                     out=move[:, m, :], in0=rate[:, m, :], scalar=2.0, in1=move[:, m, :],
                     op0=ALU.subtract, op1=ALU.mult,
                 )
-            for m in range(PACK):
+
+        def add_to_old(c, step, new, tiles):
+            move, old = move_of[c], old_state(c, step)
+            for m in tiles:
                 nc.vector.scalar_tensor_tensor(
                     out=new[:, m, :], in0=move[:, m, :], scalar=gain[:, m : m + 1], in1=old[:, m, :],
                     op0=ALU.mult, op1=ALU.add,
                 )
 
-        def round_and_quantise_h1(c):
-            h1_grouped = flips.tile([P, CHUNK, PACK], BF16, tag="h1_grouped", align_bytes=64)
-            nc.vector.tensor_copy(out=h1_grouped[:], in_=h1_of[c][:].rearrange("p t r -> p r t"))
-            state_of[c] = quantise(nc, mx, h1_grouped, "h1")
-
-        def store(c):
-            unflip_and_store(nc, banks, stores, tau2_of[c], ident_f32, out_1[chunk_rows(c), :])
-            unflip_and_store(nc, banks, stores, h2_of[c], ident_f32, out_0[chunk_rows(c), :])
+        def in_range(c):
+            return 0 <= c < N_CHUNKS
 
         load(0)
         load(1)
         flip(0)
-        quantise_input(0)
-        for i in range(N_CHUNKS + 1):
-            if i + 2 < N_CHUNKS:
+        quantise_h0(0)
+        for i in range(N_CHUNKS + 2):
+            if in_range(i + 2):
                 load(i + 2)
-            if i < N_CHUNKS:
+            if in_range(i):
                 matmuls_and_functions(i, 1)
-            if i >= 1:
-                update(i - 1, 2)
-            if i + 1 < N_CHUNKS:
+            if in_range(i - 1):
+                times_rate(i - 1)
+            if in_range(i + 1):
                 flip(i + 1)
-            if i >= 1:
-                store(i - 1)
-            if i < N_CHUNKS:
-                update(i, 1)
-            if i + 1 < N_CHUNKS:
-                quantise_input(i + 1)
-            if i < N_CHUNKS:
-                round_and_quantise_h1(i)
+            if in_range(i - 1):
+                unflip_and_store(nc, banks, stores, tau2_of[i - 1], ident_f32, out_1[chunk_rows(i - 1), :])
+            if in_range(i - 2):
+                unflip_and_store(nc, banks, stores, h2_of[i - 2], ident_f32, out_0[chunk_rows(i - 2), :])
+            if in_range(i):
+                subtract_old(i, 1)
+                times_rate(i)
+                h1 = work.tile([P, PACK, CHUNK], F32, tag="h1")
+                h1_of[i] = h1
+                add_to_old(i, 1, h1, range(PACK))
+            if in_range(i + 1):
+                quantise_h0(i + 1)
+            if in_range(i):
+                h1_grouped = flips.tile([P, CHUNK * PACK], BF16, tag="h1_grouped", align_bytes=64)
+                nc.vector.tensor_copy(
+                    out=h1_grouped[:].rearrange("p (c t) -> p c t", t=PACK), in_=h1[:].rearrange("p t c -> p c t")
+                )
+            if in_range(i - 1):
+                h2 = work.tile([P, PACK, CHUNK], F32, tag="h2")
+                h2_of[i - 1] = h2
+                add_to_old(i - 1, 2, h2, range(0, PACK // 2))
+            if in_range(i):
+                state_of[i] = quantise(nc, mx, h1_grouped, "h1")
+            if in_range(i - 1):
+                add_to_old(i - 1, 2, h2, range(PACK // 2, PACK))
+            if in_range(i):
                 matmuls_and_functions(i, 2)

@@ -203,10 +203,14 @@ def tile_liquidcell_pb_t_kernel(
                     nc.gpsimd.tensor_tensor(
                         out=move[:, m, :], in0=move[:, m, :], in1=h1_of[c][:, m, :], op=ALU.subtract
                     )
-                    nc.gpsimd.tensor_scalar(
-                        out=tau2[:, m, :], in0=tau2[:, m, :],
-                        scalar1=half_base[:, m : m + 1], scalar2=base[:, m : m + 1], op0=ALU.mult, op1=ALU.add,
-                    )
+
+        def finish_tau2(c):
+            tau2 = tau2_of[c]
+            for m in range(PACK):
+                nc.gpsimd.tensor_scalar(
+                    out=tau2[:, m, :], in0=tau2[:, m, :],
+                    scalar1=half_base[:, m : m + 1], scalar2=base[:, m : m + 1], op0=ALU.mult, op1=ALU.add,
+                )
 
         def subtract_old(c, step):
             move, old = move_of[c], old_state(c, step)
@@ -245,9 +249,8 @@ def tile_liquidcell_pb_t_kernel(
                 times_rate(i - 1)
             if in_range(i + 1):
                 flip(i + 1)
-            if in_range(i - 1):
-                unflip_and_store(nc, banks, stores, tau2_of[i - 1], ident_f32, out_1[chunk_rows(i - 1), :])
             if in_range(i - 2):
+                unflip_and_store(nc, banks, stores, tau2_of[i - 2], ident_f32, out_1[chunk_rows(i - 2), :])
                 unflip_and_store(nc, banks, stores, h2_of[i - 2], ident_f32, out_0[chunk_rows(i - 2), :])
             if in_range(i):
                 subtract_old(i, 1)
@@ -270,5 +273,6 @@ def tile_liquidcell_pb_t_kernel(
                 state_of[i] = quantise(nc, mx, h1_grouped, "h1")
             if in_range(i - 1):
                 add_to_old(i - 1, 2, h2, range(PACK // 2, PACK))
+                finish_tau2(i - 1)
             if in_range(i):
                 matmuls_and_functions(i, 2)

@@ -33,7 +33,7 @@ def load_rows(nc, pool, dram_rows):
 
 
 def flip_half(nc, banks, rows, half, ident_f32):
-    flipped = banks.tile([P, PAIR, HALF], F32, tag="flipped")
+    flipped = banks.tile([P, PAIR, HALF], F32, tag="turned")
     for jj in range(HALF // P):
         words = rows[:, half * (HALF // P) + jj, :].bitcast(F32).rearrange("p (w u) -> p u w", u=PAIR)
         for u in range(PAIR):
@@ -69,10 +69,10 @@ def quantise(nc, pool, grouped, tag):
     return codes, scales
 
 
-def weight_times_state(nc, banks, tag, weight, m, state):
+def weight_times_state(nc, banks, weight, m, state):
     w_codes, w_scales = weight
     s_codes, s_scales = state
-    product = banks.tile([P, CHUNK], F32, tag=tag)
+    product = banks.tile([P, CHUNK], F32, tag="product")
     nc.tensor.matmul_mx(
         out=product[:],
         lhsT=w_codes[:, m * P : (m + 1) * P].bitcast(FP8X4),
@@ -85,16 +85,25 @@ def weight_times_state(nc, banks, tag, weight, m, state):
     return product
 
 
-def unflip_and_store(nc, banks, pool, flipped, ident_f32, dram_rows):
+def unflip_and_store(nc, banks, pool, terms, ident_f32, dram_rows):
     rows = pool.tile([P, BLOCKS, H], F32, tag="out_rows")
+    dram_blocks = dram_rows.rearrange("(p j) f -> p j f", j=BLOCKS)
     for j in range(BLOCKS):
-        back = banks.tile([P, PACK, P], F32, tag="back")
+        back = banks.tile([P, PACK, P], F32, tag="turned")
         for m in range(PACK):
-            nc.tensor.transpose(back[:, m, :], flipped[:, m, j * P : (j + 1) * P], ident_f32[:])
+            for n, term in enumerate(terms):
+                nc.tensor.matmul(
+                    out=back[:, m, :],
+                    lhsT=term[:, m, j * P : (j + 1) * P],
+                    rhs=ident_f32[:],
+                    is_transpose=True,
+                    start=(n == 0),
+                    stop=(n == len(terms) - 1),
+                )
         nc.scalar.copy(
             out=rows[:, j, :].rearrange("r (p m) -> r p m", m=PACK), in_=back[:].rearrange("r m p -> r p m")
         )
-    nc.sync.dma_start(out=dram_rows.rearrange("(p j) f -> p j f", j=BLOCKS), in_=rows[:])
+        nc.sync.dma_start(out=dram_blocks[:, j, :], in_=rows[:, j, :])
 
 
 def tile_liquidcell_pb_t_kernel(
@@ -108,9 +117,11 @@ def tile_liquidcell_pb_t_kernel(
         flips = ctx.enter_context(tc.tile_pool(name="flips", bufs=2))
         plains = ctx.enter_context(tc.tile_pool(name="plains", bufs=4))
         mx = ctx.enter_context(tc.tile_pool(name="mx", bufs=2))
-        work = ctx.enter_context(tc.tile_pool(name="work", bufs=2))
+        step1 = ctx.enter_context(tc.tile_pool(name="step1", bufs=1))
+        step2 = ctx.enter_context(tc.tile_pool(name="step2", bufs=2))
+        states = ctx.enter_context(tc.tile_pool(name="states", bufs=3))
         stores = ctx.enter_context(tc.tile_pool(name="stores", bufs=4))
-        banks = ctx.enter_context(tc.psum_pool(name="banks", bufs=2))
+        banks = ctx.enter_context(tc.psum_pool(name="banks", bufs=4))
 
         ident_f32 = const.tile([P, P], F32)
         make_identity(nc, ident_f32[:])
@@ -153,7 +164,6 @@ def tile_liquidcell_pb_t_kernel(
         move_of = {}
         h1_of = {}
         tau2_of = {}
-        h2_of = {}
 
         def chunk_rows(c):
             return slice(c * CHUNK, (c + 1) * CHUNK)
@@ -174,21 +184,17 @@ def tile_liquidcell_pb_t_kernel(
         def quantise_h0(c):
             state_of[c] = quantise(nc, mx, h0_of[c], "h0")
 
-        def old_state(c, step):
-            if step == 1:
-                return h0_of[c][:].rearrange("p (c t) -> p t c", t=PACK)
-            return h1_of[c][:]
-
         def matmuls_and_functions(c, step):
-            rate = work.tile([P, PACK, CHUNK], F32, tag="rate")
-            move = work.tile([P, PACK, CHUNK], F32, tag="move")
+            pool = step1 if step == 1 else step2
+            rate = pool.tile([P, PACK, CHUNK], F32, tag="rate")
+            move = pool.tile([P, PACK, CHUNK], F32, tag="move")
             rate_of[c], move_of[c] = rate, move
             if step == 2:
-                tau2 = work.tile([P, PACK, CHUNK], F32, tag="tau2")
+                tau2 = pool.tile([P, PACK, CHUNK], F32, tag="tau2")
                 tau2_of[c] = tau2
             for m in range(PACK):
-                drive = weight_times_state(nc, banks, "drive", rec_weight, m, state_of[c])
-                logits = weight_times_state(nc, banks, "logits", tau_weight, m, state_of[c])
+                drive = weight_times_state(nc, banks, rec_weight, m, state_of[c])
+                logits = weight_times_state(nc, banks, tau_weight, m, state_of[c])
                 nc.vector.tensor_tensor(out=move[:, m, :], in0=drive[:], in1=ic_of[c][:, m // PAIR, :, m % PAIR], op=ALU.add)
                 nc.vector.tensor_tensor(out=rate[:, m, :], in0=logits[:], in1=x_of[c][:, m // PAIR, :, m % PAIR], op=ALU.add)
                 nc.scalar.activation(out=move[:, m, :], in_=move[:, m, :], func=ACT.Tanh)
@@ -212,26 +218,33 @@ def tile_liquidcell_pb_t_kernel(
                     scalar1=half_base[:, m : m + 1], scalar2=base[:, m : m + 1], op0=ALU.mult, op1=ALU.add,
                 )
 
-        def subtract_old(c, step):
-            move, old = move_of[c], old_state(c, step)
+        def subtract_h0(c):
+            move, h0 = move_of[c], h0_of[c][:].rearrange("p (c t) -> p t c", t=PACK)
             for m in range(PACK):
-                nc.vector.tensor_tensor(out=move[:, m, :], in0=move[:, m, :], in1=old[:, m, :], op=ALU.subtract)
+                nc.vector.tensor_tensor(out=move[:, m, :], in0=move[:, m, :], in1=h0[:, m, :], op=ALU.subtract)
 
-        def times_rate(c):
+        def times_rate(c, tiles):
             rate, move = rate_of[c], move_of[c]
-            for m in range(PACK):
+            for m in tiles:
                 nc.vector.scalar_tensor_tensor(
                     out=move[:, m, :], in0=rate[:, m, :], scalar=2.0, in1=move[:, m, :],
                     op0=ALU.subtract, op1=ALU.mult,
                 )
 
-        def add_to_old(c, step, new, tiles):
-            move, old = move_of[c], old_state(c, step)
-            for m in tiles:
+        def make_h1(c):
+            move, h0 = move_of[c], h0_of[c][:].rearrange("p (c t) -> p t c", t=PACK)
+            h1 = states.tile([P, PACK, CHUNK], F32, tag="h1")
+            h1_of[c] = h1
+            for m in range(PACK):
                 nc.vector.scalar_tensor_tensor(
-                    out=new[:, m, :], in0=move[:, m, :], scalar=gain[:, m : m + 1], in1=old[:, m, :],
+                    out=h1[:, m, :], in0=move[:, m, :], scalar=gain[:, m : m + 1], in1=h0[:, m, :],
                     op0=ALU.mult, op1=ALU.add,
                 )
+
+        def make_e2(c):
+            move = move_of[c]
+            for m in range(PACK):
+                nc.scalar.activation(out=move[:, m, :], in_=move[:, m, :], func=ACT.Copy, scale=gain[:, m : m + 1])
 
         def in_range(c):
             return 0 <= c < N_CHUNKS
@@ -245,34 +258,33 @@ def tile_liquidcell_pb_t_kernel(
                 load(i + 2)
             if in_range(i):
                 matmuls_and_functions(i, 1)
-            if in_range(i - 1):
-                times_rate(i - 1)
+            if in_range(i - 2):
+                make_e2(i - 2)
             if in_range(i + 1):
                 flip(i + 1)
             if in_range(i - 2):
-                unflip_and_store(nc, banks, stores, tau2_of[i - 2], ident_f32, out_1[chunk_rows(i - 2), :])
-                unflip_and_store(nc, banks, stores, h2_of[i - 2], ident_f32, out_0[chunk_rows(i - 2), :])
+                unflip_and_store(
+                    nc, banks, stores, [h1_of[i - 2], move_of[i - 2]], ident_f32, out_0[chunk_rows(i - 2), :]
+                )
+                unflip_and_store(nc, banks, stores, [tau2_of[i - 2]], ident_f32, out_1[chunk_rows(i - 2), :])
             if in_range(i):
-                subtract_old(i, 1)
-                times_rate(i)
-                h1 = work.tile([P, PACK, CHUNK], F32, tag="h1")
-                h1_of[i] = h1
-                add_to_old(i, 1, h1, range(PACK))
+                subtract_h0(i)
+                times_rate(i, range(PACK))
+                make_h1(i)
             if in_range(i + 1):
                 quantise_h0(i + 1)
             if in_range(i):
                 h1_grouped = flips.tile([P, CHUNK * PACK], BF16, tag="h1_grouped", align_bytes=64)
                 nc.vector.tensor_copy(
-                    out=h1_grouped[:].rearrange("p (c t) -> p c t", t=PACK), in_=h1[:].rearrange("p t c -> p c t")
+                    out=h1_grouped[:].rearrange("p (c t) -> p c t", t=PACK),
+                    in_=h1_of[i][:].rearrange("p t c -> p c t"),
                 )
             if in_range(i - 1):
-                h2 = work.tile([P, PACK, CHUNK], F32, tag="h2")
-                h2_of[i - 1] = h2
-                add_to_old(i - 1, 2, h2, range(0, PACK // 2))
+                times_rate(i - 1, range(0, PACK // 2))
             if in_range(i):
                 state_of[i] = quantise(nc, mx, h1_grouped, "h1")
             if in_range(i - 1):
-                add_to_old(i - 1, 2, h2, range(PACK // 2, PACK))
+                times_rate(i - 1, range(PACK // 2, PACK))
                 finish_tau2(i - 1)
             if in_range(i):
                 matmuls_and_functions(i, 2)

@@ -119,7 +119,7 @@ def tile_liquidcell_pb_t_kernel(
         mx = ctx.enter_context(tc.tile_pool(name="mx", bufs=2))
         step1 = ctx.enter_context(tc.tile_pool(name="step1", bufs=1))
         step2 = ctx.enter_context(tc.tile_pool(name="step2", bufs=2))
-        states = ctx.enter_context(tc.tile_pool(name="states", bufs=3))
+        states = ctx.enter_context(tc.tile_pool(name="states", bufs=2))
         stores = ctx.enter_context(tc.tile_pool(name="stores", bufs=4))
         banks = ctx.enter_context(tc.psum_pool(name="banks", bufs=4))
 
@@ -223,9 +223,9 @@ def tile_liquidcell_pb_t_kernel(
             for m in range(PACK):
                 nc.vector.tensor_tensor(out=move[:, m, :], in0=move[:, m, :], in1=h0[:, m, :], op=ALU.subtract)
 
-        def times_rate(c, tiles):
+        def times_rate(c):
             rate, move = rate_of[c], move_of[c]
-            for m in tiles:
+            for m in range(PACK):
                 nc.vector.scalar_tensor_tensor(
                     out=move[:, m, :], in0=rate[:, m, :], scalar=2.0, in1=move[:, m, :],
                     op0=ALU.subtract, op1=ALU.mult,
@@ -240,6 +240,13 @@ def tile_liquidcell_pb_t_kernel(
                     out=h1[:, m, :], in0=move[:, m, :], scalar=gain[:, m : m + 1], in1=h0[:, m, :],
                     op0=ALU.mult, op1=ALU.add,
                 )
+
+        def round_and_quantise_h1(c):
+            h1_grouped = flips.tile([P, CHUNK * PACK], BF16, tag="h1_grouped", align_bytes=64)
+            nc.vector.tensor_copy(
+                out=h1_grouped[:].rearrange("p (c t) -> p c t", t=PACK), in_=h1_of[c][:].rearrange("p t c -> p c t")
+            )
+            state_of[c] = quantise(nc, mx, h1_grouped, "h1")
 
         def make_e2(c):
             move = move_of[c]
@@ -258,33 +265,27 @@ def tile_liquidcell_pb_t_kernel(
                 load(i + 2)
             if in_range(i):
                 matmuls_and_functions(i, 1)
-            if in_range(i - 2):
-                make_e2(i - 2)
+            if in_range(i - 1):
+                times_rate(i - 1)
             if in_range(i + 1):
                 flip(i + 1)
+            if in_range(i - 1):
+                make_e2(i - 1)
             if in_range(i - 2):
-                unflip_and_store(
-                    nc, banks, stores, [h1_of[i - 2], move_of[i - 2]], ident_f32, out_0[chunk_rows(i - 2), :]
-                )
                 unflip_and_store(nc, banks, stores, [tau2_of[i - 2]], ident_f32, out_1[chunk_rows(i - 2), :])
+            if in_range(i - 1):
+                unflip_and_store(
+                    nc, banks, stores, [h1_of[i - 1], move_of[i - 1]], ident_f32, out_0[chunk_rows(i - 1), :]
+                )
             if in_range(i):
                 subtract_h0(i)
-                times_rate(i, range(PACK))
+                times_rate(i)
                 make_h1(i)
             if in_range(i + 1):
                 quantise_h0(i + 1)
             if in_range(i):
-                h1_grouped = flips.tile([P, CHUNK * PACK], BF16, tag="h1_grouped", align_bytes=64)
-                nc.vector.tensor_copy(
-                    out=h1_grouped[:].rearrange("p (c t) -> p c t", t=PACK),
-                    in_=h1_of[i][:].rearrange("p t c -> p c t"),
-                )
+                round_and_quantise_h1(i)
             if in_range(i - 1):
-                times_rate(i - 1, range(0, PACK // 2))
-            if in_range(i):
-                state_of[i] = quantise(nc, mx, h1_grouped, "h1")
-            if in_range(i - 1):
-                times_rate(i - 1, range(PACK // 2, PACK))
                 finish_tau2(i - 1)
             if in_range(i):
                 matmuls_and_functions(i, 2)

@@ -256,6 +256,11 @@ def tile_liquidcell_pb_t_kernel(
         def in_range(c):
             return 0 <= c < N_CHUNKS
 
+        gate_word = const.tile([P, 1], U32)
+
+        def hold_gpsimd_until_h1_is_quantised(c):
+            nc.gpsimd.tensor_copy(out=gate_word[:], in_=state_of[c][0][:, 0:1])
+
         load(0)
         load(1)
         flip(0)
@@ -285,6 +290,8 @@ def tile_liquidcell_pb_t_kernel(
                 quantise_h0(i + 1)
             if in_range(i):
                 round_and_quantise_h1(i)
+            if in_range(i):
+                hold_gpsimd_until_h1_is_quantised(i)
             if in_range(i - 1):
                 finish_tau2(i - 1)
             if in_range(i):

@@ -22,6 +22,7 @@ CHUNK = 512
 BLOCKS = CHUNK // P
 HALF = CHUNK // 2
 N_CHUNKS = B // CHUNK
+WIDE = 2
 
 FLOPS = 4 * 2 * B * H * H
 
@@ -134,13 +135,8 @@ def tile_liquidcell_pb_t_kernel(
         base_bf16 = const.tile([P, PACK], BF16)
         nc.sync.dma_start(out=base_bf16[:], in_=tau_base.rearrange("(p m) -> p m", m=PACK))
 
-        bias_tau = const.tile([P, PACK], F32)
-        nc.vector.tensor_scalar(out=bias_tau[:], in0=adapt_b_bf16[:], scalar1=0.5, scalar2=None, op0=ALU.mult)
-        bias_rate = const.tile([P, PACK], F32)
-        nc.vector.tensor_scalar(
-            out=bias_rate[:], in0=adapt_b_bf16[:], scalar1=0.5, scalar2=0.5 * math.log(3.0),
-            op0=ALU.mult, op1=ALU.add,
-        )
+        adapt_b = const.tile([P, PACK], F32)
+        nc.vector.tensor_copy(out=adapt_b[:], in_=adapt_b_bf16[:])
         base = const.tile([P, PACK], F32)
         nc.vector.tensor_copy(out=base[:], in_=base_bf16[:])
         half_base = const.tile([P, PACK], F32)
@@ -184,6 +180,9 @@ def tile_liquidcell_pb_t_kernel(
         def quantise_h0(c):
             state_of[c] = quantise(nc, mx, h0_of[c], "h0")
 
+        def wide_tiles():
+            return [slice(m, m + WIDE) for m in range(0, PACK, WIDE)]
+
         def matmuls_and_functions(c, step):
             pool = step1 if step == 1 else step2
             rate = pool.tile([P, PACK, CHUNK], F32, tag="rate")
@@ -194,21 +193,24 @@ def tile_liquidcell_pb_t_kernel(
                 tau2_of[c] = tau2
             for m in range(PACK):
                 drive = weight_times_state(nc, banks, rec_weight, m, state_of[c])
-                logits = weight_times_state(nc, banks, tau_weight, m, state_of[c])
                 nc.vector.tensor_tensor(out=move[:, m, :], in0=drive[:], in1=ic_of[c][:, m // PAIR, :, m % PAIR], op=ALU.add)
-                nc.vector.tensor_tensor(out=rate[:, m, :], in0=logits[:], in1=x_of[c][:, m // PAIR, :, m % PAIR], op=ALU.add)
-                nc.scalar.activation(out=move[:, m, :], in_=move[:, m, :], func=ACT.Tanh)
-                if step == 2:
-                    nc.scalar.activation(
-                        out=tau2[:, m, :], in_=rate[:, m, :], func=ACT.Tanh, bias=bias_tau[:, m : m + 1], scale=0.5
-                    )
-                nc.scalar.activation(
-                    out=rate[:, m, :], in_=rate[:, m, :], func=ACT.Tanh, bias=bias_rate[:, m : m + 1], scale=0.5
+            for m in range(PACK):
+                logits = weight_times_state(nc, banks, tau_weight, m, state_of[c])
+                nc.vector.scalar_tensor_tensor(
+                    out=rate[:, m, :], in0=logits[:], scalar=adapt_b[:, m : m + 1],
+                    in1=x_of[c][:, m // PAIR, :, m % PAIR], op0=ALU.add, op1=ALU.add,
                 )
+            for w in wide_tiles():
+                nc.scalar.activation(out=move[:, w, :], in_=move[:, w, :], func=ACT.Tanh)
                 if step == 2:
-                    nc.gpsimd.tensor_tensor(
-                        out=move[:, m, :], in0=move[:, m, :], in1=h1_of[c][:, m, :], op=ALU.subtract
-                    )
+                    nc.gpsimd.tensor_tensor(out=move[:, w, :], in0=move[:, w, :], in1=h1_of[c][:, w, :], op=ALU.subtract)
+            if step == 2:
+                for w in wide_tiles():
+                    nc.scalar.activation(out=tau2[:, w, :], in_=rate[:, w, :], func=ACT.Tanh, scale=0.5)
+            for w in wide_tiles():
+                nc.scalar.activation(
+                    out=rate[:, w, :], in_=rate[:, w, :], func=ACT.Tanh, bias=0.5 * math.log(3.0), scale=0.5
+                )
 
         def finish_tau2(c):
             tau2 = tau2_of[c]
@@ -220,14 +222,14 @@ def tile_liquidcell_pb_t_kernel(
 
         def subtract_h0(c):
             move, h0 = move_of[c], h0_of[c][:].rearrange("p (c t) -> p t c", t=PACK)
-            for m in range(PACK):
-                nc.vector.tensor_tensor(out=move[:, m, :], in0=move[:, m, :], in1=h0[:, m, :], op=ALU.subtract)
+            for w in wide_tiles():
+                nc.vector.tensor_tensor(out=move[:, w, :], in0=move[:, w, :], in1=h0[:, w, :], op=ALU.subtract)
 
         def times_rate(c):
             rate, move = rate_of[c], move_of[c]
-            for m in range(PACK):
+            for w in wide_tiles():
                 nc.vector.scalar_tensor_tensor(
-                    out=move[:, m, :], in0=rate[:, m, :], scalar=2.0, in1=move[:, m, :],
+                    out=move[:, w, :], in0=rate[:, w, :], scalar=2.0, in1=move[:, w, :],
                     op0=ALU.subtract, op1=ALU.mult,
                 )
 

@@ -23,6 +23,10 @@ BLOCKS = CHUNK // P
 HALF = CHUNK // 2
 N_CHUNKS = B // CHUNK
 WIDE = 2
+S_WIDE = 4
+N_PRODUCT_BANKS = 3
+G_AFFINE = 2
+N_TURN_BANKS = 8 - N_PRODUCT_BANKS
 
 FLOPS = 4 * 2 * B * H * H
 
@@ -40,27 +44,6 @@ def flip_half(nc, banks, rows, half, ident_f32):
         for u in range(PAIR):
             nc.tensor.transpose(flipped[:, u, jj * P : (jj + 1) * P], words[:, u, :], ident_f32[:])
     return flipped
-
-
-def flip_plain(nc, banks, pool, rows, ident_f32):
-    plain = pool.tile([P, PACK * CHUNK], BF16, tag="plain")
-    plain_words = plain[:].bitcast(F32).rearrange("p (u c) -> p u c", u=PAIR)
-    for half in range(2):
-        flipped = flip_half(nc, banks, rows, half, ident_f32)
-        nc.scalar.copy(out=plain_words[:, :, half * HALF : (half + 1) * HALF], in_=flipped[:])
-    return plain[:].rearrange("p (u c e) -> p u c e", u=PAIR, e=PAIR)
-
-
-def flip_grouped(nc, banks, pool, rows, ident_f32):
-    grouped = pool.tile([P, CHUNK * PACK], BF16, tag="grouped", align_bytes=64)
-    grouped_words = grouped[:].bitcast(F32).rearrange("p (c u) -> p c u", u=PAIR)
-    for half in range(2):
-        flipped = flip_half(nc, banks, rows, half, ident_f32)
-        nc.scalar.copy(
-            out=grouped_words[:, half * HALF : (half + 1) * HALF, :],
-            in_=flipped[:].rearrange("p u c -> p c u"),
-        )
-    return grouped
 
 
 def quantise(nc, pool, grouped, tag):
@@ -86,27 +69,6 @@ def weight_times_state(nc, banks, weight, m, state):
     return product
 
 
-def unflip_and_store(nc, banks, pool, terms, ident_f32, dram_rows):
-    rows = pool.tile([P, BLOCKS, H], F32, tag="out_rows")
-    dram_blocks = dram_rows.rearrange("(p j) f -> p j f", j=BLOCKS)
-    for j in range(BLOCKS):
-        back = banks.tile([P, PACK, P], F32, tag="turned")
-        for m in range(PACK):
-            for n, term in enumerate(terms):
-                nc.tensor.matmul(
-                    out=back[:, m, :],
-                    lhsT=term[:, m, j * P : (j + 1) * P],
-                    rhs=ident_f32[:],
-                    is_transpose=True,
-                    start=(n == 0),
-                    stop=(n == len(terms) - 1),
-                )
-        nc.scalar.copy(
-            out=rows[:, j, :].rearrange("r (p m) -> r p m", m=PACK), in_=back[:].rearrange("r m p -> r p m")
-        )
-        nc.sync.dma_start(out=dram_blocks[:, j, :], in_=rows[:, j, :])
-
-
 def tile_liquidcell_pb_t_kernel(
     tc, h, input_contrib, x_tau, W_rec, tau_w_h, tau_adapt_b, tau_base, out_0, out_1
 ):
@@ -116,13 +78,14 @@ def tile_liquidcell_pb_t_kernel(
         const = ctx.enter_context(tc.tile_pool(name="const", bufs=1))
         loads = ctx.enter_context(tc.tile_pool(name="loads", bufs=6))
         flips = ctx.enter_context(tc.tile_pool(name="flips", bufs=2))
-        plains = ctx.enter_context(tc.tile_pool(name="plains", bufs=4))
+        plains = ctx.enter_context(tc.tile_pool(name="plains", bufs=3))
         mx = ctx.enter_context(tc.tile_pool(name="mx", bufs=2))
         step1 = ctx.enter_context(tc.tile_pool(name="step1", bufs=1))
-        step2 = ctx.enter_context(tc.tile_pool(name="step2", bufs=2))
-        states = ctx.enter_context(tc.tile_pool(name="states", bufs=2))
-        stores = ctx.enter_context(tc.tile_pool(name="stores", bufs=4))
-        banks = ctx.enter_context(tc.psum_pool(name="banks", bufs=4))
+        step2 = ctx.enter_context(tc.tile_pool(name="step2", bufs=3))
+        states = ctx.enter_context(tc.tile_pool(name="states", bufs=3))
+        stores = ctx.enter_context(tc.tile_pool(name="stores", bufs=8))
+        products = ctx.enter_context(tc.psum_pool(name="products", bufs=N_PRODUCT_BANKS))
+        turns = ctx.enter_context(tc.psum_pool(name="turns", bufs=8 - N_PRODUCT_BANKS))
 
         ident_f32 = const.tile([P, P], F32)
         make_identity(nc, ident_f32[:])
@@ -147,22 +110,30 @@ def tile_liquidcell_pb_t_kernel(
         nc.vector.tensor_scalar(
             out=gain[:], in0=inverse_base[:], scalar1=-2.0 * DT / 3.0, scalar2=None, op0=ALU.mult
         )
-
-        tau_weight = quantise(nc, const, flip_grouped(nc, banks, flips, tau_weight_rows, ident_f32), "tau_weight")
-        rec_weight = quantise(nc, const, flip_grouped(nc, banks, flips, rec_weight_rows, ident_f32), "rec_weight")
+        minus_two_gain = const.tile([P, PACK], F32)
+        nc.vector.tensor_scalar(out=minus_two_gain[:], in0=gain[:], scalar1=-2.0, scalar2=None, op0=ALU.mult)
 
         rows_of = {}
+        turned_of = {}
         h0_of = {}
         x_of = {}
         ic_of = {}
-        state_of = {}
+        state0_of = {}
+        state1_of = {}
         rate_of = {}
         move_of = {}
         h1_of = {}
         tau2_of = {}
+        grouped_h1_of = {}
 
         def chunk_rows(c):
             return slice(c * CHUNK, (c + 1) * CHUNK)
+
+        def wide_tiles():
+            return [slice(m, m + WIDE) for m in range(0, PACK, WIDE)]
+
+        def s_wide_tiles():
+            return [slice(m, m + S_WIDE) for m in range(0, PACK, S_WIDE)]
 
         def load(c):
             rows_of[c] = (
@@ -171,51 +142,112 @@ def tile_liquidcell_pb_t_kernel(
                 load_rows(nc, loads, x_tau[chunk_rows(c), :]),
             )
 
-        def flip(c):
-            h_rows, ic_rows, x_rows = rows_of[c]
-            h0_of[c] = flip_grouped(nc, banks, flips, h_rows, ident_f32)
-            ic_of[c] = flip_plain(nc, banks, plains, ic_rows, ident_f32)
-            x_of[c] = flip_plain(nc, banks, plains, x_rows, ident_f32)
+        def flip_pe(key, rows, half):
+            turned_of[key] = flip_half(nc, turns, rows, half, ident_f32)
+
+        def grouped_tile(pool):
+            grouped = pool.tile([P, CHUNK * PACK], BF16, tag="grouped", align_bytes=64)
+            return grouped
+
+        def copy_grouped(key, grouped, half):
+            grouped_words = grouped[:].bitcast(F32).rearrange("p (c u) -> p c u", u=PAIR)
+            nc.scalar.copy(
+                out=grouped_words[:, half * HALF : (half + 1) * HALF, :],
+                in_=turned_of[key][:].rearrange("p u c -> p c u"),
+            )
+
+        def copy_plain(key, plain, half):
+            plain_words = plain[:].bitcast(F32).rearrange("p (u c) -> p u c", u=PAIR)
+            nc.scalar.copy(out=plain_words[:, :, half * HALF : (half + 1) * HALF], in_=turned_of[key][:])
+
+        def plain_view(plain):
+            return plain[:].rearrange("p (u c e) -> p u c e", u=PAIR, e=PAIR)
+
+        def flip_jobs(c):
+            h0_of[c] = grouped_tile(flips)
+            ic_plain = plains.tile([P, PACK * CHUNK], BF16, tag="ic")
+            ic_of[c] = plain_view(ic_plain)
+            x_plain = plains.tile([P, PACK * CHUNK], BF16, tag="x")
+            x_of[c] = plain_view(x_plain)
+            jobs = []
+            for half in range(2):
+                jobs.append((
+                    lambda half=half: flip_pe((c, 0, half), rows_of[c][0], half),
+                    lambda half=half: copy_grouped((c, 0, half), h0_of[c], half),
+                ))
+            for n, plain in ((1, ic_plain), (2, x_plain)):
+                for half in range(2):
+                    jobs.append((
+                        lambda n=n, half=half: flip_pe((c, n, half), rows_of[c][n], half),
+                        lambda n=n, half=half, plain=plain: copy_plain((c, n, half), plain, half),
+                    ))
+            return jobs
+
+        def run_jobs(jobs, before):
+            filled = 0
+            for k in range(len(jobs)):
+                while filled < min(k + N_TURN_BANKS, len(jobs)):
+                    jobs[filled][0]()
+                    filled += 1
+                if k in before:
+                    before[k]()
+                jobs[k][1]()
+
+        weights = []
+        for name, rows in (("tau_weight", tau_weight_rows), ("rec_weight", rec_weight_rows)):
+            grouped = grouped_tile(flips)
+            for half in range(2):
+                flip_pe((name, half), rows, half)
+                copy_grouped((name, half), grouped, half)
+            weights.append(quantise(nc, const, grouped, name))
+        tau_weight, rec_weight = weights
 
         def quantise_h0(c):
-            state_of[c] = quantise(nc, mx, h0_of[c], "h0")
+            state0_of[c] = quantise(nc, mx, h0_of[c], "h0")
 
-        def wide_tiles():
-            return [slice(m, m + WIDE) for m in range(0, PACK, WIDE)]
-
-        def matmuls_and_functions(c, step):
+        def products_and_sums(c, step):
             pool = step1 if step == 1 else step2
+            state = state0_of[c] if step == 1 else state1_of[c]
             rate = pool.tile([P, PACK, CHUNK], F32, tag="rate")
             move = pool.tile([P, PACK, CHUNK], F32, tag="move")
             rate_of[c], move_of[c] = rate, move
-            if step == 2:
-                tau2 = pool.tile([P, PACK, CHUNK], F32, tag="tau2")
-                tau2_of[c] = tau2
             for m in range(PACK):
-                drive = weight_times_state(nc, banks, rec_weight, m, state_of[c])
+                drive = weight_times_state(nc, products, rec_weight, m, state)
                 nc.vector.tensor_tensor(out=move[:, m, :], in0=drive[:], in1=ic_of[c][:, m // PAIR, :, m % PAIR], op=ALU.add)
             for m in range(PACK):
-                logits = weight_times_state(nc, banks, tau_weight, m, state_of[c])
+                logits = weight_times_state(nc, products, tau_weight, m, state)
                 nc.vector.scalar_tensor_tensor(
                     out=rate[:, m, :], in0=logits[:], scalar=adapt_b[:, m : m + 1],
                     in1=x_of[c][:, m // PAIR, :, m % PAIR], op0=ALU.add, op1=ALU.add,
                 )
-            for w in wide_tiles():
+
+        def tanh_move(c):
+            move = move_of[c]
+            for w in s_wide_tiles():
                 nc.scalar.activation(out=move[:, w, :], in_=move[:, w, :], func=ACT.Tanh)
-                if step == 2:
-                    nc.gpsimd.tensor_tensor(out=move[:, w, :], in0=move[:, w, :], in1=h1_of[c][:, w, :], op=ALU.subtract)
-            if step == 2:
-                for w in wide_tiles():
-                    nc.scalar.activation(out=tau2[:, w, :], in_=rate[:, w, :], func=ACT.Tanh, scale=0.5)
-            for w in wide_tiles():
+
+        def tanh_tau2(c):
+            tau2 = step2.tile([P, PACK, CHUNK], F32, tag="tau2")
+            tau2_of[c] = tau2
+            for w in s_wide_tiles():
+                nc.scalar.activation(out=tau2[:, w, :], in_=rate_of[c][:, w, :], func=ACT.Tanh, scale=0.5)
+
+        def tanh_rate(c):
+            rate = rate_of[c]
+            for w in s_wide_tiles():
                 nc.scalar.activation(
                     out=rate[:, w, :], in_=rate[:, w, :], func=ACT.Tanh, bias=0.5 * math.log(3.0), scale=0.5
                 )
 
-        def finish_tau2(c):
+        def subtract_h1(c, engine):
+            move = move_of[c]
+            for w in wide_tiles():
+                engine.tensor_tensor(out=move[:, w, :], in0=move[:, w, :], in1=h1_of[c][:, w, :], op=ALU.subtract)
+
+        def finish_tau2(c, engine, tiles):
             tau2 = tau2_of[c]
-            for m in range(PACK):
-                nc.gpsimd.tensor_scalar(
+            for m in tiles:
+                engine.tensor_scalar(
                     out=tau2[:, m, :], in0=tau2[:, m, :],
                     scalar1=half_base[:, m : m + 1], scalar2=base[:, m : m + 1], op0=ALU.mult, op1=ALU.add,
                 )
@@ -233,6 +265,19 @@ def tile_liquidcell_pb_t_kernel(
                     op0=ALU.subtract, op1=ALU.mult,
                 )
 
+        def scale_rate(c, engine):
+            rate = rate_of[c]
+            for m in range(PACK):
+                engine.tensor_scalar(
+                    out=rate[:, m, :], in0=rate[:, m, :],
+                    scalar1=gain[:, m : m + 1], scalar2=minus_two_gain[:, m : m + 1], op0=ALU.mult, op1=ALU.add,
+                )
+
+        def times_scaled_rate(c):
+            rate, move = rate_of[c], move_of[c]
+            for w in wide_tiles():
+                nc.vector.tensor_tensor(out=move[:, w, :], in0=rate[:, w, :], in1=move[:, w, :], op=ALU.mult)
+
         def make_h1(c):
             move, h0 = move_of[c], h0_of[c][:].rearrange("p (c t) -> p t c", t=PACK)
             h1 = states.tile([P, PACK, CHUNK], F32, tag="h1")
@@ -243,58 +288,128 @@ def tile_liquidcell_pb_t_kernel(
                     op0=ALU.mult, op1=ALU.add,
                 )
 
-        def round_and_quantise_h1(c):
+        def round_h1(c):
             h1_grouped = flips.tile([P, CHUNK * PACK], BF16, tag="h1_grouped", align_bytes=64)
             nc.vector.tensor_copy(
                 out=h1_grouped[:].rearrange("p (c t) -> p c t", t=PACK), in_=h1_of[c][:].rearrange("p t c -> p c t")
             )
-            state_of[c] = quantise(nc, mx, h1_grouped, "h1")
+            grouped_h1_of[c] = h1_grouped
 
-        def make_e2(c):
-            move = move_of[c]
+        def quantise_h1(c):
+            state1_of[c] = quantise(nc, mx, grouped_h1_of[c], "h1")
+
+        gate_word = const.tile([P, 1], U32)
+
+        def hold_gpsimd(c):
+            nc.gpsimd.tensor_copy(out=gate_word[:], in_=state1_of[c][0][:, 0:1])
+
+        def unflip_pe(key, terms, j):
+            back = turns.tile([P, PACK, P], F32, tag="turned")
+            turned_of[key] = back
             for m in range(PACK):
-                nc.scalar.activation(out=move[:, m, :], in_=move[:, m, :], func=ACT.Copy, scale=gain[:, m : m + 1])
+                for n, (term, factors) in enumerate(terms):
+                    nc.tensor.matmul(
+                        out=back[:, m, :],
+                        lhsT=term[:, m, j * P : (j + 1) * P],
+                        rhs=ident_f32[:] if factors is None else factors[:, m, :],
+                        is_transpose=factors is None,
+                        start=(n == 0),
+                        stop=(n == len(terms) - 1),
+                    )
+
+        def unflip_copy(key, dram_rows, j, on_vector):
+            rows = stores.tile([P, H], F32, tag="out_rows")
+            if on_vector:
+                nc.vector.tensor_copy(
+                    out=rows[:].rearrange("r (p m) -> r p m", m=PACK), in_=turned_of[key][:].rearrange("r m p -> r p m")
+                )
+            else:
+                nc.scalar.copy(
+                    out=rows[:].rearrange("r (p m) -> r p m", m=PACK), in_=turned_of[key][:].rearrange("r m p -> r p m")
+                )
+            nc.sync.dma_start(out=dram_rows.rearrange("(p j) f -> p j f", j=BLOCKS)[:, j, :], in_=rows[:])
+
+        def tau2_jobs(c, on_vector=False):
+            return [
+                (
+                    lambda j=j: unflip_pe((c, "tau2", j), [(tau2_of[c], None)], j),
+                    lambda j=j: unflip_copy((c, "tau2", j), out_1[chunk_rows(c), :], j, on_vector),
+                )
+                for j in range(BLOCKS)
+            ]
+
+        def h2_jobs(c, on_vector=False):
+            return [
+                (
+                    lambda j=j: unflip_pe((c, "h2", j), [(h1_of[c], None), (move_of[c], None)], j),
+                    lambda j=j: unflip_copy((c, "h2", j), out_0[chunk_rows(c), :], j, on_vector),
+                )
+                for j in range(BLOCKS)
+            ]
 
         def in_range(c):
             return 0 <= c < N_CHUNKS
 
-        gate_word = const.tile([P, 1], U32)
-
-        def hold_gpsimd_until_h1_is_quantised(c):
-            nc.gpsimd.tensor_copy(out=gate_word[:], in_=state_of[c][0][:, 0:1])
-
         load(0)
         load(1)
-        flip(0)
+        run_jobs(flip_jobs(0), {})
         quantise_h0(0)
-        for i in range(N_CHUNKS + 2):
+        LAST = N_CHUNKS - 1
+        for i in range(N_CHUNKS):
             if in_range(i + 2):
                 load(i + 2)
-            if in_range(i):
-                matmuls_and_functions(i, 1)
-            if in_range(i - 1):
-                times_rate(i - 1)
-            if in_range(i + 1):
-                flip(i + 1)
-            if in_range(i - 1):
-                make_e2(i - 1)
             if in_range(i - 2):
-                unflip_and_store(nc, banks, stores, [tau2_of[i - 2]], ident_f32, out_1[chunk_rows(i - 2), :])
+                hold_gpsimd(i - 1)
+                subtract_h1(i - 2, nc.gpsimd)
+                scale_rate(i - 2, nc.gpsimd)
+                finish_tau2(i - 2, nc.gpsimd, range(G_AFFINE))
+            products_and_sums(i, 1)
+            tanh_move(i)
+            tanh_rate(i)
             if in_range(i - 1):
-                unflip_and_store(
-                    nc, banks, stores, [h1_of[i - 1], move_of[i - 1]], ident_f32, out_0[chunk_rows(i - 1), :]
-                )
-            if in_range(i):
-                subtract_h0(i)
-                times_rate(i)
-                make_h1(i)
+                products_and_sums(i - 1, 2)
+                tanh_move(i - 1)
+            if in_range(i - 2):
+                times_scaled_rate(i - 2)
+                finish_tau2(i - 2, nc.vector, range(G_AFFINE, PACK))
+            jobs = []
+            before = {}
+            if in_range(i + 1):
+                jobs.extend(flip_jobs(i + 1))
+            if in_range(i - 1):
+                before[len(jobs)] = lambda: tanh_tau2(i - 1)
+            if in_range(i - 2):
+                jobs.extend(tau2_jobs(i - 2))
+            if in_range(i - 1):
+                if len(jobs) in before:
+                    before[len(jobs)] = lambda: (tanh_tau2(i - 1), tanh_rate(i - 1))
+                else:
+                    before[len(jobs)] = lambda: tanh_rate(i - 1)
+            if in_range(i - 2):
+                jobs.extend(h2_jobs(i - 2))
+            run_jobs(jobs, before)
+            if len(jobs) in before:
+                before[len(jobs)]()
+            subtract_h0(i)
+            times_rate(i)
+            make_h1(i)
             if in_range(i + 1):
                 quantise_h0(i + 1)
-            if in_range(i):
-                round_and_quantise_h1(i)
-            if in_range(i):
-                hold_gpsimd_until_h1_is_quantised(i)
-            if in_range(i - 1):
-                finish_tau2(i - 1)
-            if in_range(i):
-                matmuls_and_functions(i, 2)
+            round_h1(i)
+            quantise_h1(i)
+
+        hold_gpsimd(LAST)
+        subtract_h1(LAST - 1, nc.gpsimd)
+        products_and_sums(LAST, 2)
+        tanh_move(LAST)
+        tanh_tau2(LAST)
+        tanh_rate(LAST)
+        scale_rate(LAST - 1, nc.vector)
+        times_scaled_rate(LAST - 1)
+        finish_tau2(LAST - 1, nc.vector, range(PACK))
+        run_jobs(h2_jobs(LAST - 1) + tau2_jobs(LAST - 1), {})
+        subtract_h1(LAST, nc.vector)
+        scale_rate(LAST, nc.vector)
+        times_scaled_rate(LAST)
+        finish_tau2(LAST, nc.vector, range(PACK))
+        run_jobs(h2_jobs(LAST) + tau2_jobs(LAST, on_vector=True), {})

@@ -26,6 +26,8 @@ WIDE = 2
 S_WIDE = 4
 N_PRODUCT_BANKS = 3
 G_AFFINE = 2
+S_AFFINE = 1
+B_ON_SCALAR = (True, False)
 N_TURN_BANKS = 8 - N_PRODUCT_BANKS
 
 FLOPS = 4 * 2 * B * H * H
@@ -90,16 +92,26 @@ def tile_liquidcell_pb_t_kernel(
         ident_f32 = const.tile([P, P], F32)
         make_identity(nc, ident_f32[:])
 
-        tau_weight_rows = load_rows(nc, loads, tau_w_h)
-        rec_weight_rows = load_rows(nc, loads, W_rec)
-
         adapt_b_bf16 = const.tile([P, PACK], BF16)
         nc.sync.dma_start(out=adapt_b_bf16[:], in_=tau_adapt_b.rearrange("(p m) -> p m", m=PACK))
         base_bf16 = const.tile([P, PACK], BF16)
         nc.sync.dma_start(out=base_bf16[:], in_=tau_base.rearrange("(p m) -> p m", m=PACK))
+        first_h_rows = load_rows(nc, loads, h[0:CHUNK, :])
+        rec_weight_rows = const.tile([P, BLOCKS, H], BF16)
+        nc.sync.dma_start(out=rec_weight_rows[:], in_=W_rec.rearrange("(p j) f -> p j f", j=BLOCKS))
+        first_ic_rows = load_rows(nc, loads, input_contrib[0:CHUNK, :])
+        tau_weight_rows = const.tile([P, BLOCKS, H], BF16)
+        nc.sync.dma_start(out=tau_weight_rows[:], in_=tau_w_h.rearrange("(p j) f -> p j f", j=BLOCKS))
+        first_x_rows = load_rows(nc, loads, x_tau[0:CHUNK, :])
 
         adapt_b = const.tile([P, PACK], F32)
         nc.vector.tensor_copy(out=adapt_b[:], in_=adapt_b_bf16[:])
+        bias_tau = const.tile([P, PACK], F32)
+        nc.vector.tensor_scalar(out=bias_tau[:], in0=adapt_b_bf16[:], scalar1=0.5, scalar2=None, op0=ALU.mult)
+        bias_rate = const.tile([P, PACK], F32)
+        nc.vector.tensor_scalar(
+            out=bias_rate[:], in0=adapt_b_bf16[:], scalar1=0.5, scalar2=0.5 * math.log(3.0), op0=ALU.mult, op1=ALU.add
+        )
         base = const.tile([P, PACK], F32)
         nc.vector.tensor_copy(out=base[:], in_=base_bf16[:])
         half_base = const.tile([P, PACK], F32)
@@ -193,14 +205,14 @@ def tile_liquidcell_pb_t_kernel(
                     before[k]()
                 jobs[k][1]()
 
-        weights = []
-        for name, rows in (("tau_weight", tau_weight_rows), ("rec_weight", rec_weight_rows)):
-            grouped = grouped_tile(flips)
-            for half in range(2):
-                flip_pe((name, half), rows, half)
-                copy_grouped((name, half), grouped, half)
-            weights.append(quantise(nc, const, grouped, name))
-        tau_weight, rec_weight = weights
+        def weight_jobs(name, rows, grouped):
+            return [
+                (
+                    lambda half=half: flip_pe((name, half), rows, half),
+                    lambda half=half: copy_grouped((name, half), grouped, half),
+                )
+                for half in range(2)
+            ]
 
         def quantise_h0(c):
             state0_of[c] = quantise(nc, mx, h0_of[c], "h0")
@@ -216,28 +228,54 @@ def tile_liquidcell_pb_t_kernel(
                 nc.vector.tensor_tensor(out=move[:, m, :], in0=drive[:], in1=ic_of[c][:, m // PAIR, :, m % PAIR], op=ALU.add)
             for m in range(PACK):
                 logits = weight_times_state(nc, products, tau_weight, m, state)
-                nc.vector.scalar_tensor_tensor(
-                    out=rate[:, m, :], in0=logits[:], scalar=adapt_b[:, m : m + 1],
-                    in1=x_of[c][:, m // PAIR, :, m % PAIR], op0=ALU.add, op1=ALU.add,
-                )
+                if B_ON_SCALAR[step - 1]:
+                    nc.vector.tensor_tensor(out=rate[:, m, :], in0=logits[:], in1=x_of[c][:, m // PAIR, :, m % PAIR], op=ALU.add)
+                else:
+                    nc.vector.scalar_tensor_tensor(
+                        out=rate[:, m, :], in0=logits[:], scalar=adapt_b[:, m : m + 1],
+                        in1=x_of[c][:, m // PAIR, :, m % PAIR], op0=ALU.add, op1=ALU.add,
+                    )
 
         def tanh_move(c):
             move = move_of[c]
             for w in s_wide_tiles():
                 nc.scalar.activation(out=move[:, w, :], in_=move[:, w, :], func=ACT.Tanh)
 
-        def tanh_tau2(c):
+        def tanh_tau2(c, logits=None):
             tau2 = step2.tile([P, PACK, CHUNK], F32, tag="tau2")
             tau2_of[c] = tau2
-            for w in s_wide_tiles():
-                nc.scalar.activation(out=tau2[:, w, :], in_=rate_of[c][:, w, :], func=ACT.Tanh, scale=0.5)
+            if logits is None:
+                logits = rate_of[c]
+            if B_ON_SCALAR[1]:
+                for m in range(PACK):
+                    nc.scalar.activation(
+                        out=tau2[:, m, :], in_=logits[:, m, :], func=ACT.Tanh, bias=bias_tau[:, m : m + 1], scale=0.5
+                    )
+            else:
+                for w in s_wide_tiles():
+                    nc.scalar.activation(out=tau2[:, w, :], in_=logits[:, w, :], func=ACT.Tanh, scale=0.5)
 
-        def tanh_rate(c):
-            rate = rate_of[c]
+        def tanh_rate_into_new_tile(c):
+            logits = rate_of[c]
+            rate = step2.tile([P, PACK, CHUNK], F32, tag="rate")
             for w in s_wide_tiles():
                 nc.scalar.activation(
-                    out=rate[:, w, :], in_=rate[:, w, :], func=ACT.Tanh, bias=0.5 * math.log(3.0), scale=0.5
+                    out=rate[:, w, :], in_=logits[:, w, :], func=ACT.Tanh, bias=0.5 * math.log(3.0), scale=0.5
                 )
+            return rate
+
+        def tanh_rate(c, step):
+            rate = rate_of[c]
+            if B_ON_SCALAR[step - 1]:
+                for m in range(PACK):
+                    nc.scalar.activation(
+                        out=rate[:, m, :], in_=rate[:, m, :], func=ACT.Tanh, bias=bias_rate[:, m : m + 1], scale=0.5
+                    )
+            else:
+                for w in s_wide_tiles():
+                    nc.scalar.activation(
+                        out=rate[:, w, :], in_=rate[:, w, :], func=ACT.Tanh, bias=0.5 * math.log(3.0), scale=0.5
+                    )
 
         def subtract_h1(c, engine):
             move = move_of[c]
@@ -250,6 +288,14 @@ def tile_liquidcell_pb_t_kernel(
                 engine.tensor_scalar(
                     out=tau2[:, m, :], in0=tau2[:, m, :],
                     scalar1=half_base[:, m : m + 1], scalar2=base[:, m : m + 1], op0=ALU.mult, op1=ALU.add,
+                )
+
+        def finish_tau2_on_scalar(c, tiles):
+            tau2 = tau2_of[c]
+            for m in tiles:
+                nc.scalar.activation(
+                    out=tau2[:, m, :], in_=tau2[:, m, :], func=ACT.Identity,
+                    bias=base[:, m : m + 1], scale=half_base[:, m : m + 1],
                 )
 
         def subtract_h0(c):
@@ -271,6 +317,14 @@ def tile_liquidcell_pb_t_kernel(
                 engine.tensor_scalar(
                     out=rate[:, m, :], in0=rate[:, m, :],
                     scalar1=gain[:, m : m + 1], scalar2=minus_two_gain[:, m : m + 1], op0=ALU.mult, op1=ALU.add,
+                )
+
+        def scale_rate_on_scalar(c):
+            rate = rate_of[c]
+            for m in range(PACK):
+                nc.scalar.activation(
+                    out=rate[:, m, :], in_=rate[:, m, :], func=ACT.Identity,
+                    bias=minus_two_gain[:, m : m + 1], scale=gain[:, m : m + 1],
                 )
 
         def times_scaled_rate(c):
@@ -350,10 +404,19 @@ def tile_liquidcell_pb_t_kernel(
         def in_range(c):
             return 0 <= c < N_CHUNKS
 
-        load(0)
+        rows_of[0] = (first_h_rows, first_ic_rows, first_x_rows)
         load(1)
-        run_jobs(flip_jobs(0), {})
+        rec_grouped = flips.tile([P, CHUNK * PACK], BF16, tag="h1_grouped", align_bytes=64)
+        tau_grouped = flips.tile([P, CHUNK * PACK], BF16, tag="h1_grouped", align_bytes=64)
+        first_jobs = flip_jobs(0)
+        run_jobs(
+            first_jobs[0:2] + weight_jobs("rec", rec_weight_rows, rec_grouped) + first_jobs[2:4]
+            + weight_jobs("tau", tau_weight_rows, tau_grouped) + first_jobs[4:6],
+            {},
+        )
         quantise_h0(0)
+        rec_weight = quantise(nc, const, rec_grouped, "rec_weight")
+        tau_weight = quantise(nc, const, tau_grouped, "tau_weight")
         LAST = N_CHUNKS - 1
         for i in range(N_CHUNKS):
             if in_range(i + 2):
@@ -365,13 +428,14 @@ def tile_liquidcell_pb_t_kernel(
                 finish_tau2(i - 2, nc.gpsimd, range(G_AFFINE))
             products_and_sums(i, 1)
             tanh_move(i)
-            tanh_rate(i)
+            tanh_rate(i, 1)
             if in_range(i - 1):
                 products_and_sums(i - 1, 2)
                 tanh_move(i - 1)
             if in_range(i - 2):
                 times_scaled_rate(i - 2)
-                finish_tau2(i - 2, nc.vector, range(G_AFFINE, PACK))
+                finish_tau2_on_scalar(i - 2, range(G_AFFINE, G_AFFINE + S_AFFINE))
+                finish_tau2(i - 2, nc.vector, range(G_AFFINE + S_AFFINE, PACK))
             jobs = []
             before = {}
             if in_range(i + 1):
@@ -382,9 +446,9 @@ def tile_liquidcell_pb_t_kernel(
                 jobs.extend(tau2_jobs(i - 2))
             if in_range(i - 1):
                 if len(jobs) in before:
-                    before[len(jobs)] = lambda: (tanh_tau2(i - 1), tanh_rate(i - 1))
+                    before[len(jobs)] = lambda: (tanh_tau2(i - 1), tanh_rate(i - 1, 2))
                 else:
-                    before[len(jobs)] = lambda: tanh_rate(i - 1)
+                    before[len(jobs)] = lambda: tanh_rate(i - 1, 2)
             if in_range(i - 2):
                 jobs.extend(h2_jobs(i - 2))
             run_jobs(jobs, before)
@@ -400,16 +464,20 @@ def tile_liquidcell_pb_t_kernel(
 
         hold_gpsimd(LAST)
         subtract_h1(LAST - 1, nc.gpsimd)
+        finish_tau2_on_scalar(LAST - 1, range(PACK))
+        scale_rate_on_scalar(LAST - 1)
         products_and_sums(LAST, 2)
-        tanh_move(LAST)
-        tanh_tau2(LAST)
-        tanh_rate(LAST)
-        scale_rate(LAST - 1, nc.vector)
         times_scaled_rate(LAST - 1)
-        finish_tau2(LAST - 1, nc.vector, range(PACK))
-        run_jobs(h2_jobs(LAST - 1) + tau2_jobs(LAST - 1), {})
+        tanh_move(LAST)
+        logits_of_last = rate_of[LAST]
+        rate_of[LAST] = tanh_rate_into_new_tile(LAST)
         subtract_h1(LAST, nc.vector)
         scale_rate(LAST, nc.vector)
         times_scaled_rate(LAST)
-        finish_tau2(LAST, nc.vector, range(PACK))
-        run_jobs(h2_jobs(LAST) + tau2_jobs(LAST, on_vector=True), {})
+        run_jobs(
+            tau2_jobs(LAST - 1) + h2_jobs(LAST - 1) + h2_jobs(LAST) + tau2_jobs(LAST, on_vector=True),
+            {
+                BLOCKS: lambda: tanh_tau2(LAST, logits_of_last),
+                3 * BLOCKS - N_TURN_BANKS: lambda: finish_tau2(LAST, nc.vector, range(PACK)),
+            },
+        )

@@ -25,8 +25,8 @@ N_CHUNKS = B // CHUNK
 WIDE = 2
 S_WIDE = 4
 N_PRODUCT_BANKS = 3
-G_AFFINE = 2
-S_AFFINE = 1
+G_AFFINE = 4
+S_AFFINE = 0
 B_ON_SCALAR = (True, False)
 N_TURN_BANKS = 8 - N_PRODUCT_BANKS
 
@@ -122,6 +122,11 @@ def tile_liquidcell_pb_t_kernel(
         nc.vector.tensor_scalar(
             out=gain[:], in0=inverse_base[:], scalar1=-2.0 * DT / 3.0, scalar2=None, op0=ALU.mult
         )
+        gain_diagonal = const.tile([P, PACK, P], F32)
+        for m in range(PACK):
+            nc.vector.tensor_scalar(
+                out=gain_diagonal[:, m, :], in0=ident_f32[:], scalar1=gain[:, m : m + 1], scalar2=None, op0=ALU.mult
+            )
         minus_two_gain = const.tile([P, PACK], F32)
         nc.vector.tensor_scalar(out=minus_two_gain[:], in0=gain[:], scalar1=-2.0, scalar2=None, op0=ALU.mult)
 
@@ -392,10 +397,10 @@ def tile_liquidcell_pb_t_kernel(
                 for j in range(BLOCKS)
             ]
 
-        def h2_jobs(c, on_vector=False):
+        def h2_jobs(c, on_vector=False, scaled=False):
             return [
                 (
-                    lambda j=j: unflip_pe((c, "h2", j), [(h1_of[c], None), (move_of[c], None)], j),
+                    lambda j=j: unflip_pe((c, "h2", j), [(h1_of[c], None), (move_of[c], None if scaled else gain_diagonal)], j),
                     lambda j=j: unflip_copy((c, "h2", j), out_0[chunk_rows(c), :], j, on_vector),
                 )
                 for j in range(BLOCKS)
@@ -424,7 +429,6 @@ def tile_liquidcell_pb_t_kernel(
             if in_range(i - 2):
                 hold_gpsimd(i - 1)
                 subtract_h1(i - 2, nc.gpsimd)
-                scale_rate(i - 2, nc.gpsimd)
                 finish_tau2(i - 2, nc.gpsimd, range(G_AFFINE))
             products_and_sums(i, 1)
             tanh_move(i)
@@ -433,7 +437,7 @@ def tile_liquidcell_pb_t_kernel(
                 products_and_sums(i - 1, 2)
                 tanh_move(i - 1)
             if in_range(i - 2):
-                times_scaled_rate(i - 2)
+                times_rate(i - 2)
                 finish_tau2_on_scalar(i - 2, range(G_AFFINE, G_AFFINE + S_AFFINE))
                 finish_tau2(i - 2, nc.vector, range(G_AFFINE + S_AFFINE, PACK))
             jobs = []
@@ -475,7 +479,8 @@ def tile_liquidcell_pb_t_kernel(
         scale_rate(LAST, nc.vector)
         times_scaled_rate(LAST)
         run_jobs(
-            tau2_jobs(LAST - 1) + h2_jobs(LAST - 1) + h2_jobs(LAST) + tau2_jobs(LAST, on_vector=True),
+            tau2_jobs(LAST - 1) + h2_jobs(LAST - 1, scaled=True) + h2_jobs(LAST, scaled=True)
+            + tau2_jobs(LAST, on_vector=True),
             {
                 BLOCKS: lambda: tanh_tau2(LAST, logits_of_last),
                 3 * BLOCKS - N_TURN_BANKS: lambda: finish_tau2(LAST, nc.vector, range(PACK)),

@@ -22,19 +22,16 @@ CHUNK = 512
 BLOCKS = CHUNK // P
 HALF = CHUNK // 2
 N_CHUNKS = B // CHUNK
-WIDE = 2
-S_WIDE = 4
+LAST = N_CHUNKS - 1
+HALF_LN_3 = 0.5 * math.log(3.0)
+TILE_PAIRS = (slice(0, 2), slice(2, 4))
 N_PRODUCT_BANKS = 3
-G_AFFINE = 4
-S_AFFINE = 0
-B_ON_SCALAR = (True, False)
-N_TURN_BANKS = 8 - N_PRODUCT_BANKS
+N_TURN_BANKS = 5
 
 FLOPS = 4 * 2 * B * H * H
 
 
-def load_rows(nc, pool, dram_rows):
-    rows = pool.tile([P, BLOCKS, H], BF16, tag="rows")
+def load_rows(nc, rows, dram_rows):
     nc.sync.dma_start(out=rows[:], in_=dram_rows.rearrange("(p j) f -> p j f", j=BLOCKS))
     return rows
 
@@ -85,32 +82,35 @@ def tile_liquidcell_pb_t_kernel(
         step1 = ctx.enter_context(tc.tile_pool(name="step1", bufs=1))
         step2 = ctx.enter_context(tc.tile_pool(name="step2", bufs=3))
         states = ctx.enter_context(tc.tile_pool(name="states", bufs=3))
-        stores = ctx.enter_context(tc.tile_pool(name="stores", bufs=8))
+        stores = ctx.enter_context(tc.tile_pool(name="stores", bufs=2 * BLOCKS))
         products = ctx.enter_context(tc.psum_pool(name="products", bufs=N_PRODUCT_BANKS))
-        turns = ctx.enter_context(tc.psum_pool(name="turns", bufs=8 - N_PRODUCT_BANKS))
+        turns = ctx.enter_context(tc.psum_pool(name="turns", bufs=N_TURN_BANKS))
 
         ident_f32 = const.tile([P, P], F32)
         make_identity(nc, ident_f32[:])
+
+        def new_rows():
+            rows = loads.tile([P, BLOCKS, H], BF16, tag="rows")
+            return rows
 
         adapt_b_bf16 = const.tile([P, PACK], BF16)
         nc.sync.dma_start(out=adapt_b_bf16[:], in_=tau_adapt_b.rearrange("(p m) -> p m", m=PACK))
         base_bf16 = const.tile([P, PACK], BF16)
         nc.sync.dma_start(out=base_bf16[:], in_=tau_base.rearrange("(p m) -> p m", m=PACK))
-        first_h_rows = load_rows(nc, loads, h[0:CHUNK, :])
+
+        first_h_rows = load_rows(nc, new_rows(), h[0:CHUNK, :])
         rec_weight_rows = const.tile([P, BLOCKS, H], BF16)
-        nc.sync.dma_start(out=rec_weight_rows[:], in_=W_rec.rearrange("(p j) f -> p j f", j=BLOCKS))
-        first_ic_rows = load_rows(nc, loads, input_contrib[0:CHUNK, :])
+        load_rows(nc, rec_weight_rows, W_rec)
+        first_ic_rows = load_rows(nc, new_rows(), input_contrib[0:CHUNK, :])
         tau_weight_rows = const.tile([P, BLOCKS, H], BF16)
-        nc.sync.dma_start(out=tau_weight_rows[:], in_=tau_w_h.rearrange("(p j) f -> p j f", j=BLOCKS))
-        first_x_rows = load_rows(nc, loads, x_tau[0:CHUNK, :])
+        load_rows(nc, tau_weight_rows, tau_w_h)
+        first_x_rows = load_rows(nc, new_rows(), x_tau[0:CHUNK, :])
 
         adapt_b = const.tile([P, PACK], F32)
         nc.vector.tensor_copy(out=adapt_b[:], in_=adapt_b_bf16[:])
-        bias_tau = const.tile([P, PACK], F32)
-        nc.vector.tensor_scalar(out=bias_tau[:], in0=adapt_b_bf16[:], scalar1=0.5, scalar2=None, op0=ALU.mult)
         bias_rate = const.tile([P, PACK], F32)
         nc.vector.tensor_scalar(
-            out=bias_rate[:], in0=adapt_b_bf16[:], scalar1=0.5, scalar2=0.5 * math.log(3.0), op0=ALU.mult, op1=ALU.add
+            out=bias_rate[:], in0=adapt_b_bf16[:], scalar1=0.5, scalar2=HALF_LN_3, op0=ALU.mult, op1=ALU.add
         )
         base = const.tile([P, PACK], F32)
         nc.vector.tensor_copy(out=base[:], in_=base_bf16[:])
@@ -131,110 +131,157 @@ def tile_liquidcell_pb_t_kernel(
         nc.vector.tensor_scalar(out=minus_two_gain[:], in0=gain[:], scalar1=-2.0, scalar2=None, op0=ALU.mult)
 
         rows_of = {}
-        turned_of = {}
+        weight_of = {}
         h0_of = {}
-        x_of = {}
         ic_of = {}
-        state0_of = {}
-        state1_of = {}
+        x_of = {}
+        h0_codes_of = {}
+        h1_codes_of = {}
         rate_of = {}
         move_of = {}
         h1_of = {}
+        h1_grouped_of = {}
         tau2_of = {}
-        grouped_h1_of = {}
 
         def chunk_rows(c):
             return slice(c * CHUNK, (c + 1) * CHUNK)
 
-        def wide_tiles():
-            return [slice(m, m + WIDE) for m in range(0, PACK, WIDE)]
-
-        def s_wide_tiles():
-            return [slice(m, m + S_WIDE) for m in range(0, PACK, S_WIDE)]
+        def in_range(c):
+            return 0 <= c < N_CHUNKS
 
         def load(c):
             rows_of[c] = (
-                load_rows(nc, loads, h[chunk_rows(c), :]),
-                load_rows(nc, loads, input_contrib[chunk_rows(c), :]),
-                load_rows(nc, loads, x_tau[chunk_rows(c), :]),
+                load_rows(nc, new_rows(), h[chunk_rows(c), :]),
+                load_rows(nc, new_rows(), input_contrib[chunk_rows(c), :]),
+                load_rows(nc, new_rows(), x_tau[chunk_rows(c), :]),
             )
 
-        def flip_pe(key, rows, half):
-            turned_of[key] = flip_half(nc, turns, rows, half, ident_f32)
-
-        def grouped_tile(pool):
-            grouped = pool.tile([P, CHUNK * PACK], BF16, tag="grouped", align_bytes=64)
-            return grouped
+        filled_bank = {}
 
         def copy_grouped(key, grouped, half):
             grouped_words = grouped[:].bitcast(F32).rearrange("p (c u) -> p c u", u=PAIR)
             nc.scalar.copy(
                 out=grouped_words[:, half * HALF : (half + 1) * HALF, :],
-                in_=turned_of[key][:].rearrange("p u c -> p c u"),
+                in_=filled_bank[key][:].rearrange("p u c -> p c u"),
             )
 
         def copy_plain(key, plain, half):
             plain_words = plain[:].bitcast(F32).rearrange("p (u c) -> p u c", u=PAIR)
-            nc.scalar.copy(out=plain_words[:, :, half * HALF : (half + 1) * HALF], in_=turned_of[key][:])
+            nc.scalar.copy(out=plain_words[:, :, half * HALF : (half + 1) * HALF], in_=filled_bank[key][:])
 
-        def plain_view(plain):
-            return plain[:].rearrange("p (u c e) -> p u c e", u=PAIR, e=PAIR)
+        def fill_flipped(key, rows, half):
+            filled_bank[key] = flip_half(nc, turns, rows, half, ident_f32)
 
-        def flip_jobs(c):
-            h0_of[c] = grouped_tile(flips)
-            ic_plain = plains.tile([P, PACK * CHUNK], BF16, tag="ic")
-            ic_of[c] = plain_view(ic_plain)
-            x_plain = plains.tile([P, PACK * CHUNK], BF16, tag="x")
-            x_of[c] = plain_view(x_plain)
-            jobs = []
-            for half in range(2):
-                jobs.append((
-                    lambda half=half: flip_pe((c, 0, half), rows_of[c][0], half),
-                    lambda half=half: copy_grouped((c, 0, half), h0_of[c], half),
-                ))
-            for n, plain in ((1, ic_plain), (2, x_plain)):
-                for half in range(2):
-                    jobs.append((
-                        lambda n=n, half=half: flip_pe((c, n, half), rows_of[c][n], half),
-                        lambda n=n, half=half, plain=plain: copy_plain((c, n, half), plain, half),
-                    ))
-            return jobs
-
-        def run_jobs(jobs, before):
-            filled = 0
-            for k in range(len(jobs)):
-                while filled < min(k + N_TURN_BANKS, len(jobs)):
-                    jobs[filled][0]()
-                    filled += 1
-                if k in before:
-                    before[k]()
-                jobs[k][1]()
-
-        def weight_jobs(name, rows, grouped):
+        def grouped_jobs(name, rows, grouped):
             return [
                 (
-                    lambda half=half: flip_pe((name, half), rows, half),
+                    lambda half=half: fill_flipped((name, half), rows, half),
                     lambda half=half: copy_grouped((name, half), grouped, half),
                 )
                 for half in range(2)
             ]
 
+        def plain_jobs(name, rows, plain):
+            return [
+                (
+                    lambda half=half: fill_flipped((name, half), rows, half),
+                    lambda half=half: copy_plain((name, half), plain, half),
+                )
+                for half in range(2)
+            ]
+
+        def flip_jobs(c):
+            h_rows, ic_rows, x_rows = rows_of[c]
+            h0 = flips.tile([P, CHUNK * PACK], BF16, tag="grouped", align_bytes=64)
+            ic_plain = plains.tile([P, PACK * CHUNK], BF16, tag="ic")
+            x_plain = plains.tile([P, PACK * CHUNK], BF16, tag="x")
+            h0_of[c] = h0
+            ic_of[c] = ic_plain[:].rearrange("p (u c e) -> p u c e", u=PAIR, e=PAIR)
+            x_of[c] = x_plain[:].rearrange("p (u c e) -> p u c e", u=PAIR, e=PAIR)
+            return (
+                grouped_jobs((c, "h"), h_rows, h0) + plain_jobs((c, "ic"), ic_rows, ic_plain)
+                + plain_jobs((c, "x"), x_rows, x_plain)
+            )
+
+        def fill_rows(key, terms, j):
+            back = turns.tile([P, PACK, P], F32, tag="turned")
+            filled_bank[key] = back
+            for m in range(PACK):
+                for n, (term, factors) in enumerate(terms):
+                    nc.tensor.matmul(
+                        out=back[:, m, :],
+                        lhsT=term[:, m, j * P : (j + 1) * P],
+                        rhs=ident_f32[:] if factors is None else factors[:, m, :],
+                        is_transpose=factors is None,
+                        start=(n == 0),
+                        stop=(n == len(terms) - 1),
+                    )
+
+        def copy_and_store_rows(key, dram_rows, j, on_vector):
+            rows = stores.tile([P, H], F32, tag="out_rows")
+            out_view = rows[:].rearrange("r (p m) -> r p m", m=PACK)
+            in_view = filled_bank[key][:].rearrange("r m p -> r p m")
+            if on_vector:
+                nc.vector.tensor_copy(out=out_view, in_=in_view)
+            else:
+                nc.scalar.copy(out=out_view, in_=in_view)
+            nc.sync.dma_start(out=dram_rows.rearrange("(p j) f -> p j f", j=BLOCKS)[:, j, :], in_=rows[:])
+
+        def tau2_jobs(c, on_vector=False):
+            return [
+                (
+                    lambda j=j: fill_rows((c, "tau2", j), [(tau2_of[c], None)], j),
+                    lambda j=j: copy_and_store_rows((c, "tau2", j), out_1[chunk_rows(c), :], j, on_vector),
+                )
+                for j in range(BLOCKS)
+            ]
+
+        def h2_jobs(c, factors):
+            return [
+                (
+                    lambda j=j: fill_rows((c, "h2", j), [(h1_of[c], None), (move_of[c], factors)], j),
+                    lambda j=j: copy_and_store_rows((c, "h2", j), out_0[chunk_rows(c), :], j, False),
+                )
+                for j in range(BLOCKS)
+            ]
+
+        def run_jobs(stages):
+            jobs = []
+            work_before = {}
+            for work, stage_jobs in stages:
+                if work is not None:
+                    work_before.setdefault(len(jobs), []).append(work)
+                jobs.extend(stage_jobs)
+            filled = 0
+            for k in range(len(jobs) + 1):
+                while filled < min(k + N_TURN_BANKS, len(jobs)):
+                    jobs[filled][0]()
+                    filled += 1
+                for work in work_before.get(k, []):
+                    work()
+                if k < len(jobs):
+                    jobs[k][1]()
+
         def quantise_h0(c):
-            state0_of[c] = quantise(nc, mx, h0_of[c], "h0")
+            h0_codes_of[c] = quantise(nc, mx, h0_of[c], "h0")
 
         def products_and_sums(c, step):
             pool = step1 if step == 1 else step2
-            state = state0_of[c] if step == 1 else state1_of[c]
+            state = h0_codes_of[c] if step == 1 else h1_codes_of[c]
             rate = pool.tile([P, PACK, CHUNK], F32, tag="rate")
             move = pool.tile([P, PACK, CHUNK], F32, tag="move")
             rate_of[c], move_of[c] = rate, move
             for m in range(PACK):
-                drive = weight_times_state(nc, products, rec_weight, m, state)
-                nc.vector.tensor_tensor(out=move[:, m, :], in0=drive[:], in1=ic_of[c][:, m // PAIR, :, m % PAIR], op=ALU.add)
+                drive = weight_times_state(nc, products, weight_of["rec"], m, state)
+                nc.vector.tensor_tensor(
+                    out=move[:, m, :], in0=drive[:], in1=ic_of[c][:, m // PAIR, :, m % PAIR], op=ALU.add
+                )
             for m in range(PACK):
-                logits = weight_times_state(nc, products, tau_weight, m, state)
-                if B_ON_SCALAR[step - 1]:
-                    nc.vector.tensor_tensor(out=rate[:, m, :], in0=logits[:], in1=x_of[c][:, m // PAIR, :, m % PAIR], op=ALU.add)
+                logits = weight_times_state(nc, products, weight_of["tau"], m, state)
+                if step == 1:
+                    nc.vector.tensor_tensor(
+                        out=rate[:, m, :], in0=logits[:], in1=x_of[c][:, m // PAIR, :, m % PAIR], op=ALU.add
+                    )
                 else:
                     nc.vector.scalar_tensor_tensor(
                         out=rate[:, m, :], in0=logits[:], scalar=adapt_b[:, m : m + 1],
@@ -242,100 +289,35 @@ def tile_liquidcell_pb_t_kernel(
                     )
 
         def tanh_move(c):
-            move = move_of[c]
-            for w in s_wide_tiles():
-                nc.scalar.activation(out=move[:, w, :], in_=move[:, w, :], func=ACT.Tanh)
+            nc.scalar.activation(out=move_of[c][:], in_=move_of[c][:], func=ACT.Tanh)
 
-        def tanh_tau2(c, logits=None):
+        def tanh_rate_1(c):
+            rate = rate_of[c]
+            for m in range(PACK):
+                nc.scalar.activation(
+                    out=rate[:, m, :], in_=rate[:, m, :], func=ACT.Tanh, bias=bias_rate[:, m : m + 1], scale=0.5
+                )
+
+        def tanh_rate_2(c, rate):
+            nc.scalar.activation(out=rate[:], in_=rate_of[c][:], func=ACT.Tanh, bias=HALF_LN_3, scale=0.5)
+
+        def tanh_tau2(c, logits):
             tau2 = step2.tile([P, PACK, CHUNK], F32, tag="tau2")
             tau2_of[c] = tau2
-            if logits is None:
-                logits = rate_of[c]
-            if B_ON_SCALAR[1]:
-                for m in range(PACK):
-                    nc.scalar.activation(
-                        out=tau2[:, m, :], in_=logits[:, m, :], func=ACT.Tanh, bias=bias_tau[:, m : m + 1], scale=0.5
-                    )
-            else:
-                for w in s_wide_tiles():
-                    nc.scalar.activation(out=tau2[:, w, :], in_=logits[:, w, :], func=ACT.Tanh, scale=0.5)
-
-        def tanh_rate_into_new_tile(c):
-            logits = rate_of[c]
-            rate = step2.tile([P, PACK, CHUNK], F32, tag="rate")
-            for w in s_wide_tiles():
-                nc.scalar.activation(
-                    out=rate[:, w, :], in_=logits[:, w, :], func=ACT.Tanh, bias=0.5 * math.log(3.0), scale=0.5
-                )
-            return rate
-
-        def tanh_rate(c, step):
-            rate = rate_of[c]
-            if B_ON_SCALAR[step - 1]:
-                for m in range(PACK):
-                    nc.scalar.activation(
-                        out=rate[:, m, :], in_=rate[:, m, :], func=ACT.Tanh, bias=bias_rate[:, m : m + 1], scale=0.5
-                    )
-            else:
-                for w in s_wide_tiles():
-                    nc.scalar.activation(
-                        out=rate[:, w, :], in_=rate[:, w, :], func=ACT.Tanh, bias=0.5 * math.log(3.0), scale=0.5
-                    )
-
-        def subtract_h1(c, engine):
-            move = move_of[c]
-            for w in wide_tiles():
-                engine.tensor_tensor(out=move[:, w, :], in0=move[:, w, :], in1=h1_of[c][:, w, :], op=ALU.subtract)
-
-        def finish_tau2(c, engine, tiles):
-            tau2 = tau2_of[c]
-            for m in tiles:
-                engine.tensor_scalar(
-                    out=tau2[:, m, :], in0=tau2[:, m, :],
-                    scalar1=half_base[:, m : m + 1], scalar2=base[:, m : m + 1], op0=ALU.mult, op1=ALU.add,
-                )
-
-        def finish_tau2_on_scalar(c, tiles):
-            tau2 = tau2_of[c]
-            for m in tiles:
-                nc.scalar.activation(
-                    out=tau2[:, m, :], in_=tau2[:, m, :], func=ACT.Identity,
-                    bias=base[:, m : m + 1], scale=half_base[:, m : m + 1],
-                )
+            nc.scalar.activation(out=tau2[:], in_=logits[:], func=ACT.Tanh, scale=0.5)
 
         def subtract_h0(c):
             move, h0 = move_of[c], h0_of[c][:].rearrange("p (c t) -> p t c", t=PACK)
-            for w in wide_tiles():
+            for w in TILE_PAIRS:
                 nc.vector.tensor_tensor(out=move[:, w, :], in0=move[:, w, :], in1=h0[:, w, :], op=ALU.subtract)
 
         def times_rate(c):
             rate, move = rate_of[c], move_of[c]
-            for w in wide_tiles():
+            for w in TILE_PAIRS:
                 nc.vector.scalar_tensor_tensor(
                     out=move[:, w, :], in0=rate[:, w, :], scalar=2.0, in1=move[:, w, :],
                     op0=ALU.subtract, op1=ALU.mult,
                 )
-
-        def scale_rate(c, engine):
-            rate = rate_of[c]
-            for m in range(PACK):
-                engine.tensor_scalar(
-                    out=rate[:, m, :], in0=rate[:, m, :],
-                    scalar1=gain[:, m : m + 1], scalar2=minus_two_gain[:, m : m + 1], op0=ALU.mult, op1=ALU.add,
-                )
-
-        def scale_rate_on_scalar(c):
-            rate = rate_of[c]
-            for m in range(PACK):
-                nc.scalar.activation(
-                    out=rate[:, m, :], in_=rate[:, m, :], func=ACT.Identity,
-                    bias=minus_two_gain[:, m : m + 1], scale=gain[:, m : m + 1],
-                )
-
-        def times_scaled_rate(c):
-            rate, move = rate_of[c], move_of[c]
-            for w in wide_tiles():
-                nc.vector.tensor_tensor(out=move[:, w, :], in0=rate[:, w, :], in1=move[:, w, :], op=ALU.mult)
 
         def make_h1(c):
             move, h0 = move_of[c], h0_of[c][:].rearrange("p (c t) -> p t c", t=PACK)
@@ -349,115 +331,82 @@ def tile_liquidcell_pb_t_kernel(
 
         def round_h1(c):
             h1_grouped = flips.tile([P, CHUNK * PACK], BF16, tag="h1_grouped", align_bytes=64)
+            h1_grouped_of[c] = h1_grouped
             nc.vector.tensor_copy(
                 out=h1_grouped[:].rearrange("p (c t) -> p c t", t=PACK), in_=h1_of[c][:].rearrange("p t c -> p c t")
             )
-            grouped_h1_of[c] = h1_grouped
 
         def quantise_h1(c):
-            state1_of[c] = quantise(nc, mx, grouped_h1_of[c], "h1")
+            h1_codes_of[c] = quantise(nc, mx, h1_grouped_of[c], "h1")
+
+        def subtract_h1(c, engine):
+            move = move_of[c]
+            for w in TILE_PAIRS:
+                engine.tensor_tensor(out=move[:, w, :], in0=move[:, w, :], in1=h1_of[c][:, w, :], op=ALU.subtract)
+
+        def finish_tau2(c, engine):
+            tau2 = tau2_of[c]
+            for m in range(PACK):
+                engine.tensor_scalar(
+                    out=tau2[:, m, :], in0=tau2[:, m, :],
+                    scalar1=half_base[:, m : m + 1], scalar2=base[:, m : m + 1], op0=ALU.mult, op1=ALU.add,
+                )
+
+        def finish_tau2_on_scalar(c):
+            tau2 = tau2_of[c]
+            for m in range(PACK):
+                nc.scalar.activation(
+                    out=tau2[:, m, :], in_=tau2[:, m, :], func=ACT.Identity,
+                    bias=base[:, m : m + 1], scale=half_base[:, m : m + 1],
+                )
 
         gate_word = const.tile([P, 1], U32)
 
-        def hold_gpsimd(c):
-            nc.gpsimd.tensor_copy(out=gate_word[:], in_=state1_of[c][0][:, 0:1])
-
-        def unflip_pe(key, terms, j):
-            back = turns.tile([P, PACK, P], F32, tag="turned")
-            turned_of[key] = back
-            for m in range(PACK):
-                for n, (term, factors) in enumerate(terms):
-                    nc.tensor.matmul(
-                        out=back[:, m, :],
-                        lhsT=term[:, m, j * P : (j + 1) * P],
-                        rhs=ident_f32[:] if factors is None else factors[:, m, :],
-                        is_transpose=factors is None,
-                        start=(n == 0),
-                        stop=(n == len(terms) - 1),
-                    )
-
-        def unflip_copy(key, dram_rows, j, on_vector):
-            rows = stores.tile([P, H], F32, tag="out_rows")
-            if on_vector:
-                nc.vector.tensor_copy(
-                    out=rows[:].rearrange("r (p m) -> r p m", m=PACK), in_=turned_of[key][:].rearrange("r m p -> r p m")
-                )
-            else:
-                nc.scalar.copy(
-                    out=rows[:].rearrange("r (p m) -> r p m", m=PACK), in_=turned_of[key][:].rearrange("r m p -> r p m")
-                )
-            nc.sync.dma_start(out=dram_rows.rearrange("(p j) f -> p j f", j=BLOCKS)[:, j, :], in_=rows[:])
-
-        def tau2_jobs(c, on_vector=False):
-            return [
-                (
-                    lambda j=j: unflip_pe((c, "tau2", j), [(tau2_of[c], None)], j),
-                    lambda j=j: unflip_copy((c, "tau2", j), out_1[chunk_rows(c), :], j, on_vector),
-                )
-                for j in range(BLOCKS)
-            ]
-
-        def h2_jobs(c, on_vector=False, scaled=False):
-            return [
-                (
-                    lambda j=j: unflip_pe((c, "h2", j), [(h1_of[c], None), (move_of[c], None if scaled else gain_diagonal)], j),
-                    lambda j=j: unflip_copy((c, "h2", j), out_0[chunk_rows(c), :], j, on_vector),
-                )
-                for j in range(BLOCKS)
-            ]
-
-        def in_range(c):
-            return 0 <= c < N_CHUNKS
+        def hold_gpsimd_until_h1_is_quantised(c):
+            nc.gpsimd.tensor_copy(out=gate_word[:], in_=h1_codes_of[c][0][:, 0:1])
 
         rows_of[0] = (first_h_rows, first_ic_rows, first_x_rows)
         load(1)
         rec_grouped = flips.tile([P, CHUNK * PACK], BF16, tag="h1_grouped", align_bytes=64)
         tau_grouped = flips.tile([P, CHUNK * PACK], BF16, tag="h1_grouped", align_bytes=64)
         first_jobs = flip_jobs(0)
-        run_jobs(
-            first_jobs[0:2] + weight_jobs("rec", rec_weight_rows, rec_grouped) + first_jobs[2:4]
-            + weight_jobs("tau", tau_weight_rows, tau_grouped) + first_jobs[4:6],
-            {},
-        )
+        run_jobs([
+            (None, first_jobs[0:2]),
+            (None, grouped_jobs("rec", rec_weight_rows, rec_grouped)),
+            (None, first_jobs[2:4]),
+            (None, grouped_jobs("tau", tau_weight_rows, tau_grouped)),
+            (None, first_jobs[4:6]),
+        ])
         quantise_h0(0)
-        rec_weight = quantise(nc, const, rec_grouped, "rec_weight")
-        tau_weight = quantise(nc, const, tau_grouped, "tau_weight")
-        LAST = N_CHUNKS - 1
+        weight_of["rec"] = quantise(nc, const, rec_grouped, "rec_weight")
+        weight_of["tau"] = quantise(nc, const, tau_grouped, "tau_weight")
+
         for i in range(N_CHUNKS):
             if in_range(i + 2):
                 load(i + 2)
             if in_range(i - 2):
-                hold_gpsimd(i - 1)
+                hold_gpsimd_until_h1_is_quantised(i - 1)
                 subtract_h1(i - 2, nc.gpsimd)
-                finish_tau2(i - 2, nc.gpsimd, range(G_AFFINE))
+                finish_tau2(i - 2, nc.gpsimd)
             products_and_sums(i, 1)
             tanh_move(i)
-            tanh_rate(i, 1)
+            tanh_rate_1(i)
             if in_range(i - 1):
                 products_and_sums(i - 1, 2)
                 tanh_move(i - 1)
             if in_range(i - 2):
                 times_rate(i - 2)
-                finish_tau2_on_scalar(i - 2, range(G_AFFINE, G_AFFINE + S_AFFINE))
-                finish_tau2(i - 2, nc.vector, range(G_AFFINE + S_AFFINE, PACK))
-            jobs = []
-            before = {}
-            if in_range(i + 1):
-                jobs.extend(flip_jobs(i + 1))
-            if in_range(i - 1):
-                before[len(jobs)] = lambda: tanh_tau2(i - 1)
-            if in_range(i - 2):
-                jobs.extend(tau2_jobs(i - 2))
-            if in_range(i - 1):
-                if len(jobs) in before:
-                    before[len(jobs)] = lambda: (tanh_tau2(i - 1), tanh_rate(i - 1, 2))
-                else:
-                    before[len(jobs)] = lambda: tanh_rate(i - 1, 2)
-            if in_range(i - 2):
-                jobs.extend(h2_jobs(i - 2))
-            run_jobs(jobs, before)
-            if len(jobs) in before:
-                before[len(jobs)]()
+            run_jobs([
+                (None, flip_jobs(i + 1) if in_range(i + 1) else []),
+                (
+                    (lambda: tanh_tau2(i - 1, rate_of[i - 1])) if in_range(i - 1) else None,
+                    tau2_jobs(i - 2) if in_range(i - 2) else [],
+                ),
+                (
+                    (lambda: tanh_rate_2(i - 1, rate_of[i - 1])) if in_range(i - 1) else None,
+                    h2_jobs(i - 2, gain_diagonal) if in_range(i - 2) else [],
+                ),
+            ])
             subtract_h0(i)
             times_rate(i)
             make_h1(i)
@@ -466,23 +415,44 @@ def tile_liquidcell_pb_t_kernel(
             round_h1(i)
             quantise_h1(i)
 
-        hold_gpsimd(LAST)
+        def scale_rate(c, on_scalar):
+            rate = rate_of[c]
+            for m in range(PACK):
+                if on_scalar:
+                    nc.scalar.activation(
+                        out=rate[:, m, :], in_=rate[:, m, :], func=ACT.Identity,
+                        bias=minus_two_gain[:, m : m + 1], scale=gain[:, m : m + 1],
+                    )
+                else:
+                    nc.vector.tensor_scalar(
+                        out=rate[:, m, :], in0=rate[:, m, :],
+                        scalar1=gain[:, m : m + 1], scalar2=minus_two_gain[:, m : m + 1], op0=ALU.mult, op1=ALU.add,
+                    )
+
+        def times_scaled_rate(c):
+            rate, move = rate_of[c], move_of[c]
+            for w in TILE_PAIRS:
+                nc.vector.tensor_tensor(out=move[:, w, :], in0=rate[:, w, :], in1=move[:, w, :], op=ALU.mult)
+
+        hold_gpsimd_until_h1_is_quantised(LAST)
         subtract_h1(LAST - 1, nc.gpsimd)
-        finish_tau2_on_scalar(LAST - 1, range(PACK))
-        scale_rate_on_scalar(LAST - 1)
+        finish_tau2_on_scalar(LAST - 1)
+        scale_rate(LAST - 1, on_scalar=True)
         products_and_sums(LAST, 2)
         times_scaled_rate(LAST - 1)
         tanh_move(LAST)
-        logits_of_last = rate_of[LAST]
-        rate_of[LAST] = tanh_rate_into_new_tile(LAST)
+        last_logits = rate_of[LAST]
+        last_rate = step2.tile([P, PACK, CHUNK], F32, tag="rate")
+        tanh_rate_2(LAST, last_rate)
+        rate_of[LAST] = last_rate
         subtract_h1(LAST, nc.vector)
-        scale_rate(LAST, nc.vector)
+        scale_rate(LAST, on_scalar=False)
         times_scaled_rate(LAST)
-        run_jobs(
-            tau2_jobs(LAST - 1) + h2_jobs(LAST - 1, scaled=True) + h2_jobs(LAST, scaled=True)
-            + tau2_jobs(LAST, on_vector=True),
-            {
-                BLOCKS: lambda: tanh_tau2(LAST, logits_of_last),
-                3 * BLOCKS - N_TURN_BANKS: lambda: finish_tau2(LAST, nc.vector, range(PACK)),
-            },
-        )
+        jobs_before_last_tau2 = h2_jobs(LAST - 1, None) + h2_jobs(LAST, None)
+        cut = len(jobs_before_last_tau2) - N_TURN_BANKS
+        run_jobs([
+            (None, tau2_jobs(LAST - 1)),
+            (lambda: tanh_tau2(LAST, last_logits), jobs_before_last_tau2[:cut]),
+            (lambda: finish_tau2(LAST, nc.vector), jobs_before_last_tau2[cut:]),
+            (None, tau2_jobs(LAST, on_vector=True)),
+        ])

@@ -25,8 +25,8 @@ N_CHUNKS = B // CHUNK
 LAST = N_CHUNKS - 1
 HALF_LN_3 = 0.5 * math.log(3.0)
 TILE_PAIRS = (slice(0, 2), slice(2, 4))
-N_PRODUCT_BANKS = 3
-N_TURN_BANKS = 5
+N_PRODUCT_BANKS = 4
+N_TURN_BANKS = 4
 
 FLOPS = 4 * 2 * B * H * H
 
@@ -36,15 +36,6 @@ def load_rows(nc, rows, dram_rows):
     return rows
 
 
-def flip_half(nc, banks, rows, half, ident_f32):
-    flipped = banks.tile([P, PAIR, HALF], F32, tag="turned")
-    for jj in range(HALF // P):
-        words = rows[:, half * (HALF // P) + jj, :].bitcast(F32).rearrange("p (w u) -> p u w", u=PAIR)
-        for u in range(PAIR):
-            nc.tensor.transpose(flipped[:, u, jj * P : (jj + 1) * P], words[:, u, :], ident_f32[:])
-    return flipped
-
-
 def quantise(nc, pool, grouped, tag):
     codes = pool.tile([P, CHUNK], U32, tag=tag + "_codes", align_bytes=64)
     scales = pool.tile([P, CHUNK], U8, tag=tag + "_scales", align_bytes=64)
@@ -52,18 +43,14 @@ def quantise(nc, pool, grouped, tag):
     return codes, scales
 
 
-def weight_times_state(nc, banks, weight, m, state):
-    w_codes, w_scales = weight
-    s_codes, s_scales = state
+def multiply(nc, banks, stationary, block, moving):
+    s_codes, s_scales = stationary
+    m_codes, m_scales = moving
     product = banks.tile([P, CHUNK], F32, tag="product")
+    cols = slice(block * P, (block + 1) * P)
     nc.tensor.matmul_mx(
-        out=product[:],
-        lhsT=w_codes[:, m * P : (m + 1) * P].bitcast(FP8X4),
-        lhsT_scale=w_scales[:, m * P : (m + 1) * P],
-        rhs=s_codes[:].bitcast(FP8X4),
-        rhs_scale=s_scales[:],
-        start=True,
-        stop=True,
+        out=product[:], lhsT=s_codes[:, cols].bitcast(FP8X4), lhsT_scale=s_scales[:, cols],
+        rhs=m_codes[:].bitcast(FP8X4), rhs_scale=m_scales[:], start=True, stop=True,
     )
     return product
 
@@ -75,73 +62,29 @@ def tile_liquidcell_pb_t_kernel(
     with ExitStack() as ctx:
         ctx.enter_context(tc.manual_schedule())
         const = ctx.enter_context(tc.tile_pool(name="const", bufs=1))
-        loads = ctx.enter_context(tc.tile_pool(name="loads", bufs=6))
-        flips = ctx.enter_context(tc.tile_pool(name="flips", bufs=2))
-        plains = ctx.enter_context(tc.tile_pool(name="plains", bufs=3))
+        loads = ctx.enter_context(tc.tile_pool(name="loads", bufs=2))
+        ic_loads = ctx.enter_context(tc.tile_pool(name="ic_loads", bufs=4))
+        flips = ctx.enter_context(tc.tile_pool(name="flips", bufs=3))
+        plains = ctx.enter_context(tc.tile_pool(name="plains", bufs=4))
+        grouped_h1 = ctx.enter_context(tc.tile_pool(name="grouped_h1", bufs=2))
         mx = ctx.enter_context(tc.tile_pool(name="mx", bufs=2))
-        step1 = ctx.enter_context(tc.tile_pool(name="step1", bufs=1))
-        step2 = ctx.enter_context(tc.tile_pool(name="step2", bufs=3))
+        work = ctx.enter_context(tc.tile_pool(name="work", bufs=1))
+        step2 = ctx.enter_context(tc.tile_pool(name="step2", bufs=2))
+        pairs = ctx.enter_context(tc.tile_pool(name="pairs", bufs=2))
+        rates = ctx.enter_context(tc.tile_pool(name="rates", bufs=3))
         states = ctx.enter_context(tc.tile_pool(name="states", bufs=3))
-        stores = ctx.enter_context(tc.tile_pool(name="stores", bufs=2 * BLOCKS))
+        stores = ctx.enter_context(tc.tile_pool(name="stores", bufs=3 * BLOCKS))
         products = ctx.enter_context(tc.psum_pool(name="products", bufs=N_PRODUCT_BANKS))
         turns = ctx.enter_context(tc.psum_pool(name="turns", bufs=N_TURN_BANKS))
 
         ident_f32 = const.tile([P, P], F32)
         make_identity(nc, ident_f32[:])
+        ident_bf16 = const.tile([P, P], BF16)
+        make_identity(nc, ident_bf16[:])
 
-        def new_rows():
-            rows = loads.tile([P, BLOCKS, H], BF16, tag="rows")
-            return rows
-
-        adapt_b_bf16 = const.tile([P, PACK], BF16)
-        nc.sync.dma_start(out=adapt_b_bf16[:], in_=tau_adapt_b.rearrange("(p m) -> p m", m=PACK))
-        base_bf16 = const.tile([P, PACK], BF16)
-        nc.sync.dma_start(out=base_bf16[:], in_=tau_base.rearrange("(p m) -> p m", m=PACK))
-
-        first_h_rows = load_rows(nc, new_rows(), h[0:CHUNK, :])
-        rec_weight_rows = const.tile([P, BLOCKS, H], BF16)
-        load_rows(nc, rec_weight_rows, W_rec)
-        first_ic_rows = load_rows(nc, new_rows(), input_contrib[0:CHUNK, :])
-        tau_weight_rows = const.tile([P, BLOCKS, H], BF16)
-        load_rows(nc, tau_weight_rows, tau_w_h)
-        first_x_rows = load_rows(nc, new_rows(), x_tau[0:CHUNK, :])
-
-        adapt_b = const.tile([P, PACK], F32)
-        nc.vector.tensor_copy(out=adapt_b[:], in_=adapt_b_bf16[:])
-        bias_rate = const.tile([P, PACK], F32)
-        nc.vector.tensor_scalar(
-            out=bias_rate[:], in0=adapt_b_bf16[:], scalar1=0.5, scalar2=HALF_LN_3, op0=ALU.mult, op1=ALU.add
-        )
-        base = const.tile([P, PACK], F32)
-        nc.vector.tensor_copy(out=base[:], in_=base_bf16[:])
-        half_base = const.tile([P, PACK], F32)
-        nc.vector.tensor_scalar(out=half_base[:], in0=base_bf16[:], scalar1=0.5, scalar2=None, op0=ALU.mult)
-        inverse_base = const.tile([P, PACK], F32)
-        nc.vector.reciprocal(out=inverse_base[:], in_=base[:])
-        gain = const.tile([P, PACK], F32)
-        nc.vector.tensor_scalar(
-            out=gain[:], in0=inverse_base[:], scalar1=-2.0 * DT / 3.0, scalar2=None, op0=ALU.mult
-        )
-        gain_diagonal = const.tile([P, PACK, P], F32)
-        for m in range(PACK):
-            nc.vector.tensor_scalar(
-                out=gain_diagonal[:, m, :], in0=ident_f32[:], scalar1=gain[:, m : m + 1], scalar2=None, op0=ALU.mult
-            )
-        minus_two_gain = const.tile([P, PACK], F32)
-        nc.vector.tensor_scalar(out=minus_two_gain[:], in0=gain[:], scalar1=-2.0, scalar2=None, op0=ALU.mult)
-
-        rows_of = {}
-        weight_of = {}
-        h0_of = {}
-        ic_of = {}
-        x_of = {}
-        h0_codes_of = {}
-        h1_codes_of = {}
-        rate_of = {}
-        move_of = {}
-        h1_of = {}
-        h1_grouped_of = {}
-        tau2_of = {}
+        h_rows_of = {}
+        ic_rows_of = {}
+        x_rows_of = {}
 
         def chunk_rows(c):
             return slice(c * CHUNK, (c + 1) * CHUNK)
@@ -149,310 +92,489 @@ def tile_liquidcell_pb_t_kernel(
         def in_range(c):
             return 0 <= c < N_CHUNKS
 
-        def load(c):
-            rows_of[c] = (
-                load_rows(nc, new_rows(), h[chunk_rows(c), :]),
-                load_rows(nc, new_rows(), input_contrib[chunk_rows(c), :]),
-                load_rows(nc, new_rows(), x_tau[chunk_rows(c), :]),
+        def load_h(c):
+            h_rows = loads.tile([P, BLOCKS, H], BF16, tag="h_rows")
+            h_rows_of[c] = load_rows(nc, h_rows, h[chunk_rows(c), :])
+
+        def load_ic(c):
+            ic_rows = ic_loads.tile([P, BLOCKS, H], BF16, tag="ic_rows")
+            ic_rows_of[c] = load_rows(nc, ic_rows, input_contrib[chunk_rows(c), :])
+
+        def load_x(c):
+            x_rows = loads.tile([P, BLOCKS, H], BF16, tag="x_rows")
+            x_rows_of[c] = load_rows(nc, x_rows, x_tau[chunk_rows(c), :])
+
+        load_h(0)
+        rec_weight_rows = const.tile([P, BLOCKS, H], BF16)
+        load_rows(nc, rec_weight_rows, W_rec)
+        load_ic(0)
+        tau_weight_rows = const.tile([P, BLOCKS, H], BF16)
+        load_rows(nc, tau_weight_rows, tau_w_h)
+        adapt_b_bf16 = const.tile([P, PACK], BF16)
+        nc.sync.dma_start(out=adapt_b_bf16[:], in_=tau_adapt_b.rearrange("(p m) -> p m", m=PACK))
+        base_bf16 = const.tile([P, PACK], BF16)
+        nc.sync.dma_start(out=base_bf16[:], in_=tau_base.rearrange("(p m) -> p m", m=PACK))
+        load_x(0)
+        load_h(1)
+        load_x(1)
+        load_ic(1)
+
+        adapt_b = const.tile([P, PACK], F32)
+        bias_rate = const.tile([P, PACK], F32)
+        base = const.tile([P, PACK], F32)
+        half_base = const.tile([P, PACK], F32)
+        inverse_base = const.tile([P, PACK], F32)
+        gain = const.tile([P, PACK], F32)
+        minus_gain = const.tile([P, PACK], F32)
+        minus_two_gain = const.tile([P, PACK], F32)
+
+        def make_vectors():
+            nc.vector.tensor_copy(out=adapt_b[:], in_=adapt_b_bf16[:])
+            nc.vector.tensor_scalar(
+                out=bias_rate[:], in0=adapt_b_bf16[:], scalar1=0.5, scalar2=HALF_LN_3, op0=ALU.mult, op1=ALU.add
+            )
+            nc.vector.tensor_copy(out=base[:], in_=base_bf16[:])
+            nc.vector.tensor_scalar(out=half_base[:], in0=base_bf16[:], scalar1=0.5, scalar2=None, op0=ALU.mult)
+            nc.vector.reciprocal(out=inverse_base[:], in_=base[:])
+            nc.vector.tensor_scalar(
+                out=gain[:], in0=inverse_base[:], scalar1=-2.0 * DT / 3.0, scalar2=None, op0=ALU.mult
+            )
+            nc.vector.tensor_scalar(
+                out=minus_gain[:], in0=inverse_base[:], scalar1=2.0 * DT / 3.0, scalar2=None, op0=ALU.mult
+            )
+            nc.vector.tensor_scalar(
+                out=minus_two_gain[:], in0=inverse_base[:], scalar1=4.0 * DT / 3.0, scalar2=None, op0=ALU.mult
             )
 
-        filled_bank = {}
+        h0_of = {}
+        x_of = {}
+        weight_of = {}
+        h0_codes_of = {}
+        h1_codes_of = {}
+        z1_of = {}
+        r1_of = {}
+        z2_of = {}
+        rate_of = {}
+        move_of = {}
+        tau2_of = {}
+        h1_of = {}
+        h1_grouped_of = {}
+        bank_of = {}
 
-        def copy_grouped(key, grouped, half):
-            grouped_words = grouped[:].bitcast(F32).rearrange("p (c u) -> p c u", u=PAIR)
-            nc.scalar.copy(
-                out=grouped_words[:, half * HALF : (half + 1) * HALF, :],
-                in_=filled_bank[key][:].rearrange("p u c -> p c u"),
-            )
-
-        def copy_plain(key, plain, half):
-            plain_words = plain[:].bitcast(F32).rearrange("p (u c) -> p u c", u=PAIR)
-            nc.scalar.copy(out=plain_words[:, :, half * HALF : (half + 1) * HALF], in_=filled_bank[key][:])
-
-        def fill_flipped(key, rows, half):
-            filled_bank[key] = flip_half(nc, turns, rows, half, ident_f32)
-
-        def grouped_jobs(name, rows, grouped):
-            return [
-                (
-                    lambda half=half: fill_flipped((name, half), rows, half),
-                    lambda half=half: copy_grouped((name, half), grouped, half),
-                )
-                for half in range(2)
-            ]
-
-        def plain_jobs(name, rows, plain):
-            return [
-                (
-                    lambda half=half: fill_flipped((name, half), rows, half),
-                    lambda half=half: copy_plain((name, half), plain, half),
-                )
-                for half in range(2)
-            ]
-
-        def flip_jobs(c):
-            h_rows, ic_rows, x_rows = rows_of[c]
-            h0 = flips.tile([P, CHUNK * PACK], BF16, tag="grouped", align_bytes=64)
-            ic_plain = plains.tile([P, PACK * CHUNK], BF16, tag="ic")
-            x_plain = plains.tile([P, PACK * CHUNK], BF16, tag="x")
-            h0_of[c] = h0
-            ic_of[c] = ic_plain[:].rearrange("p (u c e) -> p u c e", u=PAIR, e=PAIR)
-            x_of[c] = x_plain[:].rearrange("p (u c e) -> p u c e", u=PAIR, e=PAIR)
-            return (
-                grouped_jobs((c, "h"), h_rows, h0) + plain_jobs((c, "ic"), ic_rows, ic_plain)
-                + plain_jobs((c, "x"), x_rows, x_plain)
-            )
-
-        def fill_rows(key, terms, j):
-            back = turns.tile([P, PACK, P], F32, tag="turned")
-            filled_bank[key] = back
-            for m in range(PACK):
-                for n, (term, factors) in enumerate(terms):
-                    nc.tensor.matmul(
-                        out=back[:, m, :],
-                        lhsT=term[:, m, j * P : (j + 1) * P],
-                        rhs=ident_f32[:] if factors is None else factors[:, m, :],
-                        is_transpose=factors is None,
-                        start=(n == 0),
-                        stop=(n == len(terms) - 1),
-                    )
-
-        def copy_and_store_rows(key, dram_rows, j, on_vector):
-            rows = stores.tile([P, H], F32, tag="out_rows")
-            out_view = rows[:].rearrange("r (p m) -> r p m", m=PACK)
-            in_view = filled_bank[key][:].rearrange("r m p -> r p m")
-            if on_vector:
-                nc.vector.tensor_copy(out=out_view, in_=in_view)
+        def fill_flipped(key, rows, half, in_product_bank=False):
+            if in_product_bank:
+                flipped = products.tile([P, PAIR, HALF], F32, tag="product")
             else:
-                nc.scalar.copy(out=out_view, in_=in_view)
-            nc.sync.dma_start(out=dram_rows.rearrange("(p j) f -> p j f", j=BLOCKS)[:, j, :], in_=rows[:])
+                flipped = turns.tile([P, PAIR, HALF], F32, tag="turned")
+            bank_of[key] = flipped
+            for jj in range(HALF // P):
+                words = rows[:, half * (HALF // P) + jj, :].bitcast(F32).rearrange("p (w u) -> p u w", u=PAIR)
+                for u in range(PAIR):
+                    nc.tensor.transpose(flipped[:, u, jj * P : (jj + 1) * P], words[:, u, :], ident_f32[:])
 
-        def tau2_jobs(c, on_vector=False):
-            return [
-                (
-                    lambda j=j: fill_rows((c, "tau2", j), [(tau2_of[c], None)], j),
-                    lambda j=j: copy_and_store_rows((c, "tau2", j), out_1[chunk_rows(c), :], j, on_vector),
-                )
-                for j in range(BLOCKS)
-            ]
+        def copy_with(on_vector, out, in_):
+            if on_vector:
+                nc.vector.tensor_copy(out=out, in_=in_)
+            else:
+                nc.scalar.copy(out=out, in_=in_)
 
-        def h2_jobs(c, factors):
-            return [
-                (
-                    lambda j=j: fill_rows((c, "h2", j), [(h1_of[c], None), (move_of[c], factors)], j),
-                    lambda j=j: copy_and_store_rows((c, "h2", j), out_0[chunk_rows(c), :], j, False),
-                )
-                for j in range(BLOCKS)
-            ]
+        def copy_grouped(key, grouped, half, on_vector):
+            words = grouped[:].bitcast(F32).rearrange("p (c u) -> p c u", u=PAIR)
+            copy_with(
+                on_vector, words[:, half * HALF : (half + 1) * HALF, :], bank_of[key][:].rearrange("p u c -> p c u")
+            )
 
-        def run_jobs(stages):
-            jobs = []
-            work_before = {}
-            for work, stage_jobs in stages:
-                if work is not None:
-                    work_before.setdefault(len(jobs), []).append(work)
-                jobs.extend(stage_jobs)
-            filled = 0
-            for k in range(len(jobs) + 1):
-                while filled < min(k + N_TURN_BANKS, len(jobs)):
-                    jobs[filled][0]()
-                    filled += 1
-                for work in work_before.get(k, []):
-                    work()
-                if k < len(jobs):
-                    jobs[k][1]()
+        def copy_plain(key, plain, half, on_vector):
+            words = plain[:].bitcast(F32).rearrange("p (u c) -> p u c", u=PAIR)
+            copy_with(on_vector, words[:, :, half * HALF : (half + 1) * HALF], bank_of[key][:])
 
-        def quantise_h0(c):
-            h0_codes_of[c] = quantise(nc, mx, h0_of[c], "h0")
+        def new_h0(c):
+            h0 = flips.tile([P, CHUNK * PACK], BF16, tag="grouped", align_bytes=64)
+            h0_of[c] = h0
 
-        def products_and_sums(c, step):
-            pool = step1 if step == 1 else step2
-            state = h0_codes_of[c] if step == 1 else h1_codes_of[c]
-            rate = pool.tile([P, PACK, CHUNK], F32, tag="rate")
-            move = pool.tile([P, PACK, CHUNK], F32, tag="move")
-            rate_of[c], move_of[c] = rate, move
-            for m in range(PACK):
-                drive = weight_times_state(nc, products, weight_of["rec"], m, state)
-                nc.vector.tensor_tensor(
-                    out=move[:, m, :], in0=drive[:], in1=ic_of[c][:, m // PAIR, :, m % PAIR], op=ALU.add
-                )
-            for m in range(PACK):
-                logits = weight_times_state(nc, products, weight_of["tau"], m, state)
+        def new_x(c):
+            x_plain = plains.tile([P, PACK * CHUNK], BF16, tag="x")
+            x_of[c] = x_plain
+
+        def h0_tile(c, m):
+            return h0_of[c][:].rearrange("p (c t) -> p t c", t=PACK)[:, m, :]
+
+        def x_tile(c, m):
+            return x_of[c][:].rearrange("p (u c e) -> p u c e", u=PAIR, e=PAIR)[:, m // PAIR, :, m % PAIR]
+
+        def product_z(step, c, j):
+            codes = h0_codes_of[c] if step == 1 else h1_codes_of[c]
+            return multiply(nc, products, codes, j, weight_of["rec"])
+
+        def product_l(step, c, m):
+            codes = h0_codes_of[c] if step == 1 else h1_codes_of[c]
+            return multiply(nc, products, weight_of["tau"], m, codes)
+
+        def add_z(step, c, j, product):
+            if j == 0:
+                z = work.tile([P, BLOCKS, H], F32, tag="z1" if step == 1 else "z2")
+                (z1_of if step == 1 else z2_of)[c] = z
+            z = (z1_of if step == 1 else z2_of)[c]
+            nc.vector.tensor_tensor(
+                out=z[:, j, :].rearrange("r (m p) -> r m p", m=PACK),
+                in0=product[:].rearrange("r (m p) -> r m p", m=PACK),
+                in1=ic_rows_of[c][:, j, :].rearrange("r (p m) -> r m p", m=PACK),
+                op=ALU.add,
+            )
+
+        def add_l(step, c, m, product):
+            if m == 0:
                 if step == 1:
-                    nc.vector.tensor_tensor(
-                        out=rate[:, m, :], in0=logits[:], in1=x_of[c][:, m // PAIR, :, m % PAIR], op=ALU.add
-                    )
+                    r1 = pairs.tile([P, PACK, CHUNK], F32, tag="r1")
+                    r1_of[c] = r1
                 else:
-                    nc.vector.scalar_tensor_tensor(
-                        out=rate[:, m, :], in0=logits[:], scalar=adapt_b[:, m : m + 1],
-                        in1=x_of[c][:, m // PAIR, :, m % PAIR], op0=ALU.add, op1=ALU.add,
-                    )
+                    rate = rates.tile([P, PACK, CHUNK], F32, tag="rate")
+                    rate_of[c] = rate
+            if step == 1:
+                nc.vector.tensor_tensor(out=r1_of[c][:, m, :], in0=product[:], in1=x_tile(c, m), op=ALU.add)
+            else:
+                nc.vector.scalar_tensor_tensor(
+                    out=rate_of[c][:, m, :], in0=product[:], scalar=adapt_b[:, m : m + 1], in1=x_tile(c, m),
+                    op0=ALU.add, op1=ALU.add,
+                )
 
-        def tanh_move(c):
-            nc.scalar.activation(out=move_of[c][:], in_=move_of[c][:], func=ACT.Tanh)
+        stream = []
+        for i in range(N_CHUNKS + 1):
+            for kind, step in (("l", 1), ("z", 1), ("z", 2), ("l", 2)) if i == 1 else (
+                ("l", 1), ("z", 2), ("z", 1), ("l", 2)
+            ):
+                c = i if step == 1 else i - 1
+                if in_range(c):
+                    stream.extend((kind, step, c, n) for n in range(PACK))
+        stream[0:PACK], stream[PACK : 2 * PACK] = stream[PACK : 2 * PACK], stream[0:PACK]
+        issued = []
 
-        def tanh_rate_1(c):
-            rate = rate_of[c]
+        def issue_until(limit):
+            while len(issued) < limit:
+                kind, step, c, n = stream[len(issued)]
+                issued.append(product_z(step, c, n) if kind == "z" else product_l(step, c, n))
+
+        drained = []
+
+        def drain(count, limit):
+            for n in range(count):
+                kind, step, c, n = stream[len(drained)]
+                product = issued[len(drained)]
+                drained.append(product)
+                if kind == "z":
+                    add_z(step, c, n, product)
+                else:
+                    add_l(step, c, n, product)
+                issue_until(min(len(drained) + N_PRODUCT_BANKS, limit))
+
+        def tanh_z1(c):
+            nc.scalar.activation(out=z1_of[c][:], in_=z1_of[c][:], func=ACT.Tanh, scale=-1.0)
+
+        def tanh_r1(c):
             for m in range(PACK):
                 nc.scalar.activation(
-                    out=rate[:, m, :], in_=rate[:, m, :], func=ACT.Tanh, bias=bias_rate[:, m : m + 1], scale=0.5
+                    out=r1_of[c][:, m, :], in_=r1_of[c][:, m, :], func=ACT.Tanh, bias=bias_rate[:, m : m + 1], scale=0.5
                 )
 
-        def tanh_rate_2(c, rate):
-            nc.scalar.activation(out=rate[:], in_=rate_of[c][:], func=ACT.Tanh, bias=HALF_LN_3, scale=0.5)
+        def fill_d1_with_h(c, m):
+            bank = turns.tile([P, CHUNK], F32, tag="turned")
+            bank_of["d1", c, m] = bank
+            nc.tensor.matmul(out=bank[:], lhsT=ident_bf16[:], rhs=h0_tile(c, m), start=True, stop=False)
 
-        def tanh_tau2(c, logits):
-            tau2 = step2.tile([P, PACK, CHUNK], F32, tag="tau2")
-            tau2_of[c] = tau2
-            nc.scalar.activation(out=tau2[:], in_=logits[:], func=ACT.Tanh, scale=0.5)
-
-        def subtract_h0(c):
-            move, h0 = move_of[c], h0_of[c][:].rearrange("p (c t) -> p t c", t=PACK)
-            for w in TILE_PAIRS:
-                nc.vector.tensor_tensor(out=move[:, w, :], in0=move[:, w, :], in1=h0[:, w, :], op=ALU.subtract)
-
-        def times_rate(c):
-            rate, move = rate_of[c], move_of[c]
-            for w in TILE_PAIRS:
-                nc.vector.scalar_tensor_tensor(
-                    out=move[:, w, :], in0=rate[:, w, :], scalar=2.0, in1=move[:, w, :],
-                    op0=ALU.subtract, op1=ALU.mult,
+        def add_minus_a1(c, m):
+            bank = bank_of["d1", c, m]
+            for j in range(BLOCKS):
+                nc.tensor.matmul(
+                    out=bank[:, j * P : (j + 1) * P], lhsT=z1_of[c][:, j, m * P : (m + 1) * P], rhs=ident_f32[:],
+                    is_transpose=True, start=False, stop=(j == BLOCKS - 1),
                 )
+
+        def start_d1(c):
+            for m in range(PACK):
+                fill_d1_with_h(c, m)
+
+        def finish_d1(c):
+            for m in range(PACK):
+                add_minus_a1(c, m)
+
+        def make_q1(c, m):
+            r1 = r1_of[c]
+            nc.vector.scalar_tensor_tensor(
+                out=r1[:, m, :], in0=r1[:, m, :], scalar=2.0, in1=bank_of["d1", c, m][:],
+                op0=ALU.subtract, op1=ALU.mult,
+            )
 
         def make_h1(c):
-            move, h0 = move_of[c], h0_of[c][:].rearrange("p (c t) -> p t c", t=PACK)
             h1 = states.tile([P, PACK, CHUNK], F32, tag="h1")
             h1_of[c] = h1
             for m in range(PACK):
                 nc.vector.scalar_tensor_tensor(
-                    out=h1[:, m, :], in0=move[:, m, :], scalar=gain[:, m : m + 1], in1=h0[:, m, :],
+                    out=h1[:, m, :], in0=r1_of[c][:, m, :], scalar=minus_gain[:, m : m + 1], in1=h0_tile(c, m),
                     op0=ALU.mult, op1=ALU.add,
                 )
 
         def round_h1(c):
-            h1_grouped = flips.tile([P, CHUNK * PACK], BF16, tag="h1_grouped", align_bytes=64)
+            h1_grouped = grouped_h1.tile([P, CHUNK * PACK], BF16, tag="h1_grouped", align_bytes=64)
             h1_grouped_of[c] = h1_grouped
             nc.vector.tensor_copy(
                 out=h1_grouped[:].rearrange("p (c t) -> p c t", t=PACK), in_=h1_of[c][:].rearrange("p t c -> p c t")
             )
 
-        def quantise_h1(c):
-            h1_codes_of[c] = quantise(nc, mx, h1_grouped_of[c], "h1")
+        def fill_z2(c, m):
+            bank = turns.tile([P, CHUNK], F32, tag="turned")
+            bank_of["z2", c, m] = bank
+            for j in range(BLOCKS):
+                nc.tensor.transpose(bank[:, j * P : (j + 1) * P], z2_of[c][:, j, m * P : (m + 1) * P], ident_f32[:])
 
-        def subtract_h1(c, engine):
+        def tanh_a2(c):
+            move = step2.tile([P, PACK, CHUNK], F32, tag="move")
+            move_of[c] = move
+            for m in range(PACK):
+                nc.scalar.activation(out=move[:, m, :], in_=bank_of["z2", c, m][:], func=ACT.Tanh)
+
+        def tanh_tau2(c):
+            tau2 = step2.tile([P, PACK, CHUNK], F32, tag="tau2")
+            tau2_of[c] = tau2
+            nc.scalar.activation(out=tau2[:], in_=rate_of[c][:], func=ACT.Tanh, scale=0.5)
+
+        def tanh_r2(c, rate):
+            nc.scalar.activation(out=rate[:], in_=rate_of[c][:], func=ACT.Tanh, bias=HALF_LN_3, scale=0.5)
+            rate_of[c] = rate
+
+        def make_d2(c, engine):
             move = move_of[c]
             for w in TILE_PAIRS:
                 engine.tensor_tensor(out=move[:, w, :], in0=move[:, w, :], in1=h1_of[c][:, w, :], op=ALU.subtract)
 
-        def finish_tau2(c, engine):
-            tau2 = tau2_of[c]
+        def affine(engine, tile, scale, bias):
             for m in range(PACK):
-                engine.tensor_scalar(
-                    out=tau2[:, m, :], in0=tau2[:, m, :],
-                    scalar1=half_base[:, m : m + 1], scalar2=base[:, m : m + 1], op0=ALU.mult, op1=ALU.add,
-                )
+                if engine is None:
+                    nc.scalar.activation(
+                        out=tile[:, m, :], in_=tile[:, m, :], func=ACT.Identity,
+                        bias=bias[:, m : m + 1], scale=scale[:, m : m + 1],
+                    )
+                else:
+                    engine.tensor_scalar(
+                        out=tile[:, m, :], in0=tile[:, m, :], scalar1=scale[:, m : m + 1], scalar2=bias[:, m : m + 1],
+                        op0=ALU.mult, op1=ALU.add,
+                    )
 
-        def finish_tau2_on_scalar(c):
-            tau2 = tau2_of[c]
+        def scale_rate(c, engine):
+            affine(engine, rate_of[c], gain, minus_two_gain)
+
+        def finish_tau2(c, engine):
+            affine(engine, tau2_of[c], half_base, base)
+
+        def make_q2(c, w):
+            move = move_of[c]
+            nc.vector.tensor_tensor(out=move[:, w, :], in0=rate_of[c][:, w, :], in1=move[:, w, :], op=ALU.mult)
+
+        def fill_rows(key, terms, j, in_product_bank):
+            if in_product_bank:
+                back = products.tile([P, PACK, P], F32, tag="product")
+            else:
+                back = turns.tile([P, PACK, P], F32, tag="turned")
+            bank_of[key] = back
             for m in range(PACK):
-                nc.scalar.activation(
-                    out=tau2[:, m, :], in_=tau2[:, m, :], func=ACT.Identity,
-                    bias=base[:, m : m + 1], scale=half_base[:, m : m + 1],
-                )
+                for n, term in enumerate(terms):
+                    nc.tensor.matmul(
+                        out=back[:, m, :], lhsT=term[:, m, j * P : (j + 1) * P], rhs=ident_f32[:], is_transpose=True,
+                        start=(n == 0), stop=(n == len(terms) - 1),
+                    )
+
+        def fill_tau2(c, j, in_product_bank=False):
+            fill_rows(("tau2", c, j), [tau2_of[c]], j, in_product_bank)
+
+        def fill_h2(c, j, in_product_bank=False):
+            fill_rows(("h2", c, j), [h1_of[c], move_of[c]], j, in_product_bank)
+
+        def copy_and_store(kind, c, j, on_vector):
+            out_rows = stores.tile([P, H], F32, tag="out_rows")
+            out_view = out_rows[:].rearrange("r (p m) -> r p m", m=PACK)
+            copy_with(on_vector, out_view, bank_of[kind, c, j][:].rearrange("r m p -> r p m"))
+            dram_rows = (out_0 if kind == "h2" else out_1)[chunk_rows(c), :]
+            nc.sync.dma_start(out=dram_rows.rearrange("(p j) f -> p j f", j=BLOCKS)[:, j, :], in_=out_rows[:])
 
         gate_word = const.tile([P, 1], U32)
 
         def hold_gpsimd_until_h1_is_quantised(c):
             nc.gpsimd.tensor_copy(out=gate_word[:], in_=h1_codes_of[c][0][:, 0:1])
 
-        rows_of[0] = (first_h_rows, first_ic_rows, first_x_rows)
-        load(1)
-        rec_grouped = flips.tile([P, CHUNK * PACK], BF16, tag="h1_grouped", align_bytes=64)
-        tau_grouped = flips.tile([P, CHUNK * PACK], BF16, tag="h1_grouped", align_bytes=64)
-        first_jobs = flip_jobs(0)
-        run_jobs([
-            (None, first_jobs[0:2]),
-            (None, grouped_jobs("rec", rec_weight_rows, rec_grouped)),
-            (None, first_jobs[2:4]),
-            (None, grouped_jobs("tau", tau_weight_rows, tau_grouped)),
-            (None, first_jobs[4:6]),
-        ])
+        rec_grouped = grouped_h1.tile([P, CHUNK * PACK], BF16, tag="h1_grouped", align_bytes=64)
+        tau_grouped = grouped_h1.tile([P, CHUNK * PACK], BF16, tag="h1_grouped", align_bytes=64)
+        new_h0(0)
+        new_x(0)
+
+        def fill_at_start(name, rows):
+            for half in range(2):
+                fill_flipped((name, half), rows, half)
+
+        def copy_at_start(name, copy, target):
+            copy((name, 0), target, 0, False)
+            copy((name, 1), target, 1, True)
+
+        def fill_flips(c):
+            for name, rows in (("h", h_rows_of[c]), ("x", x_rows_of[c])):
+                for half in range(2):
+                    fill_flipped(((name, c), half), rows, half, True)
+
+        def copy_flips(c):
+            new_h0(c)
+            new_x(c)
+            for half in range(2):
+                copy_grouped((("h", c), half), h0_of[c], half, False)
+            for half in range(2):
+                copy_plain((("x", c), half), x_of[c], half, False)
+
+        def quantise_h0(c):
+            h0_codes_of[c] = quantise(nc, mx, h0_of[c], "h0")
+
+        fill_at_start("h0", h_rows_of[0])
+        fill_at_start("rec", rec_weight_rows)
+        copy_at_start("h0", copy_grouped, h0_of[0])
         quantise_h0(0)
+        copy_at_start("rec", copy_grouped, rec_grouped)
         weight_of["rec"] = quantise(nc, const, rec_grouped, "rec_weight")
+        issue_until(PACK)
+        fill_at_start("tau", tau_weight_rows)
+        fill_at_start("x0", x_rows_of[0])
+        drain(PACK, PACK)
+        copy_at_start("tau", copy_grouped, tau_grouped)
         weight_of["tau"] = quantise(nc, const, tau_grouped, "tau_weight")
+        copy_at_start("x0", copy_plain, x_of[0])
+        make_vectors()
 
+        end_of_round = 0
         for i in range(N_CHUNKS):
-            if in_range(i + 2):
-                load(i + 2)
-            if in_range(i - 2):
+            after, before, done = in_range(i + 1), in_range(i - 1), in_range(i - 2)
+            end_of_round += 4 * PACK if before else 2 * PACK
+            limit = end_of_round
+            if done:
                 hold_gpsimd_until_h1_is_quantised(i - 1)
-                subtract_h1(i - 2, nc.gpsimd)
+                make_d2(i - 2, nc.gpsimd)
+                scale_rate(i - 2, nc.gpsimd)
                 finish_tau2(i - 2, nc.gpsimd)
-            products_and_sums(i, 1)
-            tanh_move(i)
-            tanh_rate_1(i)
-            if in_range(i - 1):
-                products_and_sums(i - 1, 2)
-                tanh_move(i - 1)
-            if in_range(i - 2):
-                times_rate(i - 2)
-            run_jobs([
-                (None, flip_jobs(i + 1) if in_range(i + 1) else []),
-                (
-                    (lambda: tanh_tau2(i - 1, rate_of[i - 1])) if in_range(i - 1) else None,
-                    tau2_jobs(i - 2) if in_range(i - 2) else [],
-                ),
-                (
-                    (lambda: tanh_rate_2(i - 1, rate_of[i - 1])) if in_range(i - 1) else None,
-                    h2_jobs(i - 2, gain_diagonal) if in_range(i - 2) else [],
-                ),
-            ])
-            subtract_h0(i)
-            times_rate(i)
-            make_h1(i)
-            if in_range(i + 1):
+            if i == 0:
+                load_h(2)
+                load_x(2)
+            if in_range(i + 2):
+                load_ic(i + 2)
+            if i == 1:
+                drain(end_of_round - 3 * PACK - len(drained), limit)
+                tanh_r1(i)
+                drain(PACK, limit)
+                tanh_z1(i)
+                start_d1(i)
+                drain(2 * PACK, limit)
+                tanh_tau2(i - 1)
+                finish_d1(i)
+            elif before:
+                drain(end_of_round - 3 * PACK - len(drained), limit)
+                tanh_r1(i)
+                drain(PACK, limit)
+                fill_z2(i - 1, 0)
+                fill_z2(i - 1, 1)
+                drain(2, limit)
+                fill_z2(i - 1, 2)
+                fill_z2(i - 1, 3)
+                tanh_a2(i - 1)
+                drain(2, limit)
+                tanh_z1(i)
+                start_d1(i)
+                drain(PACK, limit)
+                tanh_tau2(i - 1)
+                if in_range(i + 2):
+                    fill_flips(i + 2)
+                    copy_flips(i + 2)
+                finish_d1(i)
+            else:
+                tanh_z1(i)
+                issue_until(limit)
+                start_d1(i)
+                drain(PACK, limit)
+                tanh_r1(i)
+                finish_d1(i)
+            if done:
+                for w in TILE_PAIRS:
+                    make_q2(i - 2, w)
+            if done and after:
                 quantise_h0(i + 1)
-            round_h1(i)
-            quantise_h1(i)
-
-        def scale_rate(c, on_scalar):
-            rate = rate_of[c]
             for m in range(PACK):
-                if on_scalar:
-                    nc.scalar.activation(
-                        out=rate[:, m, :], in_=rate[:, m, :], func=ACT.Identity,
-                        bias=minus_two_gain[:, m : m + 1], scale=gain[:, m : m + 1],
-                    )
-                else:
-                    nc.vector.tensor_scalar(
-                        out=rate[:, m, :], in0=rate[:, m, :],
-                        scalar1=gain[:, m : m + 1], scalar2=minus_two_gain[:, m : m + 1], op0=ALU.mult, op1=ALU.add,
-                    )
+                make_q1(i, m)
+            if done:
+                for j in range(BLOCKS):
+                    fill_tau2(i - 2, j)
+            if done and after:
+                issue_until(limit + PACK)
+            if done:
+                for j in range(BLOCKS):
+                    copy_and_store("tau2", i - 2, j, False)
+                    fill_h2(i - 2, j)
+                for j in range(BLOCKS):
+                    copy_and_store("h2", i - 2, j, False)
+            if i == 0:
+                for c in (1, 2):
+                    fill_flips(c)
+                    copy_flips(c)
+            make_h1(i)
+            if i == 1:
+                for m in range(PACK):
+                    fill_z2(0, m)
+                tanh_a2(0)
+                fill_flips(3)
+                copy_flips(3)
+            if not done:
+                quantise_h0(i + 1)
+                issue_until(limit + PACK)
+            elif after:
+                drain(1, limit + PACK)
+            round_h1(i)
+            if after:
+                drain(1, limit + PACK)
+            if in_range(i + 3):
+                load_h(i + 3)
+                load_x(i + 3)
+            h1_codes_of[i] = quantise(nc, mx, h1_grouped_of[i], "h1")
+            if not after:
+                finish_tau2(LAST - 1, nc.vector)
+            if before:
+                tanh_r2(i - 1, rate_of[i - 1])
+            issue_until(len(drained) + N_PRODUCT_BANKS)
 
-        def times_scaled_rate(c):
-            rate, move = rate_of[c], move_of[c]
-            for w in TILE_PAIRS:
-                nc.vector.tensor_tensor(out=move[:, w, :], in0=rate[:, w, :], in1=move[:, w, :], op=ALU.mult)
-
+        limit = len(stream)
         hold_gpsimd_until_h1_is_quantised(LAST)
-        subtract_h1(LAST - 1, nc.gpsimd)
-        finish_tau2_on_scalar(LAST - 1)
-        scale_rate(LAST - 1, on_scalar=True)
-        products_and_sums(LAST, 2)
-        times_scaled_rate(LAST - 1)
-        tanh_move(LAST)
+        make_d2(LAST - 1, nc.gpsimd)
+        scale_rate(LAST - 1, None)
+        drain(PACK, limit)
+        for m in range(PACK):
+            fill_z2(LAST, m)
+        tanh_a2(LAST)
+        drain(PACK, limit)
+        for w in TILE_PAIRS:
+            make_q2(LAST - 1, w)
+        make_d2(LAST, nc.vector)
         last_logits = rate_of[LAST]
-        last_rate = step2.tile([P, PACK, CHUNK], F32, tag="rate")
-        tanh_rate_2(LAST, last_rate)
-        rate_of[LAST] = last_rate
-        subtract_h1(LAST, nc.vector)
-        scale_rate(LAST, on_scalar=False)
-        times_scaled_rate(LAST)
-        jobs_before_last_tau2 = h2_jobs(LAST - 1, None) + h2_jobs(LAST, None)
-        cut = len(jobs_before_last_tau2) - N_TURN_BANKS
-        run_jobs([
-            (None, tau2_jobs(LAST - 1)),
-            (lambda: tanh_tau2(LAST, last_logits), jobs_before_last_tau2[:cut]),
-            (lambda: finish_tau2(LAST, nc.vector), jobs_before_last_tau2[cut:]),
-            (None, tau2_jobs(LAST, on_vector=True)),
-        ])
+        last_tau2 = step2.tile([P, PACK, CHUNK], F32, tag="tau2")
+        tau2_of[LAST] = last_tau2
+        nc.scalar.activation(out=last_tau2[:], in_=last_logits[:], func=ACT.Tanh, scale=0.5)
+        tanh_r2(LAST, last_logits)
+        finish_tau2(LAST, nc.vector)
+        scale_rate(LAST, nc.vector)
+        for w in TILE_PAIRS:
+            make_q2(LAST, w)
+        jobs = []
+        for kind, c, fill, engines in (
+            ("tau2", LAST - 1, fill_tau2, (False, False, False, False)),
+            ("h2", LAST - 1, fill_h2, (False, False, False, False)),
+            ("tau2", LAST, fill_tau2, (False, True, False, True)),
+            ("h2", LAST, fill_h2, (False, True, False, True)),
+        ):
+            jobs.extend((kind, c, fill, engines[j], j) for j in range(BLOCKS))
+        ahead = N_PRODUCT_BANKS + N_TURN_BANKS
+        for n in range(len(jobs) + ahead):
+            if n >= ahead:
+                kind, c, fill, on_vector, j = jobs[n - ahead]
+                copy_and_store(kind, c, j, on_vector)
+            if n < len(jobs):
+                kind, c, fill, on_vector, j = jobs[n]
+                fill(c, j, n % 2 == 1)

@@ -400,6 +400,11 @@ def tile_liquidcell_pb_t_kernel(
         def hold_gpsimd_until_h1_is_quantised(c):
             nc.gpsimd.tensor_copy(out=gate_word[:], in_=h1_codes_of[c][0][:, 0:1])
 
+        gate_value = const.tile([P, 1], F32)
+
+        def hold_gpsimd_until_written(tile):
+            nc.gpsimd.tensor_copy(out=gate_value[:], in_=tile[:, PACK - 1, CHUNK - 1 : CHUNK])
+
         rec_grouped = grouped_h1.tile([P, CHUNK * PACK], BF16, tag="h1_grouped", align_bytes=64)
         tau_grouped = grouped_h1.tile([P, CHUNK * PACK], BF16, tag="h1_grouped", align_bytes=64)
         new_h0(0)
@@ -453,7 +458,6 @@ def tile_liquidcell_pb_t_kernel(
                 hold_gpsimd_until_h1_is_quantised(i - 1)
                 make_d2(i - 2, nc.gpsimd)
                 scale_rate(i - 2, nc.gpsimd)
-                finish_tau2(i - 2, nc.gpsimd)
             if i == 0:
                 load_h(2)
                 load_x(2)
@@ -494,24 +498,26 @@ def tile_liquidcell_pb_t_kernel(
                 drain(PACK, limit)
                 tanh_r1(i)
                 finish_d1(i)
+            if done and after:
+                quantise_h0(i + 1)
             if done:
                 for w in TILE_PAIRS:
                     make_q2(i - 2, w)
-            if done and after:
-                quantise_h0(i + 1)
+                hold_gpsimd_until_written(move_of[i - 2])
+                finish_tau2(i - 2, nc.gpsimd)
             for m in range(PACK):
                 make_q1(i, m)
             if done:
                 for j in range(BLOCKS):
-                    fill_tau2(i - 2, j)
+                    fill_h2(i - 2, j)
             if done and after:
                 issue_until(limit + PACK)
             if done:
                 for j in range(BLOCKS):
-                    copy_and_store("tau2", i - 2, j, False)
-                    fill_h2(i - 2, j)
-                for j in range(BLOCKS):
                     copy_and_store("h2", i - 2, j, False)
+                    fill_tau2(i - 2, j)
+                for j in range(BLOCKS):
+                    copy_and_store("tau2", i - 2, j, False)
             if i == 0:
                 for c in (1, 2):
                     fill_flips(c)
@@ -542,7 +548,7 @@ def tile_liquidcell_pb_t_kernel(
             issue_until(len(drained) + N_PRODUCT_BANKS)
 
         limit = len(stream)
-        hold_gpsimd_until_h1_is_quantised(LAST)
+        hold_gpsimd_until_written(tau2_of[LAST - 1])
         make_d2(LAST - 1, nc.gpsimd)
         scale_rate(LAST - 1, None)
         drain(PACK, limit)

@@ -346,8 +346,8 @@ def tile_liquidcell_pb_t_kernel(
             for w in TILE_PAIRS:
                 engine.tensor_tensor(out=move[:, w, :], in0=move[:, w, :], in1=h1_of[c][:, w, :], op=ALU.subtract)
 
-        def affine(engine, tile, scale, bias):
-            for m in range(PACK):
+        def affine(engine, tile, scale, bias, tiles=range(PACK)):
+            for m in tiles:
                 if engine is None:
                     nc.scalar.activation(
                         out=tile[:, m, :], in_=tile[:, m, :], func=ACT.Identity,
@@ -362,8 +362,8 @@ def tile_liquidcell_pb_t_kernel(
         def scale_rate(c, engine):
             affine(engine, rate_of[c], gain, minus_two_gain)
 
-        def finish_tau2(c, engine):
-            affine(engine, tau2_of[c], half_base, base)
+        def finish_tau2(c, engine, tiles=range(PACK)):
+            affine(engine, tau2_of[c], half_base, base, tiles)
 
         def make_q2(c, w):
             move = move_of[c]
@@ -418,10 +418,13 @@ def tile_liquidcell_pb_t_kernel(
             copy((name, 0), target, 0, False)
             copy((name, 1), target, 1, True)
 
-        def fill_flips(c):
-            for name, rows in (("h", h_rows_of[c]), ("x", x_rows_of[c])):
-                for half in range(2):
-                    fill_flipped(((name, c), half), rows, half, True)
+        def fill_h_flips(c):
+            for half in range(2):
+                fill_flipped((("h", c), half), h_rows_of[c], half, True)
+
+        def fill_x_flips(c):
+            for half in range(2):
+                fill_flipped((("x", c), half), x_rows_of[c], half, True)
 
         def copy_flips(c):
             new_h0(c)
@@ -458,6 +461,7 @@ def tile_liquidcell_pb_t_kernel(
                 hold_gpsimd_until_h1_is_quantised(i - 1)
                 make_d2(i - 2, nc.gpsimd)
                 scale_rate(i - 2, nc.gpsimd)
+                finish_tau2(i - 2, nc.gpsimd, range(1))
             if i == 0:
                 load_h(2)
                 load_x(2)
@@ -475,22 +479,27 @@ def tile_liquidcell_pb_t_kernel(
             elif before:
                 drain(end_of_round - 3 * PACK - len(drained), limit)
                 tanh_r1(i)
-                drain(PACK, limit)
+                drain(PACK - 1, limit)
+                drain(1, len(issued))
                 fill_z2(i - 1, 0)
                 fill_z2(i - 1, 1)
-                drain(2, limit)
+                drain(1, limit)
                 fill_z2(i - 1, 2)
                 fill_z2(i - 1, 3)
                 tanh_a2(i - 1)
-                drain(2, limit)
+                drain(PACK - 1, limit)
                 tanh_z1(i)
                 start_d1(i)
                 drain(PACK, limit)
                 tanh_tau2(i - 1)
+                if done:
+                    finish_tau2(i - 2, None, range(3, PACK))
                 if in_range(i + 2):
-                    fill_flips(i + 2)
-                    copy_flips(i + 2)
+                    fill_h_flips(i + 2)
                 finish_d1(i)
+                if in_range(i + 2):
+                    fill_x_flips(i + 2)
+                    copy_flips(i + 2)
             else:
                 tanh_z1(i)
                 issue_until(limit)
@@ -498,44 +507,42 @@ def tile_liquidcell_pb_t_kernel(
                 drain(PACK, limit)
                 tanh_r1(i)
                 finish_d1(i)
-            if done and after:
-                quantise_h0(i + 1)
             if done:
                 for w in TILE_PAIRS:
                     make_q2(i - 2, w)
                 hold_gpsimd_until_written(move_of[i - 2])
-                finish_tau2(i - 2, nc.gpsimd)
+                finish_tau2(i - 2, nc.gpsimd, range(1, 3))
             for m in range(PACK):
                 make_q1(i, m)
-            if done:
-                for j in range(BLOCKS):
-                    fill_h2(i - 2, j)
-            if done and after:
-                issue_until(limit + PACK)
-            if done:
-                for j in range(BLOCKS):
-                    copy_and_store("h2", i - 2, j, False)
-                    fill_tau2(i - 2, j)
-                for j in range(BLOCKS):
-                    copy_and_store("tau2", i - 2, j, False)
             if i == 0:
                 for c in (1, 2):
-                    fill_flips(c)
+                    fill_h_flips(c)
+                    fill_x_flips(c)
                     copy_flips(c)
             make_h1(i)
             if i == 1:
                 for m in range(PACK):
                     fill_z2(0, m)
                 tanh_a2(0)
-                fill_flips(3)
+                fill_h_flips(3)
+                fill_x_flips(3)
                 copy_flips(3)
-            if not done:
-                quantise_h0(i + 1)
-                issue_until(limit + PACK)
-            elif after:
-                drain(1, limit + PACK)
-            round_h1(i)
             if after:
+                quantise_h0(i + 1)
+            if done:
+                for j in range(BLOCKS):
+                    fill_h2(i - 2, j)
+            if done:
+                for j in range(BLOCKS):
+                    copy_and_store("h2", i - 2, j, False)
+                    fill_tau2(i - 2, j)
+            if after:
+                issue_until(limit + PACK)
+            if done:
+                for j in range(BLOCKS):
+                    copy_and_store("tau2", i - 2, j, False)
+            round_h1(i)
+            if i == 0:
                 drain(1, limit + PACK)
             if in_range(i + 3):
                 load_h(i + 3)

@@ -104,9 +104,18 @@ def tile_liquidcell_pb_t_kernel(
             x_rows = loads.tile([P, BLOCKS, H], BF16, tag="x_rows")
             x_rows_of[c] = load_rows(nc, x_rows, x_tau[chunk_rows(c), :])
 
-        load_h(0)
+        def load_in_halves(rows, dram_rows):
+            for half in range(2):
+                blocks = slice(half * (BLOCKS // 2), (half + 1) * (BLOCKS // 2))
+                nc.sync.dma_start(
+                    out=rows[:, blocks, :], in_=dram_rows.rearrange("(p j) f -> p j f", j=BLOCKS)[:, blocks, :]
+                )
+
         rec_weight_rows = const.tile([P, BLOCKS, H], BF16)
-        load_rows(nc, rec_weight_rows, W_rec)
+        load_in_halves(rec_weight_rows, W_rec)
+        first_h_rows = loads.tile([P, BLOCKS, H], BF16, tag="h_rows")
+        h_rows_of[0] = first_h_rows
+        load_in_halves(first_h_rows, h[chunk_rows(0), :])
         load_ic(0)
         tau_weight_rows = const.tile([P, BLOCKS, H], BF16)
         load_rows(nc, tau_weight_rows, tau_w_h)
@@ -240,12 +249,14 @@ def tile_liquidcell_pb_t_kernel(
 
         stream = []
         for i in range(N_CHUNKS + 1):
-            for kind, step in (("l", 1), ("z", 1), ("z", 2), ("l", 2)) if i == 1 else (
-                ("l", 1), ("z", 2), ("z", 1), ("l", 2)
-            ):
+            if i < 2:
+                order = (("l", 1, 0, 4), ("z", 1, 0, 4), ("z", 2, 0, 4), ("l", 2, 0, 4))
+            else:
+                order = (("l", 1, 0, 2), ("z", 2, 0, 4), ("l", 1, 2, 4), ("z", 1, 0, 4), ("l", 2, 0, 4))
+            for kind, step, first, end in order:
                 c = i if step == 1 else i - 1
                 if in_range(c):
-                    stream.extend((kind, step, c, n) for n in range(PACK))
+                    stream.extend((kind, step, c, n) for n in range(first, end))
         stream[0:PACK], stream[PACK : 2 * PACK] = stream[PACK : 2 * PACK], stream[0:PACK]
         issued = []
 
@@ -270,8 +281,8 @@ def tile_liquidcell_pb_t_kernel(
         def tanh_z1(c):
             nc.scalar.activation(out=z1_of[c][:], in_=z1_of[c][:], func=ACT.Tanh, scale=-1.0)
 
-        def tanh_r1(c):
-            for m in range(PACK):
+        def tanh_r1(c, tiles=range(PACK)):
+            for m in tiles:
                 nc.scalar.activation(
                     out=r1_of[c][:, m, :], in_=r1_of[c][:, m, :], func=ACT.Tanh, bias=bias_rate[:, m : m + 1], scale=0.5
                 )
@@ -313,11 +324,11 @@ def tile_liquidcell_pb_t_kernel(
                     op0=ALU.mult, op1=ALU.add,
                 )
 
-        def round_h1(c):
+        def round_h1(c, on_vector=True):
             h1_grouped = grouped_h1.tile([P, CHUNK * PACK], BF16, tag="h1_grouped", align_bytes=64)
             h1_grouped_of[c] = h1_grouped
-            nc.vector.tensor_copy(
-                out=h1_grouped[:].rearrange("p (c t) -> p c t", t=PACK), in_=h1_of[c][:].rearrange("p t c -> p c t")
+            copy_with(
+                on_vector, h1_grouped[:].rearrange("p (c t) -> p c t", t=PACK), h1_of[c][:].rearrange("p t c -> p c t")
             )
 
         def fill_z2(c, m):
@@ -418,13 +429,13 @@ def tile_liquidcell_pb_t_kernel(
             copy((name, 0), target, 0, False)
             copy((name, 1), target, 1, True)
 
-        def fill_h_flips(c):
+        def fill_h_flips(c, in_product_banks=True):
             for half in range(2):
-                fill_flipped((("h", c), half), h_rows_of[c], half, True)
+                fill_flipped((("h", c), half), h_rows_of[c], half, in_product_banks)
 
-        def fill_x_flips(c):
+        def fill_x_flips(c, in_product_banks=True):
             for half in range(2):
-                fill_flipped((("x", c), half), x_rows_of[c], half, True)
+                fill_flipped((("x", c), half), x_rows_of[c], half, in_product_banks)
 
         def copy_flips(c):
             new_h0(c)
@@ -437,12 +448,20 @@ def tile_liquidcell_pb_t_kernel(
         def quantise_h0(c):
             h0_codes_of[c] = quantise(nc, mx, h0_of[c], "h0")
 
-        fill_at_start("h0", h_rows_of[0])
         fill_at_start("rec", rec_weight_rows)
-        copy_at_start("h0", copy_grouped, h0_of[0])
-        quantise_h0(0)
+        fill_at_start("h0", h_rows_of[0])
         copy_at_start("rec", copy_grouped, rec_grouped)
         weight_of["rec"] = quantise(nc, const, rec_grouped, "rec_weight")
+        first_codes = mx.tile([P, CHUNK], U32, tag="h0_codes", align_bytes=64)
+        first_scales = mx.tile([P, CHUNK], U8, tag="h0_scales", align_bytes=64)
+        h0_codes_of[0] = (first_codes, first_scales)
+        for half in range(2):
+            copy_grouped(("h0", half), h0_of[0], half, False)
+            cols = slice(half * HALF, (half + 1) * HALF)
+            nc.vector.quantize_mx(
+                out=first_codes[:, cols].bitcast(FP8X4), scales=first_scales[:, cols],
+                in_=h0_of[0][:, half * HALF * PACK : (half + 1) * HALF * PACK],
+            )
         issue_until(PACK)
         fill_at_start("tau", tau_weight_rows)
         fill_at_start("x0", x_rows_of[0])
@@ -477,17 +496,19 @@ def tile_liquidcell_pb_t_kernel(
                 tanh_tau2(i - 1)
                 finish_d1(i)
             elif before:
-                drain(end_of_round - 3 * PACK - len(drained), limit)
-                tanh_r1(i)
+                drain(PACK // 2, limit)
+                tanh_r1(i, range(0, PACK // 2))
                 drain(PACK - 1, limit)
                 drain(1, len(issued))
                 fill_z2(i - 1, 0)
                 fill_z2(i - 1, 1)
-                drain(1, limit)
                 fill_z2(i - 1, 2)
+                drain(1, limit)
                 fill_z2(i - 1, 3)
                 tanh_a2(i - 1)
-                drain(PACK - 1, limit)
+                drain(PACK // 2 - 1, limit)
+                tanh_r1(i, range(PACK // 2, PACK))
+                drain(PACK, limit)
                 tanh_z1(i)
                 start_d1(i)
                 drain(PACK, limit)
@@ -515,10 +536,11 @@ def tile_liquidcell_pb_t_kernel(
             for m in range(PACK):
                 make_q1(i, m)
             if i == 0:
-                for c in (1, 2):
-                    fill_h_flips(c)
-                    fill_x_flips(c)
-                    copy_flips(c)
+                fill_h_flips(1)
+                fill_x_flips(1)
+                copy_flips(1)
+                fill_h_flips(2, in_product_banks=False)
+                fill_x_flips(2, in_product_banks=False)
             make_h1(i)
             if i == 1:
                 for m in range(PACK):
@@ -535,15 +557,19 @@ def tile_liquidcell_pb_t_kernel(
             if done:
                 for j in range(BLOCKS):
                     copy_and_store("h2", i - 2, j, False)
+                    if after and j == BLOCKS - 1:
+                        issue_until(limit + PACK // 2)
                     fill_tau2(i - 2, j)
-            if after:
-                issue_until(limit + PACK)
+            if i == 1:
+                issue_until(limit + PACK // 2)
             if done:
                 for j in range(BLOCKS):
                     copy_and_store("tau2", i - 2, j, False)
-            round_h1(i)
+            round_h1(i, on_vector=i > 0)
             if i == 0:
-                drain(1, limit + PACK)
+                copy_flips(2)
+                issue_until(limit + PACK)
+                drain(PACK, limit + PACK)
             if in_range(i + 3):
                 load_h(i + 3)
                 load_x(i + 3)
@@ -557,12 +583,16 @@ def tile_liquidcell_pb_t_kernel(
         limit = len(stream)
         hold_gpsimd_until_written(tau2_of[LAST - 1])
         make_d2(LAST - 1, nc.gpsimd)
-        scale_rate(LAST - 1, None)
+        for j in range(BLOCKS):
+            fill_tau2(LAST - 1, j)
+        for j in range(BLOCKS):
+            copy_and_store("tau2", LAST - 1, j, False)
         drain(PACK, limit)
         for m in range(PACK):
             fill_z2(LAST, m)
         tanh_a2(LAST)
         drain(PACK, limit)
+        scale_rate(LAST - 1, nc.vector)
         for w in TILE_PAIRS:
             make_q2(LAST - 1, w)
         make_d2(LAST, nc.vector)
@@ -573,14 +603,16 @@ def tile_liquidcell_pb_t_kernel(
         tanh_r2(LAST, last_logits)
         finish_tau2(LAST, nc.vector)
         scale_rate(LAST, nc.vector)
-        for w in TILE_PAIRS:
-            make_q2(LAST, w)
+        for half in range(2):
+            cols = slice(half * HALF, (half + 1) * HALF)
+            nc.vector.tensor_tensor(
+                out=move_of[LAST][:, :, cols], in0=rate_of[LAST][:, :, cols], in1=move_of[LAST][:, :, cols], op=ALU.mult
+            )
         jobs = []
         for kind, c, fill, engines in (
-            ("tau2", LAST - 1, fill_tau2, (False, False, False, False)),
             ("h2", LAST - 1, fill_h2, (False, False, False, False)),
-            ("tau2", LAST, fill_tau2, (False, True, False, True)),
-            ("h2", LAST, fill_h2, (False, True, False, True)),
+            ("tau2", LAST, fill_tau2, (False, False, False, False)),
+            ("h2", LAST, fill_h2, (True, False, True, False)),
         ):
             jobs.extend((kind, c, fill, engines[j], j) for j in range(BLOCKS))
         ahead = N_PRODUCT_BANKS + N_TURN_BANKS

@@ -27,6 +27,8 @@ HALF_LN_3 = 0.5 * math.log(3.0)
 TILE_PAIRS = (slice(0, 2), slice(2, 4))
 N_PRODUCT_BANKS = 4
 N_TURN_BANKS = 4
+VECTOR_ROUNDS = 256
+PRODUCTS_BEFORE_H2_BLOCK = 2
 
 FLOPS = 4 * 2 * B * H * H
 
@@ -127,11 +129,13 @@ def tile_liquidcell_pb_t_kernel(
         load_h(1)
         load_x(1)
         load_ic(1)
+        base_row_bf16 = const.tile([P, H], BF16)
+        nc.sync.dma_start(out=base_row_bf16[:], in_=tau_base.partition_broadcast(P))
 
         adapt_b = const.tile([P, PACK], F32)
         bias_rate = const.tile([P, PACK], F32)
+        half_base_row = const.tile([P, H], F32)
         base = const.tile([P, PACK], F32)
-        half_base = const.tile([P, PACK], F32)
         inverse_base = const.tile([P, PACK], F32)
         gain = const.tile([P, PACK], F32)
         minus_gain = const.tile([P, PACK], F32)
@@ -143,7 +147,6 @@ def tile_liquidcell_pb_t_kernel(
                 out=bias_rate[:], in0=adapt_b_bf16[:], scalar1=0.5, scalar2=HALF_LN_3, op0=ALU.mult, op1=ALU.add
             )
             nc.vector.tensor_copy(out=base[:], in_=base_bf16[:])
-            nc.vector.tensor_scalar(out=half_base[:], in0=base_bf16[:], scalar1=0.5, scalar2=None, op0=ALU.mult)
             nc.vector.reciprocal(out=inverse_base[:], in_=base[:])
             nc.vector.tensor_scalar(
                 out=gain[:], in0=inverse_base[:], scalar1=-2.0 * DT / 3.0, scalar2=None, op0=ALU.mult
@@ -324,11 +327,14 @@ def tile_liquidcell_pb_t_kernel(
                     op0=ALU.mult, op1=ALU.add,
                 )
 
-        def round_h1(c, on_vector=True):
+        def new_grouped_h1(c):
             h1_grouped = grouped_h1.tile([P, CHUNK * PACK], BF16, tag="h1_grouped", align_bytes=64)
             h1_grouped_of[c] = h1_grouped
+
+        def round_h1(c, cols, on_vector):
             copy_with(
-                on_vector, h1_grouped[:].rearrange("p (c t) -> p c t", t=PACK), h1_of[c][:].rearrange("p t c -> p c t")
+                on_vector, h1_grouped_of[c][:].rearrange("p (c t) -> p c t", t=PACK)[:, cols, :],
+                h1_of[c][:].rearrange("p t c -> p c t")[:, cols, :],
             )
 
         def fill_z2(c, m):
@@ -357,8 +363,8 @@ def tile_liquidcell_pb_t_kernel(
             for w in TILE_PAIRS:
                 engine.tensor_tensor(out=move[:, w, :], in0=move[:, w, :], in1=h1_of[c][:, w, :], op=ALU.subtract)
 
-        def affine(engine, tile, scale, bias, tiles=range(PACK)):
-            for m in tiles:
+        def affine(engine, tile, scale, bias):
+            for m in range(PACK):
                 if engine is None:
                     nc.scalar.activation(
                         out=tile[:, m, :], in_=tile[:, m, :], func=ACT.Identity,
@@ -373,12 +379,9 @@ def tile_liquidcell_pb_t_kernel(
         def scale_rate(c, engine):
             affine(engine, rate_of[c], gain, minus_two_gain)
 
-        def finish_tau2(c, engine, tiles=range(PACK)):
-            affine(engine, tau2_of[c], half_base, base, tiles)
-
-        def make_q2(c, w):
+        def make_q2(c, w, engine):
             move = move_of[c]
-            nc.vector.tensor_tensor(out=move[:, w, :], in0=rate_of[c][:, w, :], in1=move[:, w, :], op=ALU.mult)
+            engine.tensor_tensor(out=move[:, w, :], in0=rate_of[c][:, w, :], in1=move[:, w, :], op=ALU.mult)
 
         def fill_rows(key, terms, j, in_product_bank):
             if in_product_bank:
@@ -399,10 +402,17 @@ def tile_liquidcell_pb_t_kernel(
         def fill_h2(c, j, in_product_bank=False):
             fill_rows(("h2", c, j), [h1_of[c], move_of[c]], j, in_product_bank)
 
-        def copy_and_store(kind, c, j, on_vector):
+        def copy_and_store(kind, c, j, on_vector=False):
             out_rows = stores.tile([P, H], F32, tag="out_rows")
             out_view = out_rows[:].rearrange("r (p m) -> r p m", m=PACK)
-            copy_with(on_vector, out_view, bank_of[kind, c, j][:].rearrange("r m p -> r p m"))
+            in_view = bank_of[kind, c, j][:].rearrange("r m p -> r p m")
+            if kind == "tau2":
+                nc.vector.scalar_tensor_tensor(
+                    out=out_view, in0=in_view, scalar=2.0, in1=half_base_row[:].rearrange("r (p m) -> r p m", m=PACK),
+                    op0=ALU.add, op1=ALU.mult,
+                )
+            else:
+                copy_with(on_vector, out_view, in_view)
             dram_rows = (out_0 if kind == "h2" else out_1)[chunk_rows(c), :]
             nc.sync.dma_start(out=dram_rows.rearrange("(p j) f -> p j f", j=BLOCKS)[:, j, :], in_=out_rows[:])
 
@@ -480,7 +490,8 @@ def tile_liquidcell_pb_t_kernel(
                 hold_gpsimd_until_h1_is_quantised(i - 1)
                 make_d2(i - 2, nc.gpsimd)
                 scale_rate(i - 2, nc.gpsimd)
-                finish_tau2(i - 2, nc.gpsimd, range(1))
+                for w in TILE_PAIRS:
+                    make_q2(i - 2, w, nc.gpsimd)
             if i == 0:
                 load_h(2)
                 load_x(2)
@@ -497,28 +508,32 @@ def tile_liquidcell_pb_t_kernel(
                 finish_d1(i)
             elif before:
                 drain(PACK // 2, limit)
-                tanh_r1(i, range(0, PACK // 2))
                 drain(PACK - 1, limit)
                 drain(1, len(issued))
                 fill_z2(i - 1, 0)
                 fill_z2(i - 1, 1)
+                drain(1, limit)
                 fill_z2(i - 1, 2)
                 drain(1, limit)
                 fill_z2(i - 1, 3)
                 tanh_a2(i - 1)
-                drain(PACK // 2 - 1, limit)
-                tanh_r1(i, range(PACK // 2, PACK))
-                drain(PACK, limit)
+                drain(PACK + PACK // 2 - 2, limit)
                 tanh_z1(i)
-                start_d1(i)
+                tanh_r1(i)
                 drain(PACK, limit)
+                fill_tau2(i - 2, 0, True)
+                fill_d1_with_h(i, 0)
+                fill_d1_with_h(i, 1)
+                fill_tau2(i - 2, 1, True)
+                fill_d1_with_h(i, 2)
+                fill_d1_with_h(i, 3)
+                fill_tau2(i - 2, 2, True)
+                for j in range(BLOCKS - 1):
+                    copy_and_store("tau2", i - 2, j)
                 tanh_tau2(i - 1)
-                if done:
-                    finish_tau2(i - 2, None, range(3, PACK))
-                if in_range(i + 2):
-                    fill_h_flips(i + 2)
                 finish_d1(i)
                 if in_range(i + 2):
+                    fill_h_flips(i + 2)
                     fill_x_flips(i + 2)
                     copy_flips(i + 2)
             else:
@@ -528,11 +543,6 @@ def tile_liquidcell_pb_t_kernel(
                 drain(PACK, limit)
                 tanh_r1(i)
                 finish_d1(i)
-            if done:
-                for w in TILE_PAIRS:
-                    make_q2(i - 2, w)
-                hold_gpsimd_until_written(move_of[i - 2])
-                finish_tau2(i - 2, nc.gpsimd, range(1, 3))
             for m in range(PACK):
                 make_q1(i, m)
             if i == 0:
@@ -551,21 +561,29 @@ def tile_liquidcell_pb_t_kernel(
                 copy_flips(3)
             if after:
                 quantise_h0(i + 1)
+            new_grouped_h1(i)
+            if i == 1:
+                round_h1(i, slice(0, CHUNK), on_vector=True)
+            else:
+                round_h1(i, slice(0, VECTOR_ROUNDS), on_vector=True)
+                round_h1(i, slice(VECTOR_ROUNDS, CHUNK), on_vector=False)
             if done:
-                for j in range(BLOCKS):
-                    fill_h2(i - 2, j)
-            if done:
-                for j in range(BLOCKS):
-                    copy_and_store("h2", i - 2, j, False)
-                    if after and j == BLOCKS - 1:
+                fill_tau2(i - 2, BLOCKS - 1)
+                copy_and_store("tau2", i - 2, BLOCKS - 1)
+                if not after:
+                    fill_tau2(LAST - 1, 0, True)
+                    fill_tau2(LAST - 1, 1, True)
+                for j in range(BLOCKS - 1):
+                    if after and j == PRODUCTS_BEFORE_H2_BLOCK:
                         issue_until(limit + PACK // 2)
-                    fill_tau2(i - 2, j)
+                    fill_h2(i - 2, j)
+                for j in range(BLOCKS - 1):
+                    copy_and_store("h2", i - 2, j)
             if i == 1:
                 issue_until(limit + PACK // 2)
-            if done:
-                for j in range(BLOCKS):
-                    copy_and_store("tau2", i - 2, j, False)
-            round_h1(i, on_vector=i > 0)
+                nc.vector.tensor_scalar(
+                    out=half_base_row[:], in0=base_row_bf16[:], scalar1=0.5, scalar2=None, op0=ALU.mult
+                )
             if i == 0:
                 copy_flips(2)
                 issue_until(limit + PACK)
@@ -574,34 +592,39 @@ def tile_liquidcell_pb_t_kernel(
                 load_h(i + 3)
                 load_x(i + 3)
             h1_codes_of[i] = quantise(nc, mx, h1_grouped_of[i], "h1")
-            if not after:
-                finish_tau2(LAST - 1, nc.vector)
             if before:
                 tanh_r2(i - 1, rate_of[i - 1])
+            if not after:
+                issue_until(len(drained) + N_PRODUCT_BANKS - 2)
+                copy_and_store("tau2", LAST - 1, 0)
+                copy_and_store("tau2", LAST - 1, 1)
             issue_until(len(drained) + N_PRODUCT_BANKS)
+            if done:
+                fill_h2(i - 2, BLOCKS - 1)
+                copy_and_store("h2", i - 2, BLOCKS - 1)
 
         limit = len(stream)
-        hold_gpsimd_until_written(tau2_of[LAST - 1])
+        hold_gpsimd_until_h1_is_quantised(LAST)
         make_d2(LAST - 1, nc.gpsimd)
-        for j in range(BLOCKS):
-            fill_tau2(LAST - 1, j)
-        for j in range(BLOCKS):
-            copy_and_store("tau2", LAST - 1, j, False)
+        scale_rate(LAST - 1, None)
         drain(PACK, limit)
         for m in range(PACK):
             fill_z2(LAST, m)
         tanh_a2(LAST)
         drain(PACK, limit)
-        scale_rate(LAST - 1, nc.vector)
+        for j in (2, 3):
+            fill_tau2(LAST - 1, j, True)
+        for j in (2, 3):
+            copy_and_store("tau2", LAST - 1, j)
         for w in TILE_PAIRS:
-            make_q2(LAST - 1, w)
+            make_q2(LAST - 1, w, nc.vector)
         make_d2(LAST, nc.vector)
         last_logits = rate_of[LAST]
+        last_rate = rates.tile([P, PACK, CHUNK], F32, tag="rate")
+        tanh_r2(LAST, last_rate)
         last_tau2 = step2.tile([P, PACK, CHUNK], F32, tag="tau2")
         tau2_of[LAST] = last_tau2
         nc.scalar.activation(out=last_tau2[:], in_=last_logits[:], func=ACT.Tanh, scale=0.5)
-        tanh_r2(LAST, last_logits)
-        finish_tau2(LAST, nc.vector)
         scale_rate(LAST, nc.vector)
         for half in range(2):
             cols = slice(half * HALF, (half + 1) * HALF)
@@ -609,17 +632,13 @@ def tile_liquidcell_pb_t_kernel(
                 out=move_of[LAST][:, :, cols], in0=rate_of[LAST][:, :, cols], in1=move_of[LAST][:, :, cols], op=ALU.mult
             )
         jobs = []
-        for kind, c, fill, engines in (
-            ("h2", LAST - 1, fill_h2, (False, False, False, False)),
-            ("tau2", LAST, fill_tau2, (False, False, False, False)),
-            ("h2", LAST, fill_h2, (True, False, True, False)),
-        ):
-            jobs.extend((kind, c, fill, engines[j], j) for j in range(BLOCKS))
+        for kind, c, fill in (("h2", LAST - 1, fill_h2), ("tau2", LAST, fill_tau2), ("h2", LAST, fill_h2)):
+            jobs.extend((kind, c, fill, j) for j in range(BLOCKS))
         ahead = N_PRODUCT_BANKS + N_TURN_BANKS
         for n in range(len(jobs) + ahead):
             if n >= ahead:
-                kind, c, fill, on_vector, j = jobs[n - ahead]
-                copy_and_store(kind, c, j, on_vector)
+                kind, c, fill, j = jobs[n - ahead]
+                copy_and_store(kind, c, j)
             if n < len(jobs):
-                kind, c, fill, on_vector, j = jobs[n]
+                kind, c, fill, j = jobs[n]
                 fill(c, j, n % 2 == 1)

@@ -363,8 +363,8 @@ def tile_liquidcell_pb_t_kernel(
             for w in TILE_PAIRS:
                 engine.tensor_tensor(out=move[:, w, :], in0=move[:, w, :], in1=h1_of[c][:, w, :], op=ALU.subtract)
 
-        def affine(engine, tile, scale, bias):
-            for m in range(PACK):
+        def affine(engine, tile, scale, bias, tiles=range(PACK)):
+            for m in tiles:
                 if engine is None:
                     nc.scalar.activation(
                         out=tile[:, m, :], in_=tile[:, m, :], func=ACT.Identity,
@@ -376,8 +376,8 @@ def tile_liquidcell_pb_t_kernel(
                         op0=ALU.mult, op1=ALU.add,
                     )
 
-        def scale_rate(c, engine):
-            affine(engine, rate_of[c], gain, minus_two_gain)
+        def scale_rate(c, engine, tiles=range(PACK)):
+            affine(engine, rate_of[c], gain, minus_two_gain, tiles)
 
         def make_q2(c, w, engine):
             move = move_of[c]
@@ -489,7 +489,7 @@ def tile_liquidcell_pb_t_kernel(
             if done:
                 hold_gpsimd_until_h1_is_quantised(i - 1)
                 make_d2(i - 2, nc.gpsimd)
-                scale_rate(i - 2, nc.gpsimd)
+                scale_rate(i - 2, nc.gpsimd, range(0, 2))
                 for w in TILE_PAIRS:
                     make_q2(i - 2, w, nc.gpsimd)
             if i == 0:
@@ -594,6 +594,8 @@ def tile_liquidcell_pb_t_kernel(
             h1_codes_of[i] = quantise(nc, mx, h1_grouped_of[i], "h1")
             if before:
                 tanh_r2(i - 1, rate_of[i - 1])
+                if after:
+                    scale_rate(i - 1, None, range(2, PACK))
             if not after:
                 issue_until(len(drained) + N_PRODUCT_BANKS - 2)
                 copy_and_store("tau2", LAST - 1, 0)

@@ -27,7 +27,7 @@ HALF_LN_3 = 0.5 * math.log(3.0)
 TILE_PAIRS = (slice(0, 2), slice(2, 4))
 N_PRODUCT_BANKS = 4
 N_TURN_BANKS = 4
-VECTOR_ROUNDS = 256
+VECTOR_ROUNDS = 272
 PRODUCTS_BEFORE_H2_BLOCK = 2
 
 FLOPS = 4 * 2 * B * H * H
@@ -65,6 +65,7 @@ def tile_liquidcell_pb_t_kernel(
         ctx.enter_context(tc.manual_schedule())
         const = ctx.enter_context(tc.tile_pool(name="const", bufs=1))
         loads = ctx.enter_context(tc.tile_pool(name="loads", bufs=2))
+        h_loads = ctx.enter_context(tc.tile_pool(name="h_loads", bufs=4))
         ic_loads = ctx.enter_context(tc.tile_pool(name="ic_loads", bufs=4))
         flips = ctx.enter_context(tc.tile_pool(name="flips", bufs=3))
         plains = ctx.enter_context(tc.tile_pool(name="plains", bufs=4))
@@ -72,10 +73,11 @@ def tile_liquidcell_pb_t_kernel(
         mx = ctx.enter_context(tc.tile_pool(name="mx", bufs=2))
         work = ctx.enter_context(tc.tile_pool(name="work", bufs=1))
         step2 = ctx.enter_context(tc.tile_pool(name="step2", bufs=2))
-        pairs = ctx.enter_context(tc.tile_pool(name="pairs", bufs=2))
+        pairs = ctx.enter_context(tc.tile_pool(name="pairs", bufs=1))
         rates = ctx.enter_context(tc.tile_pool(name="rates", bufs=3))
         states = ctx.enter_context(tc.tile_pool(name="states", bufs=3))
-        stores = ctx.enter_context(tc.tile_pool(name="stores", bufs=3 * BLOCKS))
+        stores = ctx.enter_context(tc.tile_pool(name="stores", bufs=6))
+        tau_stores = ctx.enter_context(tc.tile_pool(name="tau_stores", bufs=2))
         products = ctx.enter_context(tc.psum_pool(name="products", bufs=N_PRODUCT_BANKS))
         turns = ctx.enter_context(tc.psum_pool(name="turns", bufs=N_TURN_BANKS))
 
@@ -95,7 +97,7 @@ def tile_liquidcell_pb_t_kernel(
             return 0 <= c < N_CHUNKS
 
         def load_h(c):
-            h_rows = loads.tile([P, BLOCKS, H], BF16, tag="h_rows")
+            h_rows = h_loads.tile([P, BLOCKS, H], BF16, tag="h_rows")
             h_rows_of[c] = load_rows(nc, h_rows, h[chunk_rows(c), :])
 
         def load_ic(c):
@@ -115,7 +117,7 @@ def tile_liquidcell_pb_t_kernel(
 
         rec_weight_rows = const.tile([P, BLOCKS, H], BF16)
         load_in_halves(rec_weight_rows, W_rec)
-        first_h_rows = loads.tile([P, BLOCKS, H], BF16, tag="h_rows")
+        first_h_rows = h_loads.tile([P, BLOCKS, H], BF16, tag="h_rows")
         h_rows_of[0] = first_h_rows
         load_in_halves(first_h_rows, h[chunk_rows(0), :])
         load_ic(0)
@@ -293,7 +295,12 @@ def tile_liquidcell_pb_t_kernel(
         def fill_d1_with_h(c, m):
             bank = turns.tile([P, CHUNK], F32, tag="turned")
             bank_of["d1", c, m] = bank
-            nc.tensor.matmul(out=bank[:], lhsT=ident_bf16[:], rhs=h0_tile(c, m), start=True, stop=False)
+            for j in range(BLOCKS):
+                nc.tensor.matmul(
+                    out=bank[:, j * P : (j + 1) * P],
+                    lhsT=h_rows_of[c][:, j, :].rearrange("r (p m) -> r m p", m=PACK)[:, m, :], rhs=ident_bf16[:],
+                    start=(j == 0), stop=False,
+                )
 
         def add_minus_a1(c, m):
             bank = bank_of["d1", c, m]
@@ -402,19 +409,29 @@ def tile_liquidcell_pb_t_kernel(
         def fill_h2(c, j, in_product_bank=False):
             fill_rows(("h2", c, j), [h1_of[c], move_of[c]], j, in_product_bank)
 
-        def copy_and_store(kind, c, j, on_vector=False):
-            out_rows = stores.tile([P, H], F32, tag="out_rows")
-            out_view = out_rows[:].rearrange("r (p m) -> r p m", m=PACK)
+        tau_rows_of = {}
+
+        def copy_and_store(kind, c, j):
             in_view = bank_of[kind, c, j][:].rearrange("r m p -> r p m")
             if kind == "tau2":
+                if j == 0:
+                    tau_rows = tau_stores.tile([P, BLOCKS, H], F32, tag="tau_rows")
+                    tau_rows_of[c] = tau_rows
+                tau_rows = tau_rows_of[c]
                 nc.vector.scalar_tensor_tensor(
-                    out=out_view, in0=in_view, scalar=2.0, in1=half_base_row[:].rearrange("r (p m) -> r p m", m=PACK),
-                    op0=ALU.add, op1=ALU.mult,
+                    out=tau_rows[:, j, :].rearrange("r (p m) -> r p m", m=PACK), in0=in_view, scalar=2.0,
+                    in1=half_base_row[:].rearrange("r (p m) -> r p m", m=PACK), op0=ALU.add, op1=ALU.mult,
                 )
+                dram_blocks = out_1[chunk_rows(c), :].rearrange("(p j) f -> p j f", j=BLOCKS)
+                if c == LAST:
+                    nc.sync.dma_start(out=dram_blocks[:, j, :], in_=tau_rows[:, j, :])
+                elif j == BLOCKS - 1:
+                    nc.sync.dma_start(out=dram_blocks, in_=tau_rows[:])
             else:
-                copy_with(on_vector, out_view, in_view)
-            dram_rows = (out_0 if kind == "h2" else out_1)[chunk_rows(c), :]
-            nc.sync.dma_start(out=dram_rows.rearrange("(p j) f -> p j f", j=BLOCKS)[:, j, :], in_=out_rows[:])
+                out_rows = stores.tile([P, H], F32, tag="out_rows")
+                nc.scalar.copy(out=out_rows[:].rearrange("r (p m) -> r p m", m=PACK), in_=in_view)
+                dram_blocks = out_0[chunk_rows(c), :].rearrange("(p j) f -> p j f", j=BLOCKS)
+                nc.sync.dma_start(out=dram_blocks[:, j, :], in_=out_rows[:])
 
         gate_word = const.tile([P, 1], U32)
 
@@ -489,7 +506,7 @@ def tile_liquidcell_pb_t_kernel(
             if done:
                 hold_gpsimd_until_h1_is_quantised(i - 1)
                 make_d2(i - 2, nc.gpsimd)
-                scale_rate(i - 2, nc.gpsimd, range(0, 2))
+                scale_rate(i - 2, nc.gpsimd, range(0, 3))
                 for w in TILE_PAIRS:
                     make_q2(i - 2, w, nc.gpsimd)
             if i == 0:
@@ -508,6 +525,9 @@ def tile_liquidcell_pb_t_kernel(
                 finish_d1(i)
             elif before:
                 drain(PACK // 2, limit)
+                if in_range(i - 3):
+                    fill_h2(i - 3, BLOCKS - 1)
+                    copy_and_store("h2", i - 3, BLOCKS - 1)
                 drain(PACK - 1, limit)
                 drain(1, len(issued))
                 fill_z2(i - 1, 0)
@@ -595,13 +615,13 @@ def tile_liquidcell_pb_t_kernel(
             if before:
                 tanh_r2(i - 1, rate_of[i - 1])
                 if after:
-                    scale_rate(i - 1, None, range(2, PACK))
+                    scale_rate(i - 1, None, range(3, PACK))
             if not after:
                 issue_until(len(drained) + N_PRODUCT_BANKS - 2)
                 copy_and_store("tau2", LAST - 1, 0)
                 copy_and_store("tau2", LAST - 1, 1)
             issue_until(len(drained) + N_PRODUCT_BANKS)
-            if done:
+            if not after:
                 fill_h2(i - 2, BLOCKS - 1)
                 copy_and_store("h2", i - 2, BLOCKS - 1)
 

@@ -28,6 +28,7 @@ TILE_PAIRS = (slice(0, 2), slice(2, 4))
 N_PRODUCT_BANKS = 4
 N_TURN_BANKS = 4
 VECTOR_ROUNDS = 272
+LINE = 4
 PRODUCTS_BEFORE_H2_BLOCK = 2
 
 FLOPS = 4 * 2 * B * H * H
@@ -340,8 +341,9 @@ def tile_liquidcell_pb_t_kernel(
 
         def round_h1(c, cols, on_vector):
             copy_with(
-                on_vector, h1_grouped_of[c][:].rearrange("p (c t) -> p c t", t=PACK)[:, cols, :],
-                h1_of[c][:].rearrange("p t c -> p c t")[:, cols, :],
+                on_vector,
+                h1_grouped_of[c][:, cols.start * PACK : cols.stop * PACK].rearrange("p (c i t) -> p c t i", i=LINE, t=PACK),
+                h1_of[c][:, :, cols].rearrange("p t (c i) -> p c t i", i=LINE),
             )
 
         def fill_z2(c, m):
@@ -536,10 +538,11 @@ def tile_liquidcell_pb_t_kernel(
                 fill_z2(i - 1, 2)
                 drain(1, limit)
                 fill_z2(i - 1, 3)
+                tanh_r1(i, range(0, 2))
                 tanh_a2(i - 1)
                 drain(PACK + PACK // 2 - 2, limit)
                 tanh_z1(i)
-                tanh_r1(i)
+                tanh_r1(i, range(2, PACK))
                 drain(PACK, limit)
                 fill_tau2(i - 2, 0, True)
                 fill_d1_with_h(i, 0)

@@ -27,7 +27,8 @@ HALF_LN_3 = 0.5 * math.log(3.0)
 TILE_PAIRS = (slice(0, 2), slice(2, 4))
 N_PRODUCT_BANKS = 4
 N_TURN_BANKS = 4
-VECTOR_ROUNDS = 272
+VECTOR_ROUNDS = 64
+H2_BEFORE_ROUNDING = 0
 LINE = 4
 PRODUCTS_BEFORE_H2_BLOCK = 2
 
@@ -75,7 +76,7 @@ def tile_liquidcell_pb_t_kernel(
         work = ctx.enter_context(tc.tile_pool(name="work", bufs=1))
         step2 = ctx.enter_context(tc.tile_pool(name="step2", bufs=2))
         pairs = ctx.enter_context(tc.tile_pool(name="pairs", bufs=1))
-        rates = ctx.enter_context(tc.tile_pool(name="rates", bufs=3))
+        rates = ctx.enter_context(tc.tile_pool(name="rates", bufs=2))
         states = ctx.enter_context(tc.tile_pool(name="states", bufs=3))
         stores = ctx.enter_context(tc.tile_pool(name="stores", bufs=6))
         tau_stores = ctx.enter_context(tc.tile_pool(name="tau_stores", bufs=2))
@@ -133,7 +134,6 @@ def tile_liquidcell_pb_t_kernel(
         load_x(1)
         load_ic(1)
         base_row_bf16 = const.tile([P, H], BF16)
-        nc.sync.dma_start(out=base_row_bf16[:], in_=tau_base.partition_broadcast(P))
 
         adapt_b = const.tile([P, PACK], F32)
         bias_rate = const.tile([P, PACK], F32)
@@ -329,11 +329,13 @@ def tile_liquidcell_pb_t_kernel(
         def make_h1(c):
             h1 = states.tile([P, PACK, CHUNK], F32, tag="h1")
             h1_of[c] = h1
-            for m in range(PACK):
-                nc.vector.scalar_tensor_tensor(
-                    out=h1[:, m, :], in0=r1_of[c][:, m, :], scalar=minus_gain[:, m : m + 1], in1=h0_tile(c, m),
-                    op0=ALU.mult, op1=ALU.add,
-                )
+            for half in range(2):
+                cols = slice(half * HALF, (half + 1) * HALF)
+                for m in range(PACK):
+                    nc.vector.scalar_tensor_tensor(
+                        out=h1[:, m, cols], in0=r1_of[c][:, m, cols], scalar=minus_gain[:, m : m + 1],
+                        in1=h0_tile(c, m)[:, cols], op0=ALU.mult, op1=ALU.add,
+                    )
 
         def new_grouped_h1(c):
             h1_grouped = grouped_h1.tile([P, CHUNK * PACK], BF16, tag="h1_grouped", align_bytes=64)
@@ -344,6 +346,18 @@ def tile_liquidcell_pb_t_kernel(
                 on_vector,
                 h1_grouped_of[c][:, cols.start * PACK : cols.stop * PACK].rearrange("p (c i t) -> p c t i", i=LINE, t=PACK),
                 h1_of[c][:, :, cols].rearrange("p t (c i) -> p c t i", i=LINE),
+            )
+
+        def quantise_h1_half(c, half):
+            if half == 0:
+                codes = mx.tile([P, CHUNK], U32, tag="h1_codes", align_bytes=64)
+                scales = mx.tile([P, CHUNK], U8, tag="h1_scales", align_bytes=64)
+                h1_codes_of[c] = (codes, scales)
+            codes, scales = h1_codes_of[c]
+            cols = slice(half * HALF, (half + 1) * HALF)
+            nc.vector.quantize_mx(
+                out=codes[:, cols].bitcast(FP8X4), scales=scales[:, cols],
+                in_=h1_grouped_of[c][:, half * HALF * PACK : (half + 1) * HALF * PACK],
             )
 
         def fill_z2(c, m):
@@ -438,7 +452,7 @@ def tile_liquidcell_pb_t_kernel(
         gate_word = const.tile([P, 1], U32)
 
         def hold_gpsimd_until_h1_is_quantised(c):
-            nc.gpsimd.tensor_copy(out=gate_word[:], in_=h1_codes_of[c][0][:, 0:1])
+            nc.gpsimd.tensor_copy(out=gate_word[:], in_=h1_codes_of[c][0][:, CHUNK - 1 : CHUNK])
 
         gate_value = const.tile([P, 1], F32)
 
@@ -508,7 +522,7 @@ def tile_liquidcell_pb_t_kernel(
             if done:
                 hold_gpsimd_until_h1_is_quantised(i - 1)
                 make_d2(i - 2, nc.gpsimd)
-                scale_rate(i - 2, nc.gpsimd, range(0, 3))
+                scale_rate(i - 2, nc.gpsimd, range(0, 4))
                 for w in TILE_PAIRS:
                     make_q2(i - 2, w, nc.gpsimd)
             if i == 0:
@@ -542,7 +556,7 @@ def tile_liquidcell_pb_t_kernel(
                 tanh_a2(i - 1)
                 drain(PACK + PACK // 2 - 2, limit)
                 tanh_z1(i)
-                tanh_r1(i, range(2, PACK))
+                tanh_r1(i, (3, 2))
                 drain(PACK, limit)
                 fill_tau2(i - 2, 0, True)
                 fill_d1_with_h(i, 0)
@@ -588,20 +602,29 @@ def tile_liquidcell_pb_t_kernel(
             if i == 1:
                 round_h1(i, slice(0, CHUNK), on_vector=True)
             else:
-                round_h1(i, slice(0, VECTOR_ROUNDS), on_vector=True)
-                round_h1(i, slice(VECTOR_ROUNDS, CHUNK), on_vector=False)
+                round_h1(i, slice(0, HALF), on_vector=False)
+                if VECTOR_ROUNDS:
+                    round_h1(i, slice(HALF, HALF + VECTOR_ROUNDS), on_vector=True)
+                if done:
+                    for j in range(H2_BEFORE_ROUNDING):
+                        fill_h2(i - 2, j)
+                        copy_and_store("h2", i - 2, j)
+                round_h1(i, slice(HALF + VECTOR_ROUNDS, CHUNK), on_vector=False)
+            quantise_h1_half(i, 0)
             if done:
                 fill_tau2(i - 2, BLOCKS - 1)
                 copy_and_store("tau2", i - 2, BLOCKS - 1)
                 if not after:
                     fill_tau2(LAST - 1, 0, True)
                     fill_tau2(LAST - 1, 1, True)
-                for j in range(BLOCKS - 1):
+                for j in range(H2_BEFORE_ROUNDING, BLOCKS - 1):
                     if after and j == PRODUCTS_BEFORE_H2_BLOCK:
                         issue_until(limit + PACK // 2)
                     fill_h2(i - 2, j)
-                for j in range(BLOCKS - 1):
+                for j in range(H2_BEFORE_ROUNDING, BLOCKS - 1):
                     copy_and_store("h2", i - 2, j)
+            if i == 0:
+                nc.sync.dma_start(out=base_row_bf16[:], in_=tau_base.partition_broadcast(P))
             if i == 1:
                 issue_until(limit + PACK // 2)
                 nc.vector.tensor_scalar(
@@ -614,11 +637,11 @@ def tile_liquidcell_pb_t_kernel(
             if in_range(i + 3):
                 load_h(i + 3)
                 load_x(i + 3)
-            h1_codes_of[i] = quantise(nc, mx, h1_grouped_of[i], "h1")
+            quantise_h1_half(i, 1)
             if before:
                 tanh_r2(i - 1, rate_of[i - 1])
                 if after:
-                    scale_rate(i - 1, None, range(3, PACK))
+                    scale_rate(i - 1, None, range(4, PACK))
             if not after:
                 issue_until(len(drained) + N_PRODUCT_BANKS - 2)
                 copy_and_store("tau2", LAST - 1, 0)
@@ -645,7 +668,7 @@ def tile_liquidcell_pb_t_kernel(
             make_q2(LAST - 1, w, nc.vector)
         make_d2(LAST, nc.vector)
         last_logits = rate_of[LAST]
-        last_rate = rates.tile([P, PACK, CHUNK], F32, tag="rate")
+        last_rate = pairs.tile([P, PACK, CHUNK], F32, tag="r1")
         tanh_r2(LAST, last_rate)
         last_tau2 = step2.tile([P, PACK, CHUNK], F32, tag="tau2")
         tau2_of[LAST] = last_tau2

@@ -27,7 +27,7 @@ HALF_LN_3 = 0.5 * math.log(3.0)
 TILE_PAIRS = (slice(0, 2), slice(2, 4))
 N_PRODUCT_BANKS = 4
 N_TURN_BANKS = 4
-VECTOR_ROUNDS = 64
+VECTOR_ROUNDS = 96
 H2_BEFORE_ROUNDING = 0
 LINE = 4
 PRODUCTS_BEFORE_H2_BLOCK = 2
@@ -565,7 +565,8 @@ def tile_liquidcell_pb_t_kernel(
                 fill_d1_with_h(i, 2)
                 fill_d1_with_h(i, 3)
                 fill_tau2(i - 2, 2, True)
-                for j in range(BLOCKS - 1):
+                fill_tau2(i - 2, 3, True)
+                for j in range(BLOCKS):
                     copy_and_store("tau2", i - 2, j)
                 tanh_tau2(i - 1)
                 finish_d1(i)
@@ -602,25 +603,23 @@ def tile_liquidcell_pb_t_kernel(
             if i == 1:
                 round_h1(i, slice(0, CHUNK), on_vector=True)
             else:
-                round_h1(i, slice(0, HALF), on_vector=False)
-                if VECTOR_ROUNDS:
-                    round_h1(i, slice(HALF, HALF + VECTOR_ROUNDS), on_vector=True)
                 if done:
                     for j in range(H2_BEFORE_ROUNDING):
                         fill_h2(i - 2, j)
                         copy_and_store("h2", i - 2, j)
+                round_h1(i, slice(0, HALF), on_vector=False)
+                if VECTOR_ROUNDS:
+                    round_h1(i, slice(HALF, HALF + VECTOR_ROUNDS), on_vector=True)
                 round_h1(i, slice(HALF + VECTOR_ROUNDS, CHUNK), on_vector=False)
             quantise_h1_half(i, 0)
             if done:
-                fill_tau2(i - 2, BLOCKS - 1)
-                copy_and_store("tau2", i - 2, BLOCKS - 1)
                 if not after:
                     fill_tau2(LAST - 1, 0, True)
                     fill_tau2(LAST - 1, 1, True)
                 for j in range(H2_BEFORE_ROUNDING, BLOCKS - 1):
-                    if after and j == PRODUCTS_BEFORE_H2_BLOCK:
-                        issue_until(limit + PACK // 2)
                     fill_h2(i - 2, j)
+                if after:
+                    issue_until(limit + PACK // 2)
                 for j in range(H2_BEFORE_ROUNDING, BLOCKS - 1):
                     copy_and_store("h2", i - 2, j)
             if i == 0:

import math
from contextlib import ExitStack

import concourse.mybir as mybir
from concourse.masks import make_identity

F32 = mybir.dt.float32
BF16 = mybir.dt.bfloat16
U32 = mybir.dt.uint32
U8 = mybir.dt.uint8
FP8X4 = mybir.dt.float8_e4m3fn_x4
ALU = mybir.AluOpType
ACT = mybir.ActivationFunctionType

B = 4096
H = 512
DT = 0.1
P = 128
PACK = 4
PAIR = 2
CHUNK = 512
BLOCKS = CHUNK // P
HALF = CHUNK // 2
N_CHUNKS = B // CHUNK
LAST = N_CHUNKS - 1
HALF_LN_3 = 0.5 * math.log(3.0)
TILE_PAIRS = (slice(0, 2), slice(2, 4))
N_PRODUCT_BANKS = 4
N_TURN_BANKS = 4
VECTOR_ROUNDS = 96
H2_BEFORE_ROUNDING = 0
LINE = 4
PRODUCTS_BEFORE_H2_BLOCK = 2

FLOPS = 4 * 2 * B * H * H


def load_rows(nc, rows, dram_rows):
    nc.sync.dma_start(out=rows[:], in_=dram_rows.rearrange("(p j) f -> p j f", j=BLOCKS))
    return rows


def quantise(nc, pool, grouped, tag):
    codes = pool.tile([P, CHUNK], U32, tag=tag + "_codes", align_bytes=64)
    scales = pool.tile([P, CHUNK], U8, tag=tag + "_scales", align_bytes=64)
    nc.vector.quantize_mx(out=codes[:].bitcast(FP8X4), scales=scales[:], in_=grouped[:])
    return codes, scales


def multiply(nc, banks, stationary, block, moving):
    s_codes, s_scales = stationary
    m_codes, m_scales = moving
    product = banks.tile([P, CHUNK], F32, tag="product")
    cols = slice(block * P, (block + 1) * P)
    nc.tensor.matmul_mx(
        out=product[:], lhsT=s_codes[:, cols].bitcast(FP8X4), lhsT_scale=s_scales[:, cols],
        rhs=m_codes[:].bitcast(FP8X4), rhs_scale=m_scales[:], start=True, stop=True,
    )
    return product


def tile_liquidcell_pb_t_kernel(
    tc, h, input_contrib, x_tau, W_rec, tau_w_h, tau_adapt_b, tau_base, out_0, out_1
):
    nc = tc.nc
    with ExitStack() as ctx:
        ctx.enter_context(tc.manual_schedule())
        const = ctx.enter_context(tc.tile_pool(name="const", bufs=1))
        loads = ctx.enter_context(tc.tile_pool(name="loads", bufs=2))
        h_loads = ctx.enter_context(tc.tile_pool(name="h_loads", bufs=4))
        ic_loads = ctx.enter_context(tc.tile_pool(name="ic_loads", bufs=4))
        flips = ctx.enter_context(tc.tile_pool(name="flips", bufs=3))
        plains = ctx.enter_context(tc.tile_pool(name="plains", bufs=4))
        grouped_h1 = ctx.enter_context(tc.tile_pool(name="grouped_h1", bufs=2))
        mx = ctx.enter_context(tc.tile_pool(name="mx", bufs=2))
        work = ctx.enter_context(tc.tile_pool(name="work", bufs=1))
        step2 = ctx.enter_context(tc.tile_pool(name="step2", bufs=2))
        pairs = ctx.enter_context(tc.tile_pool(name="pairs", bufs=1))
        rates = ctx.enter_context(tc.tile_pool(name="rates", bufs=2))
        states = ctx.enter_context(tc.tile_pool(name="states", bufs=3))
        stores = ctx.enter_context(tc.tile_pool(name="stores", bufs=6))
        tau_stores = ctx.enter_context(tc.tile_pool(name="tau_stores", bufs=2))
        products = ctx.enter_context(tc.psum_pool(name="products", bufs=N_PRODUCT_BANKS))
        turns = ctx.enter_context(tc.psum_pool(name="turns", bufs=N_TURN_BANKS))

        ident_f32 = const.tile([P, P], F32)
        make_identity(nc, ident_f32[:])
        ident_bf16 = const.tile([P, P], BF16)
        make_identity(nc, ident_bf16[:])

        h_rows_of = {}
        ic_rows_of = {}
        x_rows_of = {}

        def chunk_rows(c):
            return slice(c * CHUNK, (c + 1) * CHUNK)

        def in_range(c):
            return 0 <= c < N_CHUNKS

        def load_h(c):
            h_rows = h_loads.tile([P, BLOCKS, H], BF16, tag="h_rows")
            h_rows_of[c] = load_rows(nc, h_rows, h[chunk_rows(c), :])

        def load_ic(c):
            ic_rows = ic_loads.tile([P, BLOCKS, H], BF16, tag="ic_rows")
            ic_rows_of[c] = load_rows(nc, ic_rows, input_contrib[chunk_rows(c), :])

        def load_x(c):
            x_rows = loads.tile([P, BLOCKS, H], BF16, tag="x_rows")
            x_rows_of[c] = load_rows(nc, x_rows, x_tau[chunk_rows(c), :])

        def load_in_halves(rows, dram_rows):
            for half in range(2):
                blocks = slice(half * (BLOCKS // 2), (half + 1) * (BLOCKS // 2))
                nc.sync.dma_start(
                    out=rows[:, blocks, :], in_=dram_rows.rearrange("(p j) f -> p j f", j=BLOCKS)[:, blocks, :]
                )

        rec_weight_rows = const.tile([P, BLOCKS, H], BF16)
        load_in_halves(rec_weight_rows, W_rec)
        first_h_rows = h_loads.tile([P, BLOCKS, H], BF16, tag="h_rows")
        h_rows_of[0] = first_h_rows
        load_in_halves(first_h_rows, h[chunk_rows(0), :])
        load_ic(0)
        tau_weight_rows = const.tile([P, BLOCKS, H], BF16)
        load_rows(nc, tau_weight_rows, tau_w_h)
        adapt_b_bf16 = const.tile([P, PACK], BF16)
        nc.sync.dma_start(out=adapt_b_bf16[:], in_=tau_adapt_b.rearrange("(p m) -> p m", m=PACK))
        base_bf16 = const.tile([P, PACK], BF16)
        nc.sync.dma_start(out=base_bf16[:], in_=tau_base.rearrange("(p m) -> p m", m=PACK))
        load_x(0)
        load_h(1)
        load_x(1)
        load_ic(1)
        base_row_bf16 = const.tile([P, H], BF16)

        adapt_b = const.tile([P, PACK], F32)
        bias_rate = const.tile([P, PACK], F32)
        half_base_row = const.tile([P, H], F32)
        base = const.tile([P, PACK], F32)
        inverse_base = const.tile([P, PACK], F32)
        gain = const.tile([P, PACK], F32)
        minus_gain = const.tile([P, PACK], F32)
        minus_two_gain = const.tile([P, PACK], F32)

        def make_vectors():
            nc.vector.tensor_copy(out=adapt_b[:], in_=adapt_b_bf16[:])
            nc.vector.tensor_scalar(
                out=bias_rate[:], in0=adapt_b_bf16[:], scalar1=0.5, scalar2=HALF_LN_3, op0=ALU.mult, op1=ALU.add
            )
            nc.vector.tensor_copy(out=base[:], in_=base_bf16[:])
            nc.vector.reciprocal(out=inverse_base[:], in_=base[:])
            nc.vector.tensor_scalar(
                out=gain[:], in0=inverse_base[:], scalar1=-2.0 * DT / 3.0, scalar2=None, op0=ALU.mult
            )
            nc.vector.tensor_scalar(
                out=minus_gain[:], in0=inverse_base[:], scalar1=2.0 * DT / 3.0, scalar2=None, op0=ALU.mult
            )
            nc.vector.tensor_scalar(
                out=minus_two_gain[:], in0=inverse_base[:], scalar1=4.0 * DT / 3.0, scalar2=None, op0=ALU.mult
            )

        h0_of = {}
        x_of = {}
        weight_of = {}
        h0_codes_of = {}
        h1_codes_of = {}
        z1_of = {}
        r1_of = {}
        z2_of = {}
        rate_of = {}
        move_of = {}
        tau2_of = {}
        h1_of = {}
        h1_grouped_of = {}
        bank_of = {}

        def fill_flipped(key, rows, half, in_product_bank=False):
            if in_product_bank:
                flipped = products.tile([P, PAIR, HALF], F32, tag="product")
            else:
                flipped = turns.tile([P, PAIR, HALF], F32, tag="turned")
            bank_of[key] = flipped
            for jj in range(HALF // P):
                words = rows[:, half * (HALF // P) + jj, :].bitcast(F32).rearrange("p (w u) -> p u w", u=PAIR)
                for u in range(PAIR):
                    nc.tensor.transpose(flipped[:, u, jj * P : (jj + 1) * P], words[:, u, :], ident_f32[:])

        def copy_with(on_vector, out, in_):
            if on_vector:
                nc.vector.tensor_copy(out=out, in_=in_)
            else:
                nc.scalar.copy(out=out, in_=in_)

        def copy_grouped(key, grouped, half, on_vector):
            words = grouped[:].bitcast(F32).rearrange("p (c u) -> p c u", u=PAIR)
            copy_with(
                on_vector, words[:, half * HALF : (half + 1) * HALF, :], bank_of[key][:].rearrange("p u c -> p c u")
            )

        def copy_plain(key, plain, half, on_vector):
            words = plain[:].bitcast(F32).rearrange("p (u c) -> p u c", u=PAIR)
            copy_with(on_vector, words[:, :, half * HALF : (half + 1) * HALF], bank_of[key][:])

        def new_h0(c):
            h0 = flips.tile([P, CHUNK * PACK], BF16, tag="grouped", align_bytes=64)
            h0_of[c] = h0

        def new_x(c):
            x_plain = plains.tile([P, PACK * CHUNK], BF16, tag="x")
            x_of[c] = x_plain

        def h0_tile(c, m):
            return h0_of[c][:].rearrange("p (c t) -> p t c", t=PACK)[:, m, :]

        def x_tile(c, m):
            return x_of[c][:].rearrange("p (u c e) -> p u c e", u=PAIR, e=PAIR)[:, m // PAIR, :, m % PAIR]

        def product_z(step, c, j):
            codes = h0_codes_of[c] if step == 1 else h1_codes_of[c]
            return multiply(nc, products, codes, j, weight_of["rec"])

        def product_l(step, c, m):
            codes = h0_codes_of[c] if step == 1 else h1_codes_of[c]
            return multiply(nc, products, weight_of["tau"], m, codes)

        def add_z(step, c, j, product):
            if j == 0:
                z = work.tile([P, BLOCKS, H], F32, tag="z1" if step == 1 else "z2")
                (z1_of if step == 1 else z2_of)[c] = z
            z = (z1_of if step == 1 else z2_of)[c]
            nc.vector.tensor_tensor(
                out=z[:, j, :].rearrange("r (m p) -> r m p", m=PACK),
                in0=product[:].rearrange("r (m p) -> r m p", m=PACK),
                in1=ic_rows_of[c][:, j, :].rearrange("r (p m) -> r m p", m=PACK),
                op=ALU.add,
            )

        def add_l(step, c, m, product):
            if m == 0:
                if step == 1:
                    r1 = pairs.tile([P, PACK, CHUNK], F32, tag="r1")
                    r1_of[c] = r1
                else:
                    rate = rates.tile([P, PACK, CHUNK], F32, tag="rate")
                    rate_of[c] = rate
            if step == 1:
                nc.vector.tensor_tensor(out=r1_of[c][:, m, :], in0=product[:], in1=x_tile(c, m), op=ALU.add)
            else:
                nc.vector.scalar_tensor_tensor(
                    out=rate_of[c][:, m, :], in0=product[:], scalar=adapt_b[:, m : m + 1], in1=x_tile(c, m),
                    op0=ALU.add, op1=ALU.add,
                )

        stream = []
        for i in range(N_CHUNKS + 1):
            if i < 2:
                order = (("l", 1, 0, 4), ("z", 1, 0, 4), ("z", 2, 0, 4), ("l", 2, 0, 4))
            else:
                order = (("l", 1, 0, 2), ("z", 2, 0, 4), ("l", 1, 2, 4), ("z", 1, 0, 4), ("l", 2, 0, 4))
            for kind, step, first, end in order:
                c = i if step == 1 else i - 1
                if in_range(c):
                    stream.extend((kind, step, c, n) for n in range(first, end))
        stream[0:PACK], stream[PACK : 2 * PACK] = stream[PACK : 2 * PACK], stream[0:PACK]
        issued = []

        def issue_until(limit):
            while len(issued) < limit:
                kind, step, c, n = stream[len(issued)]
                issued.append(product_z(step, c, n) if kind == "z" else product_l(step, c, n))

        drained = []

        def drain(count, limit):
            for n in range(count):
                kind, step, c, n = stream[len(drained)]
                product = issued[len(drained)]
                drained.append(product)
                if kind == "z":
                    add_z(step, c, n, product)
                else:
                    add_l(step, c, n, product)
                issue_until(min(len(drained) + N_PRODUCT_BANKS, limit))

        def tanh_z1(c):
            nc.scalar.activation(out=z1_of[c][:], in_=z1_of[c][:], func=ACT.Tanh, scale=-1.0)

        def tanh_r1(c, tiles=range(PACK)):
            for m in tiles:
                nc.scalar.activation(
                    out=r1_of[c][:, m, :], in_=r1_of[c][:, m, :], func=ACT.Tanh, bias=bias_rate[:, m : m + 1], scale=0.5
                )

        def fill_d1_with_h(c, m):
            bank = turns.tile([P, CHUNK], F32, tag="turned")
            bank_of["d1", c, m] = bank
            for j in range(BLOCKS):
                nc.tensor.matmul(
                    out=bank[:, j * P : (j + 1) * P],
                    lhsT=h_rows_of[c][:, j, :].rearrange("r (p m) -> r m p", m=PACK)[:, m, :], rhs=ident_bf16[:],
                    start=(j == 0), stop=False,
                )

        def add_minus_a1(c, m):
            bank = bank_of["d1", c, m]
            for j in range(BLOCKS):
                nc.tensor.matmul(
                    out=bank[:, j * P : (j + 1) * P], lhsT=z1_of[c][:, j, m * P : (m + 1) * P], rhs=ident_f32[:],
                    is_transpose=True, start=False, stop=(j == BLOCKS - 1),
                )

        def start_d1(c):
            for m in range(PACK):
                fill_d1_with_h(c, m)

        def finish_d1(c):
            for m in range(PACK):
                add_minus_a1(c, m)

        def make_q1(c, m):
            r1 = r1_of[c]
            nc.vector.scalar_tensor_tensor(
                out=r1[:, m, :], in0=r1[:, m, :], scalar=2.0, in1=bank_of["d1", c, m][:],
                op0=ALU.subtract, op1=ALU.mult,
            )

        def make_h1(c):
            h1 = states.tile([P, PACK, CHUNK], F32, tag="h1")
            h1_of[c] = h1
            for half in range(2):
                cols = slice(half * HALF, (half + 1) * HALF)
                for m in range(PACK):
                    nc.vector.scalar_tensor_tensor(
                        out=h1[:, m, cols], in0=r1_of[c][:, m, cols], scalar=minus_gain[:, m : m + 1],
                        in1=h0_tile(c, m)[:, cols], op0=ALU.mult, op1=ALU.add,
                    )

        def new_grouped_h1(c):
            h1_grouped = grouped_h1.tile([P, CHUNK * PACK], BF16, tag="h1_grouped", align_bytes=64)
            h1_grouped_of[c] = h1_grouped

        def round_h1(c, cols, on_vector):
            copy_with(
                on_vector,
                h1_grouped_of[c][:, cols.start * PACK : cols.stop * PACK].rearrange("p (c i t) -> p c t i", i=LINE, t=PACK),
                h1_of[c][:, :, cols].rearrange("p t (c i) -> p c t i", i=LINE),
            )

        def quantise_h1_half(c, half):
            if half == 0:
                codes = mx.tile([P, CHUNK], U32, tag="h1_codes", align_bytes=64)
                scales = mx.tile([P, CHUNK], U8, tag="h1_scales", align_bytes=64)
                h1_codes_of[c] = (codes, scales)
            codes, scales = h1_codes_of[c]
            cols = slice(half * HALF, (half + 1) * HALF)
            nc.vector.quantize_mx(
                out=codes[:, cols].bitcast(FP8X4), scales=scales[:, cols],
                in_=h1_grouped_of[c][:, half * HALF * PACK : (half + 1) * HALF * PACK],
            )

        def fill_z2(c, m):
            bank = turns.tile([P, CHUNK], F32, tag="turned")
            bank_of["z2", c, m] = bank
            for j in range(BLOCKS):
                nc.tensor.transpose(bank[:, j * P : (j + 1) * P], z2_of[c][:, j, m * P : (m + 1) * P], ident_f32[:])

        def tanh_a2(c):
            move = step2.tile([P, PACK, CHUNK], F32, tag="move")
            move_of[c] = move
            for m in range(PACK):
                nc.scalar.activation(out=move[:, m, :], in_=bank_of["z2", c, m][:], func=ACT.Tanh)

        def tanh_tau2(c):
            tau2 = step2.tile([P, PACK, CHUNK], F32, tag="tau2")
            tau2_of[c] = tau2
            nc.scalar.activation(out=tau2[:], in_=rate_of[c][:], func=ACT.Tanh, scale=0.5)

        def tanh_r2(c, rate):
            nc.scalar.activation(out=rate[:], in_=rate_of[c][:], func=ACT.Tanh, bias=HALF_LN_3, scale=0.5)
            rate_of[c] = rate

        def make_d2(c, engine):
            move = move_of[c]
            for w in TILE_PAIRS:
                engine.tensor_tensor(out=move[:, w, :], in0=move[:, w, :], in1=h1_of[c][:, w, :], op=ALU.subtract)

        def affine(engine, tile, scale, bias, tiles=range(PACK)):
            for m in tiles:
                if engine is None:
                    nc.scalar.activation(
                        out=tile[:, m, :], in_=tile[:, m, :], func=ACT.Identity,
                        bias=bias[:, m : m + 1], scale=scale[:, m : m + 1],
                    )
                else:
                    engine.tensor_scalar(
                        out=tile[:, m, :], in0=tile[:, m, :], scalar1=scale[:, m : m + 1], scalar2=bias[:, m : m + 1],
                        op0=ALU.mult, op1=ALU.add,
                    )

        def scale_rate(c, engine, tiles=range(PACK)):
            affine(engine, rate_of[c], gain, minus_two_gain, tiles)

        def make_q2(c, w, engine):
            move = move_of[c]
            engine.tensor_tensor(out=move[:, w, :], in0=rate_of[c][:, w, :], in1=move[:, w, :], op=ALU.mult)

        def fill_rows(key, terms, j, in_product_bank):
            if in_product_bank:
                back = products.tile([P, PACK, P], F32, tag="product")
            else:
                back = turns.tile([P, PACK, P], F32, tag="turned")
            bank_of[key] = back
            for m in range(PACK):
                for n, term in enumerate(terms):
                    nc.tensor.matmul(
                        out=back[:, m, :], lhsT=term[:, m, j * P : (j + 1) * P], rhs=ident_f32[:], is_transpose=True,
                        start=(n == 0), stop=(n == len(terms) - 1),
                    )

        def fill_tau2(c, j, in_product_bank=False):
            fill_rows(("tau2", c, j), [tau2_of[c]], j, in_product_bank)

        def fill_h2(c, j, in_product_bank=False):
            fill_rows(("h2", c, j), [h1_of[c], move_of[c]], j, in_product_bank)

        tau_rows_of = {}

        def copy_and_store(kind, c, j):
            in_view = bank_of[kind, c, j][:].rearrange("r m p -> r p m")
            if kind == "tau2":
                if j == 0:
                    tau_rows = tau_stores.tile([P, BLOCKS, H], F32, tag="tau_rows")
                    tau_rows_of[c] = tau_rows
                tau_rows = tau_rows_of[c]
                nc.vector.scalar_tensor_tensor(
                    out=tau_rows[:, j, :].rearrange("r (p m) -> r p m", m=PACK), in0=in_view, scalar=2.0,
                    in1=half_base_row[:].rearrange("r (p m) -> r p m", m=PACK), op0=ALU.add, op1=ALU.mult,
                )
                dram_blocks = out_1[chunk_rows(c), :].rearrange("(p j) f -> p j f", j=BLOCKS)
                if c == LAST:
                    nc.sync.dma_start(out=dram_blocks[:, j, :], in_=tau_rows[:, j, :])
                elif j == BLOCKS - 1:
                    nc.sync.dma_start(out=dram_blocks, in_=tau_rows[:])
            else:
                out_rows = stores.tile([P, H], F32, tag="out_rows")
                nc.scalar.copy(out=out_rows[:].rearrange("r (p m) -> r p m", m=PACK), in_=in_view)
                dram_blocks = out_0[chunk_rows(c), :].rearrange("(p j) f -> p j f", j=BLOCKS)
                nc.sync.dma_start(out=dram_blocks[:, j, :], in_=out_rows[:])

        gate_word = const.tile([P, 1], U32)

        def hold_gpsimd_until_h1_is_quantised(c):
            nc.gpsimd.tensor_copy(out=gate_word[:], in_=h1_codes_of[c][0][:, CHUNK - 1 : CHUNK])

        gate_value = const.tile([P, 1], F32)

        def hold_gpsimd_until_written(tile):
            nc.gpsimd.tensor_copy(out=gate_value[:], in_=tile[:, PACK - 1, CHUNK - 1 : CHUNK])

        rec_grouped = grouped_h1.tile([P, CHUNK * PACK], BF16, tag="h1_grouped", align_bytes=64)
        tau_grouped = grouped_h1.tile([P, CHUNK * PACK], BF16, tag="h1_grouped", align_bytes=64)
        new_h0(0)
        new_x(0)

        def fill_at_start(name, rows):
            for half in range(2):
                fill_flipped((name, half), rows, half)

        def copy_at_start(name, copy, target):
            copy((name, 0), target, 0, False)
            copy((name, 1), target, 1, True)

        def fill_h_flips(c, in_product_banks=True):
            for half in range(2):
                fill_flipped((("h", c), half), h_rows_of[c], half, in_product_banks)

        def fill_x_flips(c, in_product_banks=True):
            for half in range(2):
                fill_flipped((("x", c), half), x_rows_of[c], half, in_product_banks)

        def copy_flips(c):
            new_h0(c)
            new_x(c)
            for half in range(2):
                copy_grouped((("h", c), half), h0_of[c], half, False)
            for half in range(2):
                copy_plain((("x", c), half), x_of[c], half, False)

        def quantise_h0(c):
            h0_codes_of[c] = quantise(nc, mx, h0_of[c], "h0")

        fill_at_start("rec", rec_weight_rows)
        fill_at_start("h0", h_rows_of[0])
        copy_at_start("rec", copy_grouped, rec_grouped)
        weight_of["rec"] = quantise(nc, const, rec_grouped, "rec_weight")
        first_codes = mx.tile([P, CHUNK], U32, tag="h0_codes", align_bytes=64)
        first_scales = mx.tile([P, CHUNK], U8, tag="h0_scales", align_bytes=64)
        h0_codes_of[0] = (first_codes, first_scales)
        for half in range(2):
            copy_grouped(("h0", half), h0_of[0], half, False)
            cols = slice(half * HALF, (half + 1) * HALF)
            nc.vector.quantize_mx(
                out=first_codes[:, cols].bitcast(FP8X4), scales=first_scales[:, cols],
                in_=h0_of[0][:, half * HALF * PACK : (half + 1) * HALF * PACK],
            )
        issue_until(PACK)
        fill_at_start("tau", tau_weight_rows)
        fill_at_start("x0", x_rows_of[0])
        drain(PACK, PACK)
        copy_at_start("tau", copy_grouped, tau_grouped)
        weight_of["tau"] = quantise(nc, const, tau_grouped, "tau_weight")
        copy_at_start("x0", copy_plain, x_of[0])
        make_vectors()

        end_of_round = 0
        for i in range(N_CHUNKS):
            after, before, done = in_range(i + 1), in_range(i - 1), in_range(i - 2)
            end_of_round += 4 * PACK if before else 2 * PACK
            limit = end_of_round
            if done:
                hold_gpsimd_until_h1_is_quantised(i - 1)
                make_d2(i - 2, nc.gpsimd)
                scale_rate(i - 2, nc.gpsimd, range(0, 4))
                for w in TILE_PAIRS:
                    make_q2(i - 2, w, nc.gpsimd)
            if i == 0:
                load_h(2)
                load_x(2)
            if in_range(i + 2):
                load_ic(i + 2)
            if i == 1:
                drain(end_of_round - 3 * PACK - len(drained), limit)
                tanh_r1(i)
                drain(PACK, limit)
                tanh_z1(i)
                start_d1(i)
                drain(2 * PACK, limit)
                tanh_tau2(i - 1)
                finish_d1(i)
            elif before:
                drain(PACK // 2, limit)
                if in_range(i - 3):
                    fill_h2(i - 3, BLOCKS - 1)
                    copy_and_store("h2", i - 3, BLOCKS - 1)
                drain(PACK - 1, limit)
                drain(1, len(issued))
                fill_z2(i - 1, 0)
                fill_z2(i - 1, 1)
                drain(1, limit)
                fill_z2(i - 1, 2)
                drain(1, limit)
                fill_z2(i - 1, 3)
                tanh_r1(i, range(0, 2))
                tanh_a2(i - 1)
                drain(PACK + PACK // 2 - 2, limit)
                tanh_z1(i)
                tanh_r1(i, (3, 2))
                drain(PACK, limit)
                fill_tau2(i - 2, 0, True)
                fill_d1_with_h(i, 0)
                fill_d1_with_h(i, 1)
                fill_tau2(i - 2, 1, True)
                fill_d1_with_h(i, 2)
                fill_d1_with_h(i, 3)
                fill_tau2(i - 2, 2, True)
                fill_tau2(i - 2, 3, True)
                for j in range(BLOCKS):
                    copy_and_store("tau2", i - 2, j)
                tanh_tau2(i - 1)
                finish_d1(i)
                if in_range(i + 2):
                    fill_h_flips(i + 2)
                    fill_x_flips(i + 2)
                    copy_flips(i + 2)
            else:
                tanh_z1(i)
                issue_until(limit)
                start_d1(i)
                drain(PACK, limit)
                tanh_r1(i)
                finish_d1(i)
            for m in range(PACK):
                make_q1(i, m)
            if i == 0:
                fill_h_flips(1)
                fill_x_flips(1)
                copy_flips(1)
                fill_h_flips(2, in_product_banks=False)
                fill_x_flips(2, in_product_banks=False)
            make_h1(i)
            if i == 1:
                for m in range(PACK):
                    fill_z2(0, m)
                tanh_a2(0)
                fill_h_flips(3)
                fill_x_flips(3)
                copy_flips(3)
            if after:
                quantise_h0(i + 1)
            new_grouped_h1(i)
            if i == 1:
                round_h1(i, slice(0, CHUNK), on_vector=True)
            else:
                if done:
                    for j in range(H2_BEFORE_ROUNDING):
                        fill_h2(i - 2, j)
                        copy_and_store("h2", i - 2, j)
                round_h1(i, slice(0, HALF), on_vector=False)
                if VECTOR_ROUNDS:
                    round_h1(i, slice(HALF, HALF + VECTOR_ROUNDS), on_vector=True)
                round_h1(i, slice(HALF + VECTOR_ROUNDS, CHUNK), on_vector=False)
            quantise_h1_half(i, 0)
            if done:
                if not after:
                    fill_tau2(LAST - 1, 0, True)
                    fill_tau2(LAST - 1, 1, True)
                for j in range(H2_BEFORE_ROUNDING, BLOCKS - 1):
                    fill_h2(i - 2, j)
                if after:
                    issue_until(limit + PACK // 2)
                for j in range(H2_BEFORE_ROUNDING, BLOCKS - 1):
                    copy_and_store("h2", i - 2, j)
            if i == 0:
                nc.sync.dma_start(out=base_row_bf16[:], in_=tau_base.partition_broadcast(P))
            if i == 1:
                issue_until(limit + PACK // 2)
                nc.vector.tensor_scalar(
                    out=half_base_row[:], in0=base_row_bf16[:], scalar1=0.5, scalar2=None, op0=ALU.mult
                )
            if i == 0:
                copy_flips(2)
                issue_until(limit + PACK)
                drain(PACK, limit + PACK)
            if in_range(i + 3):
                load_h(i + 3)
                load_x(i + 3)
            quantise_h1_half(i, 1)
            if before:
                tanh_r2(i - 1, rate_of[i - 1])
                if after:
                    scale_rate(i - 1, None, range(4, PACK))
            if not after:
                issue_until(len(drained) + N_PRODUCT_BANKS - 2)
                copy_and_store("tau2", LAST - 1, 0)
                copy_and_store("tau2", LAST - 1, 1)
            issue_until(len(drained) + N_PRODUCT_BANKS)
            if not after:
                fill_h2(i - 2, BLOCKS - 1)
                copy_and_store("h2", i - 2, BLOCKS - 1)

        limit = len(stream)
        hold_gpsimd_until_h1_is_quantised(LAST)
        make_d2(LAST - 1, nc.gpsimd)
        scale_rate(LAST - 1, None)
        drain(PACK, limit)
        for m in range(PACK):
            fill_z2(LAST, m)
        tanh_a2(LAST)
        drain(PACK, limit)
        for j in (2, 3):
            fill_tau2(LAST - 1, j, True)
        for j in (2, 3):
            copy_and_store("tau2", LAST - 1, j)
        for w in TILE_PAIRS:
            make_q2(LAST - 1, w, nc.vector)
        make_d2(LAST, nc.vector)
        last_logits = rate_of[LAST]
        last_rate = pairs.tile([P, PACK, CHUNK], F32, tag="r1")
        tanh_r2(LAST, last_rate)
        last_tau2 = step2.tile([P, PACK, CHUNK], F32, tag="tau2")
        tau2_of[LAST] = last_tau2
        nc.scalar.activation(out=last_tau2[:], in_=last_logits[:], func=ACT.Tanh, scale=0.5)
        scale_rate(LAST, nc.vector)
        for half in range(2):
            cols = slice(half * HALF, (half + 1) * HALF)
            nc.vector.tensor_tensor(
                out=move_of[LAST][:, :, cols], in0=rate_of[LAST][:, :, cols], in1=move_of[LAST][:, :, cols], op=ALU.mult
            )
        jobs = []
        for kind, c, fill in (("h2", LAST - 1, fill_h2), ("tau2", LAST, fill_tau2), ("h2", LAST, fill_h2)):
            jobs.extend((kind, c, fill, j) for j in range(BLOCKS))
        ahead = N_PRODUCT_BANKS + N_TURN_BANKS
        for n in range(len(jobs) + ahead):
            if n >= ahead:
                kind, c, fill, j = jobs[n - ahead]
                copy_and_store(kind, c, j)
            if n < len(jobs):
                kind, c, fill, j = jobs[n]
                fill(c, j, n % 2 == 1)
